import numpy as np
import ml_dtypes


def mxq(x, axis, fmt="e4m3"):
    dtype, down = {"e4m3": (ml_dtypes.float8_e4m3fn, 7), "e5m2": (ml_dtypes.float8_e5m2, 14)}[fmt]
    v = np.moveaxis(np.asarray(x, np.float32).astype(ml_dtypes.bfloat16).astype(np.float64), axis, -1)
    blocks = v.reshape(v.shape[:-1] + (-1, 32))
    amax = np.abs(blocks).max(-1, keepdims=True)
    byte = np.maximum(np.where(amax > 0, np.frexp(amax)[1] - 1 + 127, 0) - down, 1)
    scale = np.exp2(byte - 127.0)
    codes = (blocks / scale).astype(np.float32).astype(dtype).astype(np.float64)
    return np.moveaxis((codes * scale).reshape(v.shape), -1, axis)


WIDE = False


def mx_kscale(k):
    if not WIDE:
        return np.ones(k)
    levels = np.array([10, -10, 5, -5, 0])
    a = np.random.permutation(np.resize(levels, k // 512 * 4)).reshape(k // 512, 4)
    idx = np.arange(k)
    return np.exp2(a[idx // 512, idx % 128 // 32])


BF16 = ml_dtypes.bfloat16


def bf(x):
    return np.asarray(x, np.float32).astype(BF16)


def f64(x):
    return np.asarray(x).astype(np.float64)


B, D, S = 256, 512, 16


def softplus(v):
    return np.maximum(v, 0.0) + np.log(1.0 + np.exp(-np.abs(v)))


def silu(v):
    return v / (1.0 + np.exp(-v))


def setup_inputs():
    k = mx_kscale(D)
    w = 1.0 / np.sqrt(D)
    return {
        "x": bf(np.random.standard_normal((B, D)) * k),
        "h": bf(np.random.standard_normal((B, D, S))),
        "in_proj_w": bf(np.random.standard_normal((D, D)) * 1.5 * w / k[None, :]),
        "dt_proj_w": bf(np.random.standard_normal((D, D)) * w / k[None, :]),
        "dt_proj_b": bf(-1.5 + 0.5 * np.random.standard_normal(D)),
        "bc_proj_w": bf(np.random.standard_normal((D * S * 2, D)) * w / k[None, :]),
        "A_log": bf(np.log(np.tile(np.arange(1, S + 1), (D, 1))) + 0.1 * np.random.standard_normal((D, S))),
        "D_param": bf(1.0 + 0.1 * np.random.standard_normal(D)),
        "out_proj_w": bf(np.random.standard_normal((D, D)) * w),
        "out_proj_b": bf(0.5 * np.random.standard_normal(D)),
    }


def reference(x, h, in_proj_w, dt_proj_w, dt_proj_b, bc_proj_w, A_log, D_param, out_proj_w, out_proj_b):
    xq = mxq(f64(x), 1, "e4m3")
    u = xq @ mxq(f64(in_proj_w), 1, "e4m3").T
    delta = softplus((xq @ mxq(f64(dt_proj_w), 1, "e4m3").T) + f64(dt_proj_b))[..., None]
    bc = (xq @ mxq(f64(bc_proj_w), 1, "e4m3").T).reshape(B, D, 2, S)
    b_t = bc[:, :, 0, :]
    c_t = bc[:, :, 1, :]
    a = -np.exp(f64(A_log))[None]
    d_a = np.exp(delta * a)
    h_new = d_a * f64(h) + delta * b_t * u[..., None]
    y = (h_new * c_t).sum(axis=-1) + f64(D_param) * u
    out = (mxq(silu(y), 1, "e4m3") @ mxq(f64(out_proj_w), 1, "e4m3").T) + f64(out_proj_b)
    return out, h_new

@@ -1,0 +1,450 @@
+from contextlib import ExitStack
+
+import concourse.mybir as mybir
+from concourse.masks import make_identity
+
+F32 = mybir.dt.float32
+BF16 = mybir.dt.bfloat16
+U32 = mybir.dt.uint32
+U8 = mybir.dt.uint8
+FP8X4 = mybir.dt.float8_e4m3fn_x4
+ACT = mybir.ActivationFunctionType
+ALU = mybir.AluOpType
+
+P = 128
+B = 256
+D = 512
+S = 16
+RT = B // P
+CT = D // P
+NG = 4
+NN = S // NG
+NSTEP = CT * NG
+PF = 3
+
+FLOPS = 2 * B * D * (3 * D + 2 * D * S)
+
+PIN = True
+ADD_ON_GPSIMD = True
+
+
+def tile_mambacell_pa_kernel(
+    tc, x, h, in_proj_w, dt_proj_w, dt_proj_b, bc_proj_w, a_log, d_param, out_proj_w, out_proj_b, out, h_new
+):
+    nc = tc.nc
+    with ExitStack() as ctx:
+        if PIN:
+            ctx.enter_context(tc.manual_schedule())
+        const = ctx.enter_context(tc.tile_pool(name="const", bufs=1))
+        stg = ctx.enter_context(tc.tile_pool(name="stg", bufs=1))
+        wstp = ctx.enter_context(tc.tile_pool(name="wstp", bufs=3))
+        wgp = ctx.enter_context(tc.tile_pool(name="wgp", bufs=2))
+        wcp = ctx.enter_context(tc.tile_pool(name="wcp", bufs=3))
+        hp = ctx.enter_context(tc.tile_pool(name="hp", bufs=4))
+        ep = ctx.enter_context(tc.tile_pool(name="ep", bufs=3))
+        tp = ctx.enter_context(tc.tile_pool(name="tp", bufs=4))
+        hnp = ctx.enter_context(tc.tile_pool(name="hnp", bufs=4))
+        psw = ctx.enter_context(tc.psum_pool(name="psw", bufs=2))
+        pst = ctx.enter_context(tc.psum_pool(name="pst", bufs=4))
+        psy = ctx.enter_context(tc.psum_pool(name="psy", bufs=1))
+
+        ident_f = const.tile([P, P], F32, name="ident_f")
+        make_identity(nc, ident_f[:])
+        ident_b = const.tile([P, P], BF16, name="ident_b")
+        make_identity(nc, ident_b[:])
+
+        vrows = stg.tile([P, P], BF16, name="vrows")
+        nc.vector.memset(vrows[:], 0.0)
+        a_sb = stg.tile([P, CT * S], BF16, name="a_sb")
+        ob = const.tile([P, D], BF16, name="ob")
+
+        x_sb = stg.tile([P, RT * D], BF16, name="x_sb")
+        nc.sync.dma_start(
+            out=x_sb[:].rearrange("p (t k) -> p t k", t=RT), in_=x.rearrange("(t p) k -> p t k", p=P)
+        )
+        dtw_sb = stg.tile([P, CT * D], BF16, name="dtw_sb")
+        nc.sync.dma_start(
+            out=dtw_sb[:].rearrange("p (t k) -> p t k", t=CT), in_=dt_proj_w.rearrange("(t p) k -> p t k", p=P)
+        )
+        inw_sb = stg.tile([P, CT * D], BF16, name="inw_sb")
+        nc.sync.dma_start(
+            out=inw_sb[:].rearrange("p (t k) -> p t k", t=CT), in_=in_proj_w.rearrange("(t p) k -> p t k", p=P)
+        )
+        nc.scalar.dma_start(out=a_sb[:].rearrange("p (t n) -> p t n", t=CT), in_=a_log.rearrange("(t p) n -> p t n", p=P))
+        nc.scalar.dma_start(out=vrows[0:CT, :], in_=dt_proj_b.rearrange("(t c) -> t c", c=P))
+        nc.scalar.dma_start(out=vrows[CT : 2 * CT, :], in_=d_param.rearrange("(t c) -> t c", c=P))
+        nc.scalar.dma_start(out=ob[:], in_=out_proj_b.partition_broadcast(P))
+
+        wview = bc_proj_w.rearrange("(t p j g n) k -> t g p j n k", p=P, j=2, g=NG, n=NN)
+        hview = h.rearrange("b c n -> b (c n)")
+        hnview = h_new.rearrange("b c n -> b (c n)")
+        wst = {}
+        w_ps = {}
+        wg = {}
+        wc = {}
+        ws = {}
+        h_sb = {}
+        e_t = {}
+        e_ps = {}
+        b_ps = {}
+        c_ps = {}
+        t2 = {}
+        t3 = {}
+        t4 = {}
+        hn = {}
+
+        def load_w(s):
+            wst[s] = wstp.tile([P, 2 * NN * D], BF16, name="wst%d" % s, tag="wst")
+            nc.sync.dma_start(
+                out=wst[s][:].rearrange("p (j n k) -> p j n k", j=2, n=NN), in_=wview[s // NG, s % NG]
+            )
+
+        def load_h(ct):
+            for rt in range(RT):
+                h_sb[(ct, rt)] = hp.tile([P, P * S], BF16, name="h%d_%d" % (ct, rt), tag="h")
+                nc.sync.dma_start(
+                    out=h_sb[(ct, rt)][:], in_=hview[rt * P : (rt + 1) * P, ct * P * S : (ct + 1) * P * S]
+                )
+
+        load_w(0)
+        load_h(0)
+        load_w(1)
+        load_w(2)
+        wo_sb = stg.tile([P, CT * D], BF16, name="wo_sb")
+
+        def words_to_bank(src_words, first_col, name):
+            ps = psw.tile([P, 512], F32, name=name, tag="wps")
+            for j in range(2):
+                for u in range(2):
+                    col = first_col + j * 256 + u * P
+                    nc.tensor.transpose(ps[:, (j * 2 + u) * P : (j * 2 + u + 1) * P], src_words[:, col : col + P], ident_f[:])
+            return ps
+
+        def bank_to_grouped(eng_copy, ps, dst_words):
+            eng_copy(
+                out=dst_words.rearrange("p (j c u) -> p j c u", j=2, u=2),
+                in_=ps[:].rearrange("p (j u c) -> p j c u", j=2, u=2),
+            )
+
+        xg = stg.tile([P, 4 * B], BF16, name="xg", align_bytes=64)
+        xc = const.tile([P, B], U32, name="xc", align_bytes=64)
+        xs = const.tile([P, B], U8, name="xs", align_bytes=64)
+        xp = words_to_bank(x_sb[:].bitcast(F32), 0, "xp")
+        bank_to_grouped(nc.vector.tensor_copy, xp, xg[:].bitcast(F32))
+
+        def prep_512(w_sb, nm, engs):
+            grouped = stg.tile([P, 4 * D], BF16, name="g_" + nm, align_bytes=64)
+            codes = const.tile([P, D], U32, name="c_" + nm, align_bytes=64)
+            scales = const.tile([P, D], U8, name="s_" + nm, align_bytes=64)
+            for half in range(2):
+                ps = words_to_bank(w_sb[:].bitcast(F32), half * 512, "ps_%s%d" % (nm, half))
+                bank_to_grouped(engs[half], ps, grouped[:].bitcast(F32)[:, half * 512 : (half + 1) * 512])
+            return grouped, codes, scales
+
+        a_exp = stg.tile([P, CT * S], F32, name="a_exp")
+        nc.scalar.activation(out=a_exp[:], in_=a_sb[:], func=ACT.Exp)
+
+        dtg, dtc, dts = prep_512(dtw_sb, "dt", [nc.vector.tensor_copy, nc.scalar.copy])
+        nc.vector.quantize_mx(out=xc[:].bitcast(FP8X4), scales=xs[:], in_=xg[:])
+
+        vps = pst.tile([P, 1024], BF16, name="vps", tag="st")
+        nc.tensor.transpose(vps[:, 0:P], vrows[:], ident_b[:])
+        vec = const.tile([P, 2 * CT], F32, name="vec")
+        nc.vector.tensor_copy(out=vec[:], in_=vps[:, 0 : 2 * CT])
+        nc.vector.quantize_mx(out=dtc[:].bitcast(FP8X4), scales=dts[:], in_=dtg[:])
+        neg_a = const.tile([P, CT * S], F32, name="neg_a")
+        nc.vector.tensor_scalar(out=neg_a[:], in0=a_exp[:], scalar1=-1.0, scalar2=None, op0=ALU.mult)
+
+        ing, inc, ins = prep_512(inw_sb, "in", [nc.scalar.copy, nc.scalar.copy])
+
+        def proj_t(codes, scales, nm):
+            banks = []
+            for half in range(2):
+                ps = pst.tile([P, 512], F32, name="pj_%s%d" % (nm, half), tag="st")
+                for j in range(2):
+                    ct = half * 2 + j
+                    nc.tensor.matmul_mx(
+                        out=ps[:, j * B : (j + 1) * B],
+                        lhsT=codes[:, ct * P : (ct + 1) * P].bitcast(FP8X4),
+                        lhsT_scale=scales[:, ct * P : (ct + 1) * P],
+                        rhs=xc[:].bitcast(FP8X4),
+                        rhs_scale=xs[:],
+                        start=True,
+                        stop=True,
+                    )
+                banks.append(ps)
+            return banks
+
+        d_banks = proj_t(dtc, dts, "dt")
+        nc.vector.quantize_mx(out=inc[:].bitcast(FP8X4), scales=ins[:], in_=ing[:])
+        u_banks = proj_t(inc, ins, "in")
+
+        sp_abs = stg.tile([P, CT * B], F32, name="sp_abs")
+        sp_exp = sp_abs
+        sp_ln = sp_abs
+        sp_max = stg.tile([P, CT * B], F32, name="sp_max")
+        delta_t = const.tile([P, CT * B], F32, name="delta_t")
+        for ct in range(CT):
+            src = d_banks[ct // 2][:, (ct % 2) * B : (ct % 2 + 1) * B]
+            nc.scalar.activation(
+                out=sp_abs[:, ct * B : (ct + 1) * B], in_=src, func=ACT.Abs, bias=vec[:, ct : ct + 1], scale=1.0
+            )
+            nc.vector.tensor_scalar(
+                out=sp_max[:, ct * B : (ct + 1) * B],
+                in0=src,
+                scalar1=vec[:, ct : ct + 1],
+                scalar2=0.0,
+                op0=ALU.add,
+                op1=ALU.max,
+            )
+        nc.scalar.activation(out=sp_exp[:], in_=sp_abs[:], func=ACT.Exp, scale=-1.0)
+        nc.scalar.activation(out=sp_ln[:], in_=sp_exp[:], func=ACT.Ln, bias=1.0, scale=1.0)
+
+        du_skip = const.tile([P, CT * B], F32, name="du_skip")
+        for ct in range(CT):
+            nc.vector.tensor_scalar(
+                out=du_skip[:, ct * B : (ct + 1) * B],
+                in0=u_banks[ct // 2][:, (ct % 2) * B : (ct % 2 + 1) * B],
+                scalar1=vec[:, CT + ct : CT + ct + 1],
+                scalar2=None,
+                op0=ALU.mult,
+            )
+        def w_tr(s, b):
+            w_ps[(s, b)] = words_to_bank(wst[s][:].bitcast(F32), b * 512, "wps%d_%d" % (s, b))
+
+        def w_ev(s, b, eng_copy):
+            if b == 0:
+                wg[s] = wgp.tile([P, 4 * 2 * NN * P], BF16, name="wg%d" % s, tag="wg", align_bytes=64)
+            bank_to_grouped(eng_copy, w_ps[(s, b)], wg[s][:].bitcast(F32)[:, b * 512 : (b + 1) * 512])
+
+        def w_bank(s, b, eng_copy):
+            w_tr(s, b)
+            w_ev(s, b, eng_copy)
+
+        def quant(s, j):
+            if j == 0:
+                wc[s] = wcp.tile([P, 2 * NN * P], U32, name="wc%d" % s, tag="wc", align_bytes=64)
+                ws[s] = wcp.tile([P, 2 * NN * P], U8, name="ws%d" % s, tag="ws", align_bytes=64)
+            nc.vector.quantize_mx(
+                out=wc[s][:, j * 512 : (j + 1) * 512].bitcast(FP8X4),
+                scales=ws[s][:, j * 512 : (j + 1) * 512],
+                in_=wg[s][:, j * 2048 : (j + 1) * 2048],
+            )
+
+        def exps(s):
+            ct = s // NG
+            g = s % NG
+            e_t[s] = ep.tile([P, NN * B], F32, name="et%d" % s, tag="et")
+            for i in range(NN):
+                n = g * NN + i
+                nc.scalar.activation(
+                    out=e_t[s][:, i * B : (i + 1) * B],
+                    in_=delta_t[:, ct * B : (ct + 1) * B],
+                    func=ACT.Exp,
+                    scale=neg_a[:, ct * S + n : ct * S + n + 1],
+                )
+
+        def e_trans(s, rt):
+            e_ps[(s, rt)] = pst.tile([P, 512], F32, name="eps%d_%d" % (s, rt), tag="st")
+            for i in range(NN):
+                nc.tensor.transpose(
+                    e_ps[(s, rt)][:, i * P : (i + 1) * P], e_t[s][:, i * B + rt * P : i * B + (rt + 1) * P], ident_f[:]
+                )
+
+        def mx_bc(s, rt, j, store, nm):
+            store[(s, rt)] = pst.tile([P, 512], F32, name="%s%d_%d" % (nm, s, rt), tag="st")
+            nc.tensor.matmul_mx(
+                out=store[(s, rt)][:],
+                lhsT=xc[:, rt * P : (rt + 1) * P].bitcast(FP8X4),
+                lhsT_scale=xs[:, rt * P : (rt + 1) * P],
+                rhs=wc[s][:, j * 512 : (j + 1) * 512].bitcast(FP8X4),
+                rhs_scale=ws[s][:, j * 512 : (j + 1) * 512],
+                start=True,
+                stop=True,
+            )
+
+        def by_channel(ps):
+            return ps[:].rearrange("p (n c) -> p c n", n=NN)
+
+        def compact(t):
+            return t[:].rearrange("p (c n) -> p c n", n=NN)
+
+        def natural(t, g):
+            return t[:].rearrange("p (c n) -> p c n", n=S)[:, :, g * NN : (g + 1) * NN]
+
+        def v_t2(s, rt):
+            t2[(s, rt)] = tp.tile([P, 512], F32, name="t2_%d_%d" % (s, rt), tag="t2")
+            nc.vector.tensor_tensor(
+                out=compact(t2[(s, rt)]), in0=by_channel(e_ps[(s, rt)]), in1=natural(h_sb[(s // NG, rt)], s % NG), op=ALU.mult
+            )
+
+        def v_t3(s, rt):
+            ct = s // NG
+            t3[(s, rt)] = tp.tile([P, 512], F32, name="t3_%d_%d" % (s, rt), tag="t3")
+            nc.vector.tensor_tensor(
+                out=compact(t3[(s, rt)]),
+                in0=by_channel(b_ps[(s, rt)]),
+                in1=du[rt][:, ct * P : (ct + 1) * P].unsqueeze(2).to_broadcast([P, P, NN]),
+                op=ALU.mult,
+            )
+
+        def add_hn(s, rt):
+            ct = s // NG
+            g = s % NG
+            if g == 0:
+                hn[(ct, rt)] = hnp.tile([P, P * S], F32, name="hn%d_%d" % (ct, rt), tag="hn")
+            eng = nc.gpsimd if ADD_ON_GPSIMD else nc.vector
+            eng.tensor_tensor(out=natural(hn[(ct, rt)], g), in0=compact(t2[(s, rt)]), in1=compact(t3[(s, rt)]), op=ALU.add)
+            if g == NG - 1:
+                nc.sync.dma_start(out=hnview[rt * P : (rt + 1) * P, ct * P * S : (ct + 1) * P * S], in_=hn[(ct, rt)][:])
+
+        def v_t4(s, rt):
+            t4[(s, rt)] = tp.tile([P, 512], F32, name="t4_%d_%d" % (s, rt), tag="t4")
+            nc.vector.tensor_tensor(
+                out=compact(t4[(s, rt)]), in0=by_channel(c_ps[(s, rt)]), in1=natural(hn[(s // NG, rt)], s % NG), op=ALU.mult
+            )
+
+        def y_acc(s, rt):
+            ct = s // NG
+            g = s % NG
+            for i in range(NN):
+                nc.tensor.matmul(
+                    out=y_ps[rt][:, ct * P : (ct + 1) * P],
+                    lhsT=compact(t4[(s, rt)])[:, :, i],
+                    rhs=ident_f[:],
+                    is_transpose=True,
+                    start=(g == 0 and i == 0),
+                    stop=(g == NG - 1 and i == NN - 1),
+                )
+
+        def fin_y(ct):
+            for rt in range(RT):
+                lo = ct * B + rt * P
+                nc.vector.tensor_tensor(
+                    out=y_f[:, lo : lo + P], in0=y_ps[rt][:, ct * P : (ct + 1) * P], in1=du_skip[:, lo : lo + P], op=ALU.add
+                )
+
+        def silu(ct):
+            nc.scalar.activation(
+                out=sg[:].rearrange("p (r t) -> p r t", t=CT)[:, :, ct], in_=y_f[:, ct * B : (ct + 1) * B], func=ACT.Silu
+            )
+
+        y_ps = [psy.tile([P, 512], F32, name="y_ps%d" % rt) for rt in range(RT)]
+        y_f = const.tile([P, CT * B], F32, name="y_f")
+        sg = const.tile([P, CT * B], BF16, name="sg", align_bytes=64)
+
+        for b in range(4):
+            w_bank(0, b, nc.vector.tensor_copy)
+        w_tr(1, 0)
+        w_tr(1, 1)
+        quant(0, 0)
+        nc.vector.tensor_tensor(out=delta_t[:], in0=sp_max[:], in1=sp_ln[:], op=ALU.add)
+        du_t = stg.tile([P, CT * B], F32, name="du_t")
+        for half in range(2):
+            nc.vector.tensor_tensor(
+                out=du_t[:, half * 512 : (half + 1) * 512],
+                in0=u_banks[half][:],
+                in1=delta_t[:, half * 512 : (half + 1) * 512],
+                op=ALU.mult,
+            )
+        exps(0)
+        du = []
+        for rt in range(RT):
+            dps = pst.tile([P, 512], F32, name="dups%d" % rt, tag="st")
+            for ct in range(CT):
+                nc.tensor.transpose(dps[:, ct * P : (ct + 1) * P], du_t[:, ct * B + rt * P : ct * B + (rt + 1) * P], ident_f[:])
+            du.append(const.tile([P, D], F32, name="du%d" % rt))
+            nc.scalar.copy(out=du[rt][:], in_=dps[:])
+
+        wog = stg.tile([P, 4 * D], BF16, name="wog", align_bytes=64)
+        woc = const.tile([P, D], U32, name="woc", align_bytes=64)
+        wos = const.tile([P, D], U8, name="wos", align_bytes=64)
+
+        def prep_wo(half):
+            ps = psw.tile([P, 1024], BF16, name="wops%d" % half, tag="wps")
+            for a in range(2):
+                ot = half * 2 + a
+                for t in range(CT):
+                    nc.tensor.transpose(
+                        ps[:, (a * CT + t) * P : (a * CT + t + 1) * P], wo_sb[:, ot * D + t * P : ot * D + (t + 1) * P], ident_b[:]
+                    )
+            nc.scalar.copy(
+                out=wog[:, half * 1024 : (half + 1) * 1024].rearrange("p (a o t) -> p a o t", a=2, t=CT),
+                in_=ps[:].rearrange("p (a t o) -> p a o t", a=2, t=CT),
+            )
+
+        for s in range(NSTEP + 2):
+            nxt = s + 1
+            if s + PF < NSTEP:
+                load_w(s + PF)
+            if s % NG == 1 and s // NG + 1 < CT:
+                load_h(s // NG + 1)
+            if s == 2:
+                nc.sync.dma_start(
+                    out=wo_sb[:].rearrange("p (t k) -> p t k", t=CT), in_=out_proj_w.rearrange("(t p) k -> p t k", p=P)
+                )
+            if s == 0:
+                w_ev(nxt, 0, nc.scalar.copy)
+                w_ev(nxt, 1, nc.scalar.copy)
+            elif nxt < NSTEP:
+                w_bank(nxt, 0, nc.scalar.copy)
+                w_bank(nxt, 1, nc.scalar.copy)
+            if s < NSTEP:
+                e_trans(s, 0)
+                e_trans(s, 1)
+            if nxt < NSTEP:
+                exps(nxt)
+            if s >= 2:
+                y_acc(s - 2, 0)
+                y_acc(s - 2, 1)
+            if nxt < NSTEP:
+                w_bank(nxt, 2, nc.scalar.copy)
+                w_bank(nxt, 3, nc.scalar.copy)
+            if s == 5 or s == 6:
+                prep_wo(s - 5)
+            if s < NSTEP:
+                quant(s, 1)
+            if 0 < nxt < NSTEP and s > 0:
+                quant(nxt, 0)
+            if s == 7:
+                nc.vector.quantize_mx(out=woc[:].bitcast(FP8X4), scales=wos[:], in_=wog[:])
+            if s < NSTEP:
+                mx_bc(s, 0, 0, b_ps, "bps")
+                mx_bc(s, 1, 0, b_ps, "bps")
+            if 1 <= s <= NSTEP:
+                mx_bc(s - 1, 0, 1, c_ps, "cps")
+                mx_bc(s - 1, 1, 1, c_ps, "cps")
+            if s < NSTEP:
+                for rt in range(RT):
+                    v_t2(s, rt)
+                    v_t3(s, rt)
+                    add_hn(s, rt)
+            if 1 <= s <= NSTEP:
+                v_t4(s - 1, 0)
+                v_t4(s - 1, 1)
+            if s == 0:
+                quant(nxt, 0)
+            if s >= 2 and (s - 2) % NG == NG - 1:
+                fin_y((s - 2) // NG)
+            if s == NSTEP - 1:
+                for ct in range(CT - 1):
+                    silu(ct)
+        silu(CT - 1)
+
+        sc = const.tile([P, B], U32, name="sc", align_bytes=64)
+        ss = const.tile([P, B], U8, name="ss", align_bytes=64)
+        nc.vector.quantize_mx(out=sc[:].bitcast(FP8X4), scales=ss[:], in_=sg[:])
+        for rt in range(RT):
+            ops = pst.tile([P, 512], F32, name="ops%d" % rt, tag="st")
+            nc.tensor.matmul_mx(
+                out=ops[:],
+                lhsT=sc[:, rt * P : (rt + 1) * P].bitcast(FP8X4),
+                lhsT_scale=ss[:, rt * P : (rt + 1) * P],
+                rhs=woc[:].bitcast(FP8X4),
+                rhs_scale=wos[:],
+                start=True,
+                stop=True,
+            )
+            o_sb = tp.tile([P, D], F32, name="o_sb%d" % rt, tag="o_sb", bufs=2)
+            nc.vector.tensor_tensor(out=o_sb[:], in0=ops[:], in1=ob[:], op=ALU.add)
+            nc.sync.dma_start(out=out[rt * P : (rt + 1) * P, :], in_=o_sb[:])

@@ -394,6 +394,9 @@ def tile_mambacell_pa_kernel(
                 e_trans(s, 1)
             if nxt < NSTEP:
                 exps(nxt)
+            if 1 <= s <= NSTEP:
+                mx_bc(s - 1, 0, 1, c_ps, "cps")
+                mx_bc(s - 1, 1, 1, c_ps, "cps")
             if s >= 2:
                 y_acc(s - 2, 0)
                 y_acc(s - 2, 1)
@@ -403,29 +406,26 @@ def tile_mambacell_pa_kernel(
             if s == 5 or s == 6:
                 prep_wo(s - 5)
             if s < NSTEP:
+                mx_bc(s, 0, 0, b_ps, "bps")
+                mx_bc(s, 1, 0, b_ps, "bps")
+            if s < NSTEP:
                 quant(s, 1)
-            if 0 < nxt < NSTEP and s > 0:
+            if 0 < s and nxt < NSTEP:
                 quant(nxt, 0)
             if s == 7:
                 nc.vector.quantize_mx(out=woc[:].bitcast(FP8X4), scales=wos[:], in_=wog[:])
-            if s < NSTEP:
-                mx_bc(s, 0, 0, b_ps, "bps")
-                mx_bc(s, 1, 0, b_ps, "bps")
+            if s >= 2 and (s - 2) % NG == NG - 1:
+                fin_y((s - 2) // NG)
             if 1 <= s <= NSTEP:
-                mx_bc(s - 1, 0, 1, c_ps, "cps")
-                mx_bc(s - 1, 1, 1, c_ps, "cps")
+                v_t4(s - 1, 0)
+                v_t4(s - 1, 1)
             if s < NSTEP:
                 for rt in range(RT):
                     v_t2(s, rt)
                     v_t3(s, rt)
                     add_hn(s, rt)
-            if 1 <= s <= NSTEP:
-                v_t4(s - 1, 0)
-                v_t4(s - 1, 1)
             if s == 0:
                 quant(nxt, 0)
-            if s >= 2 and (s - 2) % NG == NG - 1:
-                fin_y((s - 2) // NG)
             if s == NSTEP - 1:
                 for ct in range(CT - 1):
                     silu(ct)

@@ -55,8 +55,13 @@ def tile_mambacell_pa_kernel(
 
         vrows = stg.tile([P, P], BF16, name="vrows")
         nc.vector.memset(vrows[:], 0.0)
+        one = stg.tile([P, 1], F32, name="one")
+        nc.vector.memset(one[:], 1.0)
         a_sb = stg.tile([P, CT * S], BF16, name="a_sb")
         ob = const.tile([P, D], BF16, name="ob")
+        nc.scalar.dma_start(out=vrows[0:CT, :], in_=dt_proj_b.rearrange("(t c) -> t c", c=P))
+        nc.scalar.dma_start(out=vrows[CT : 2 * CT, :], in_=d_param.rearrange("(t c) -> t c", c=P))
+        nc.scalar.dma_start(out=a_sb[:].rearrange("p (t n) -> p t n", t=CT), in_=a_log.rearrange("(t p) n -> p t n", p=P))
 
         x_sb = stg.tile([P, RT * D], BF16, name="x_sb")
         nc.sync.dma_start(
@@ -70,10 +75,7 @@ def tile_mambacell_pa_kernel(
         nc.sync.dma_start(
             out=inw_sb[:].rearrange("p (t k) -> p t k", t=CT), in_=in_proj_w.rearrange("(t p) k -> p t k", p=P)
         )
-        nc.scalar.dma_start(out=a_sb[:].rearrange("p (t n) -> p t n", t=CT), in_=a_log.rearrange("(t p) n -> p t n", p=P))
-        nc.scalar.dma_start(out=vrows[0:CT, :], in_=dt_proj_b.rearrange("(t c) -> t c", c=P))
-        nc.scalar.dma_start(out=vrows[CT : 2 * CT, :], in_=d_param.rearrange("(t c) -> t c", c=P))
-        nc.scalar.dma_start(out=ob[:], in_=out_proj_b.partition_broadcast(P))
+        wo_sb = stg.tile([P, CT * D], BF16, name="wo_sb")
 
         wview = bc_proj_w.rearrange("(t p j g n) k -> t g p j n k", p=P, j=2, g=NG, n=NN)
         hview = h.rearrange("b c n -> b (c n)")
@@ -110,7 +112,8 @@ def tile_mambacell_pa_kernel(
         load_h(0)
         load_w(1)
         load_w(2)
-        wo_sb = stg.tile([P, CT * D], BF16, name="wo_sb")
+
+        nc.scalar.activation(out=one[:], in_=one[:], func=ACT.Ln)
 
         def words_to_bank(src_words, first_col, name):
             ps = psw.tile([P, 512], F32, name=name, tag="wps")
@@ -141,26 +144,20 @@ def tile_mambacell_pa_kernel(
                 bank_to_grouped(engs[half], ps, grouped[:].bitcast(F32)[:, half * 512 : (half + 1) * 512])
             return grouped, codes, scales
 
-        a_exp = stg.tile([P, CT * S], F32, name="a_exp")
-        nc.scalar.activation(out=a_exp[:], in_=a_sb[:], func=ACT.Exp)
-
         dtg, dtc, dts = prep_512(dtw_sb, "dt", [nc.vector.tensor_copy, nc.scalar.copy])
         nc.vector.quantize_mx(out=xc[:].bitcast(FP8X4), scales=xs[:], in_=xg[:])
+        nc.vector.quantize_mx(out=dtc[:].bitcast(FP8X4), scales=dts[:], in_=dtg[:])
+        ing, inc, ins = prep_512(inw_sb, "in", [nc.scalar.copy, nc.vector.tensor_copy])
 
         vps = pst.tile([P, 1024], BF16, name="vps", tag="st")
         nc.tensor.transpose(vps[:, 0:P], vrows[:], ident_b[:])
         vec = const.tile([P, 2 * CT], F32, name="vec")
         nc.vector.tensor_copy(out=vec[:], in_=vps[:, 0 : 2 * CT])
-        nc.vector.quantize_mx(out=dtc[:].bitcast(FP8X4), scales=dts[:], in_=dtg[:])
-        neg_a = const.tile([P, CT * S], F32, name="neg_a")
-        nc.vector.tensor_scalar(out=neg_a[:], in0=a_exp[:], scalar1=-1.0, scalar2=None, op0=ALU.mult)
 
-        ing, inc, ins = prep_512(inw_sb, "in", [nc.scalar.copy, nc.scalar.copy])
-
-        def proj_t(codes, scales, nm):
+        def proj_t(codes, scales, nm, pool, tags):
             banks = []
             for half in range(2):
-                ps = pst.tile([P, 512], F32, name="pj_%s%d" % (nm, half), tag="st")
+                ps = pool.tile([P, 512], F32, name="pj_%s%d" % (nm, half), tag=tags[half])
                 for j in range(2):
                     ct = half * 2 + j
                     nc.tensor.matmul_mx(
@@ -175,40 +172,51 @@ def tile_mambacell_pa_kernel(
                 banks.append(ps)
             return banks
 
-        d_banks = proj_t(dtc, dts, "dt")
+        d_banks = proj_t(dtc, dts, "dt", pst, ["st", "st"])
         nc.vector.quantize_mx(out=inc[:].bitcast(FP8X4), scales=ins[:], in_=ing[:])
-        u_banks = proj_t(inc, ins, "in")
+        u_banks = proj_t(inc, ins, "in", psy, ["y0", "y1"])
 
-        sp_abs = stg.tile([P, CT * B], F32, name="sp_abs")
-        sp_exp = sp_abs
-        sp_ln = sp_abs
+        sp = stg.tile([P, CT * B], F32, name="sp")
         sp_max = stg.tile([P, CT * B], F32, name="sp_max")
         delta_t = const.tile([P, CT * B], F32, name="delta_t")
-        for ct in range(CT):
-            src = d_banks[ct // 2][:, (ct % 2) * B : (ct % 2 + 1) * B]
+        u_t = const.tile([P, CT * B], F32, name="u_t")
+        du_t = stg.tile([P, CT * B], F32, name="du_t")
+        du = const.tile([P, CT * B], F32, name="du")
+        a_exp = stg.tile([P, CT * S], F32, name="a_exp")
+        neg_a = const.tile([P, CT * S], F32, name="neg_a")
+
+        def cols(t, ct):
+            return t[:, ct * B : (ct + 1) * B]
+
+        def sp_abs(ct):
             nc.scalar.activation(
-                out=sp_abs[:, ct * B : (ct + 1) * B], in_=src, func=ACT.Abs, bias=vec[:, ct : ct + 1], scale=1.0
+                out=cols(sp, ct), in_=cols(d_banks[ct // 2], ct % 2), func=ACT.Abs, bias=vec[:, ct : ct + 1], scale=1.0
             )
+
+        def sp_relu(ct):
             nc.vector.tensor_scalar(
-                out=sp_max[:, ct * B : (ct + 1) * B],
-                in0=src,
+                out=cols(sp_max, ct),
+                in0=cols(d_banks[ct // 2], ct % 2),
                 scalar1=vec[:, ct : ct + 1],
                 scalar2=0.0,
                 op0=ALU.add,
                 op1=ALU.max,
             )
-        nc.scalar.activation(out=sp_exp[:], in_=sp_abs[:], func=ACT.Exp, scale=-1.0)
-        nc.scalar.activation(out=sp_ln[:], in_=sp_exp[:], func=ACT.Ln, bias=1.0, scale=1.0)
 
-        du_skip = const.tile([P, CT * B], F32, name="du_skip")
-        for ct in range(CT):
-            nc.vector.tensor_scalar(
-                out=du_skip[:, ct * B : (ct + 1) * B],
-                in0=u_banks[ct // 2][:, (ct % 2) * B : (ct % 2 + 1) * B],
-                scalar1=vec[:, CT + ct : CT + ct + 1],
-                scalar2=None,
-                op0=ALU.mult,
-            )
+        def sp_log(ct):
+            nc.scalar.activation(out=cols(sp, ct), in_=cols(sp, ct), func=ACT.Exp, scale=-1.0)
+            nc.scalar.activation(out=cols(sp, ct), in_=cols(sp, ct), func=ACT.Ln, bias=1.0, scale=1.0)
+
+        def sp_sum(ct, eng, u_src):
+            eng.tensor_tensor(out=cols(delta_t, ct), in0=cols(sp_max, ct), in1=cols(sp, ct), op=ALU.add)
+            eng.tensor_tensor(out=cols(du_t, ct), in0=u_src, in1=cols(delta_t, ct), op=ALU.mult)
+
+        def du_turn(ct, eng_copy):
+            dps = pst.tile([P, 512], F32, name="dups%d" % ct, tag="st")
+            for rt in range(RT):
+                nc.tensor.transpose(dps[:, rt * P : (rt + 1) * P], du_t[:, ct * B + rt * P : ct * B + (rt + 1) * P], ident_f[:])
+            eng_copy(out=cols(du, ct), in_=dps[:, 0:B])
+
         def w_tr(s, b):
             w_ps[(s, b)] = words_to_bank(wst[s][:].bitcast(F32), b * 512, "wps%d_%d" % (s, b))
 
@@ -239,7 +247,7 @@ def tile_mambacell_pa_kernel(
                 n = g * NN + i
                 nc.scalar.activation(
                     out=e_t[s][:, i * B : (i + 1) * B],
-                    in_=delta_t[:, ct * B : (ct + 1) * B],
+                    in_=cols(delta_t, ct),
                     func=ACT.Exp,
                     scale=neg_a[:, ct * S + n : ct * S + n + 1],
                 )
@@ -279,21 +287,20 @@ def tile_mambacell_pa_kernel(
             )
 
         def v_t3(s, rt):
-            ct = s // NG
+            lo = (s // NG * RT + rt) * P
             t3[(s, rt)] = tp.tile([P, 512], F32, name="t3_%d_%d" % (s, rt), tag="t3")
             nc.vector.tensor_tensor(
                 out=compact(t3[(s, rt)]),
                 in0=by_channel(b_ps[(s, rt)]),
-                in1=du[rt][:, ct * P : (ct + 1) * P].unsqueeze(2).to_broadcast([P, P, NN]),
+                in1=du[:, lo : lo + P].unsqueeze(2).to_broadcast([P, P, NN]),
                 op=ALU.mult,
             )
 
-        def add_hn(s, rt):
+        def add_hn(s, rt, eng):
             ct = s // NG
             g = s % NG
             if g == 0:
                 hn[(ct, rt)] = hnp.tile([P, P * S], F32, name="hn%d_%d" % (ct, rt), tag="hn")
-            eng = nc.gpsimd if ADD_ON_GPSIMD else nc.vector
             eng.tensor_tensor(out=natural(hn[(ct, rt)], g), in0=compact(t2[(s, rt)]), in1=compact(t3[(s, rt)]), op=ALU.add)
             if g == NG - 1:
                 nc.sync.dma_start(out=hnview[rt * P : (rt + 1) * P, ct * P * S : (ct + 1) * P * S], in_=hn[(ct, rt)][:])
@@ -317,45 +324,25 @@ def tile_mambacell_pa_kernel(
                     stop=(g == NG - 1 and i == NN - 1),
                 )
 
-        def fin_y(ct):
-            for rt in range(RT):
-                lo = ct * B + rt * P
-                nc.vector.tensor_tensor(
-                    out=y_f[:, lo : lo + P], in0=y_ps[rt][:, ct * P : (ct + 1) * P], in1=du_skip[:, lo : lo + P], op=ALU.add
-                )
-
-        def silu(ct):
-            nc.scalar.activation(
-                out=sg[:].rearrange("p (r t) -> p r t", t=CT)[:, :, ct], in_=y_f[:, ct * B : (ct + 1) * B], func=ACT.Silu
+        def fin_y(ct, rt):
+            lo = ct * B + rt * P
+            nc.vector.scalar_tensor_tensor(
+                out=y_f[:, lo : lo + P],
+                in0=u_t[:, lo : lo + P],
+                scalar=vec[:, CT + ct : CT + ct + 1],
+                in1=y_ps[rt][:, ct * P : (ct + 1) * P],
+                op0=ALU.mult,
+                op1=ALU.add,
             )
 
-        y_ps = [psy.tile([P, 512], F32, name="y_ps%d" % rt) for rt in range(RT)]
+        def silu(ct, rt):
+            lo = ct * B + rt * P
+            nc.scalar.activation(
+                out=sg[:].rearrange("p (r t) -> p r t", t=CT)[:, rt * P : (rt + 1) * P, ct], in_=y_f[:, lo : lo + P], func=ACT.Silu
+            )
+
         y_f = const.tile([P, CT * B], F32, name="y_f")
         sg = const.tile([P, CT * B], BF16, name="sg", align_bytes=64)
-
-        for b in range(4):
-            w_bank(0, b, nc.vector.tensor_copy)
-        w_tr(1, 0)
-        w_tr(1, 1)
-        quant(0, 0)
-        nc.vector.tensor_tensor(out=delta_t[:], in0=sp_max[:], in1=sp_ln[:], op=ALU.add)
-        du_t = stg.tile([P, CT * B], F32, name="du_t")
-        for half in range(2):
-            nc.vector.tensor_tensor(
-                out=du_t[:, half * 512 : (half + 1) * 512],
-                in0=u_banks[half][:],
-                in1=delta_t[:, half * 512 : (half + 1) * 512],
-                op=ALU.mult,
-            )
-        exps(0)
-        du = []
-        for rt in range(RT):
-            dps = pst.tile([P, 512], F32, name="dups%d" % rt, tag="st")
-            for ct in range(CT):
-                nc.tensor.transpose(dps[:, ct * P : (ct + 1) * P], du_t[:, ct * B + rt * P : ct * B + (rt + 1) * P], ident_f[:])
-            du.append(const.tile([P, D], F32, name="du%d" % rt))
-            nc.scalar.copy(out=du[rt][:], in_=dps[:])
-
         wog = stg.tile([P, 4 * D], BF16, name="wog", align_bytes=64)
         woc = const.tile([P, D], U32, name="woc", align_bytes=64)
         wos = const.tile([P, D], U8, name="wos", align_bytes=64)
@@ -373,71 +360,130 @@ def tile_mambacell_pa_kernel(
                 in_=ps[:].rearrange("p (a t o) -> p a o t", a=2, t=CT),
             )
 
-        for s in range(NSTEP + 2):
+        nc.scalar.activation(out=a_exp[:], in_=a_sb[:], func=ACT.Exp)
+        nc.vector.tensor_scalar(out=neg_a[:], in0=a_exp[:], scalar1=-1.0, scalar2=None, op0=ALU.mult)
+        sp_abs(0)
+        sp_relu(0)
+        sp_log(0)
+        sp_abs(1)
+        sp_relu(1)
+        sp_relu(2)
+        w_tr(0, 0)
+        w_tr(0, 1)
+        sp_sum(0, nc.vector, cols(u_banks[0], 0))
+        exps(0)
+        du_turn(0, nc.vector.tensor_copy)
+        sp_relu(3)
+        w_ev(0, 0, nc.vector.tensor_copy)
+        w_ev(0, 1, nc.vector.tensor_copy)
+        quant(0, 0)
+        sp_abs(2)
+        sp_abs(3)
+        e_trans(0, 0)
+        e_trans(0, 1)
+        w_bank(0, 2, nc.scalar.copy)
+        w_bank(0, 3, nc.scalar.copy)
+        mx_bc(0, 0, 0, b_ps, "bps")
+        mx_bc(0, 1, 0, b_ps, "bps")
+        add_eng = nc.gpsimd if ADD_ON_GPSIMD else nc.vector
+
+        for s in range(NSTEP):
             nxt = s + 1
             if s + PF < NSTEP:
                 load_w(s + PF)
             if s % NG == 1 and s // NG + 1 < CT:
                 load_h(s // NG + 1)
-            if s == 2:
+            if s == 8:
                 nc.sync.dma_start(
                     out=wo_sb[:].rearrange("p (t k) -> p t k", t=CT), in_=out_proj_w.rearrange("(t p) k -> p t k", p=P)
                 )
-            if s == 0:
-                w_ev(nxt, 0, nc.scalar.copy)
-                w_ev(nxt, 1, nc.scalar.copy)
-            elif nxt < NSTEP:
+                nc.sync.dma_start(out=ob[:], in_=out_proj_b.partition_broadcast(P))
+            if nxt < NSTEP:
                 w_bank(nxt, 0, nc.scalar.copy)
                 w_bank(nxt, 1, nc.scalar.copy)
-            if s < NSTEP:
+            if 0 < s < NSTEP:
                 e_trans(s, 0)
                 e_trans(s, 1)
             if nxt < NSTEP:
                 exps(nxt)
-            if 1 <= s <= NSTEP:
-                mx_bc(s - 1, 0, 1, c_ps, "cps")
-                mx_bc(s - 1, 1, 1, c_ps, "cps")
             if s >= 2:
                 y_acc(s - 2, 0)
                 y_acc(s - 2, 1)
-            if nxt < NSTEP:
+            if s == 0:
+                w_tr(nxt, 2)
+                w_tr(nxt, 3)
+            elif nxt < NSTEP:
                 w_bank(nxt, 2, nc.scalar.copy)
                 w_bank(nxt, 3, nc.scalar.copy)
-            if s == 5 or s == 6:
-                prep_wo(s - 5)
-            if s < NSTEP:
-                mx_bc(s, 0, 0, b_ps, "bps")
-                mx_bc(s, 1, 0, b_ps, "bps")
-            if s < NSTEP:
+            if s % NG == 1 and s // NG + 1 < CT:
+                sp_log(s // NG + 1)
+            if s % NG == 3 and s // NG + 1 < CT:
+                du_turn(s // NG + 1, nc.scalar.copy)
+            if s == NSTEP - 1:
+                prep_wo(0)
+                prep_wo(1)
+            if 0 < s < NSTEP:
                 quant(s, 1)
             if 0 < s and nxt < NSTEP:
                 quant(nxt, 0)
-            if s == 7:
-                nc.vector.quantize_mx(out=woc[:].bitcast(FP8X4), scales=wos[:], in_=wog[:])
-            if s >= 2 and (s - 2) % NG == NG - 1:
-                fin_y((s - 2) // NG)
+            if 0 < s < NSTEP:
+                mx_bc(s, 0, 0, b_ps, "bps")
+                mx_bc(s, 1, 0, b_ps, "bps")
             if 1 <= s <= NSTEP:
-                v_t4(s - 1, 0)
-                v_t4(s - 1, 1)
+                mx_bc(s - 1, 0, 1, c_ps, "cps")
+                mx_bc(s - 1, 1, 1, c_ps, "cps")
+            if s == NSTEP - 1:
+                mx_bc(s, 0, 1, c_ps, "cps")
+                mx_bc(s, 1, 1, c_ps, "cps")
+            if s >= 2 and (s - 2) % NG == NG - 1:
+                for rt in range(RT):
+                    fin_y((s - 2) // NG, rt)
+            if s % NG == 2 and s // NG + 1 < CT:
+                sp_sum(s // NG + 1, nc.vector, cols(u_t, s // NG + 1))
             if s < NSTEP:
                 for rt in range(RT):
                     v_t2(s, rt)
                     v_t3(s, rt)
-                    add_hn(s, rt)
+                    add_hn(s, rt, add_eng)
+            if 1 <= s <= NSTEP:
+                v_t4(s - 1, 0)
+                v_t4(s - 1, 1)
             if s == 0:
+                for half in range(2):
+                    nc.vector.tensor_copy(out=u_t[:, half * 512 : (half + 1) * 512], in_=u_banks[half][:])
+                w_ev(nxt, 2, nc.vector.tensor_copy)
+                w_ev(nxt, 3, nc.vector.tensor_copy)
+                quant(s, 1)
                 quant(nxt, 0)
+                y_ps = [psy.tile([P, 512], F32, name="y_ps%d" % rt, tag="y%d" % rt) for rt in range(RT)]
             if s == NSTEP - 1:
                 for ct in range(CT - 1):
-                    silu(ct)
-        silu(CT - 1)
+                    for rt in range(RT):
+                        silu(ct, rt)
 
+        last = NSTEP - 1
+        v_t4(last, 0)
+        v_t4(last, 1)
+        nc.vector.quantize_mx(out=woc[:].bitcast(FP8X4), scales=wos[:], in_=wog[:])
         sc = const.tile([P, B], U32, name="sc", align_bytes=64)
         ss = const.tile([P, B], U8, name="ss", align_bytes=64)
-        nc.vector.quantize_mx(out=sc[:].bitcast(FP8X4), scales=ss[:], in_=sg[:])
+        y_acc(last - 1, 0)
+        y_acc(last - 1, 1)
         for rt in range(RT):
-            ops = pst.tile([P, 512], F32, name="ops%d" % rt, tag="st")
+            y_acc(last, rt)
+            fin_y(CT - 1, rt)
+            silu(CT - 1, rt)
+        for rt in range(RT):
+            nc.vector.quantize_mx(
+                out=sc[:, rt * P : (rt + 1) * P].bitcast(FP8X4),
+                scales=ss[:, rt * P : (rt + 1) * P],
+                in_=sg[:, rt * 4 * P : (rt + 1) * 4 * P],
+            )
+        o_ps = []
+        for rt in range(RT):
+            o_ps.append(pst.tile([P, 512], F32, name="ops%d" % rt, tag="st"))
             nc.tensor.matmul_mx(
-                out=ops[:],
+                out=o_ps[rt][:],
                 lhsT=sc[:, rt * P : (rt + 1) * P].bitcast(FP8X4),
                 lhsT_scale=ss[:, rt * P : (rt + 1) * P],
                 rhs=woc[:].bitcast(FP8X4),
@@ -445,6 +491,7 @@ def tile_mambacell_pa_kernel(
                 start=True,
                 stop=True,
             )
+        for rt in range(RT):
             o_sb = tp.tile([P, D], F32, name="o_sb%d" % rt, tag="o_sb", bufs=2)
-            nc.vector.tensor_tensor(out=o_sb[:], in0=ops[:], in1=ob[:], op=ALU.add)
+            nc.vector.tensor_tensor(out=o_sb[:], in0=o_ps[rt][:], in1=ob[:], op=ALU.add)
             nc.sync.dma_start(out=out[rt * P : (rt + 1) * P, :], in_=o_sb[:])

@@ -26,6 +26,10 @@ FLOPS = 2 * B * D * (3 * D + 2 * D * S)
 
 PIN = True
 ADD_ON_GPSIMD = True
+GT2_FROM = 3
+V_EVAC = ((2, 0), (2, 1))
+U_ON_V = True
+SP_ALL = False
 
 
 def tile_mambacell_pa_kernel(
@@ -88,6 +92,7 @@ def tile_mambacell_pa_kernel(
         h_sb = {}
         e_t = {}
         e_ps = {}
+        e_sb = {}
         b_ps = {}
         c_ps = {}
         t2 = {}
@@ -113,7 +118,7 @@ def tile_mambacell_pa_kernel(
         load_w(1)
         load_w(2)
 
-        nc.scalar.activation(out=one[:], in_=one[:], func=ACT.Ln)
+        nc.scalar.activation(out=one[:], in_=one[:], func=ACT.Exp)
 
         def words_to_bank(src_words, first_col, name):
             ps = psw.tile([P, 512], F32, name=name, tag="wps")
@@ -203,9 +208,10 @@ def tile_mambacell_pa_kernel(
                 op1=ALU.max,
             )
 
-        def sp_log(ct):
-            nc.scalar.activation(out=cols(sp, ct), in_=cols(sp, ct), func=ACT.Exp, scale=-1.0)
-            nc.scalar.activation(out=cols(sp, ct), in_=cols(sp, ct), func=ACT.Ln, bias=1.0, scale=1.0)
+        def sp_log(lo, hi):
+            part = sp[:, lo * B : hi * B]
+            nc.scalar.activation(out=part, in_=part, func=ACT.Exp, scale=-1.0)
+            nc.scalar.activation(out=part, in_=part, func=ACT.Ln, bias=1.0, scale=1.0)
 
         def sp_sum(ct, eng, u_src):
             eng.tensor_tensor(out=cols(delta_t, ct), in0=cols(sp_max, ct), in1=cols(sp, ct), op=ALU.add)
@@ -286,6 +292,16 @@ def tile_mambacell_pa_kernel(
                 out=compact(t2[(s, rt)]), in0=by_channel(e_ps[(s, rt)]), in1=natural(h_sb[(s // NG, rt)], s % NG), op=ALU.mult
             )
 
+        def e_out(s, rt):
+            e_sb[(s, rt)] = tp.tile([P, 512], F32, name="esb_%d_%d" % (s, rt), tag="esb")
+            nc.scalar.copy(out=compact(e_sb[(s, rt)]), in_=by_channel(e_ps[(s, rt)]))
+
+        def g_t2(s, rt):
+            t2[(s, rt)] = tp.tile([P, 512], F32, name="t2_%d_%d" % (s, rt), tag="t2")
+            nc.gpsimd.tensor_tensor(
+                out=compact(t2[(s, rt)]), in0=compact(e_sb[(s, rt)]), in1=natural(h_sb[(s // NG, rt)], s % NG), op=ALU.mult
+            )
+
         def v_t3(s, rt):
             lo = (s // NG * RT + rt) * P
             t3[(s, rt)] = tp.tile([P, 512], F32, name="t3_%d_%d" % (s, rt), tag="t3")
@@ -364,21 +380,29 @@ def tile_mambacell_pa_kernel(
         nc.vector.tensor_scalar(out=neg_a[:], in0=a_exp[:], scalar1=-1.0, scalar2=None, op0=ALU.mult)
         sp_abs(0)
         sp_relu(0)
-        sp_log(0)
-        sp_abs(1)
-        sp_relu(1)
-        sp_relu(2)
+        if SP_ALL:
+            for ct in range(1, CT):
+                sp_abs(ct)
+                sp_relu(ct)
+            sp_log(0, CT)
+        else:
+            sp_log(0, 1)
+            sp_abs(1)
+            sp_relu(1)
+            sp_relu(2)
         w_tr(0, 0)
         w_tr(0, 1)
         sp_sum(0, nc.vector, cols(u_banks[0], 0))
         exps(0)
         du_turn(0, nc.vector.tensor_copy)
-        sp_relu(3)
+        if not SP_ALL:
+            sp_relu(3)
         w_ev(0, 0, nc.vector.tensor_copy)
         w_ev(0, 1, nc.vector.tensor_copy)
         quant(0, 0)
-        sp_abs(2)
-        sp_abs(3)
+        if not SP_ALL:
+            sp_abs(2)
+            sp_abs(3)
         e_trans(0, 0)
         e_trans(0, 1)
         w_bank(0, 2, nc.scalar.copy)
@@ -386,6 +410,9 @@ def tile_mambacell_pa_kernel(
         mx_bc(0, 0, 0, b_ps, "bps")
         mx_bc(0, 1, 0, b_ps, "bps")
         add_eng = nc.gpsimd if ADD_ON_GPSIMD else nc.vector
+
+        def ev_eng(s, b):
+            return nc.vector.tensor_copy if (s, b) in V_EVAC else nc.scalar.copy
 
         for s in range(NSTEP):
             nxt = s + 1
@@ -399,24 +426,23 @@ def tile_mambacell_pa_kernel(
                 )
                 nc.sync.dma_start(out=ob[:], in_=out_proj_b.partition_broadcast(P))
             if nxt < NSTEP:
-                w_bank(nxt, 0, nc.scalar.copy)
-                w_bank(nxt, 1, nc.scalar.copy)
+                w_bank(nxt, 0, ev_eng(nxt, 0))
+                w_bank(nxt, 1, ev_eng(nxt, 1))
             if 0 < s < NSTEP:
                 e_trans(s, 0)
                 e_trans(s, 1)
+                if s >= GT2_FROM:
+                    e_out(s, 1)
             if nxt < NSTEP:
                 exps(nxt)
             if s >= 2:
                 y_acc(s - 2, 0)
                 y_acc(s - 2, 1)
-            if s == 0:
-                w_tr(nxt, 2)
-                w_tr(nxt, 3)
-            elif nxt < NSTEP:
-                w_bank(nxt, 2, nc.scalar.copy)
-                w_bank(nxt, 3, nc.scalar.copy)
-            if s % NG == 1 and s // NG + 1 < CT:
-                sp_log(s // NG + 1)
+            if nxt < NSTEP:
+                w_bank(nxt, 2, ev_eng(nxt, 2))
+                w_bank(nxt, 3, ev_eng(nxt, 3))
+            if s == 1 and not SP_ALL:
+                sp_log(1, CT)
             if s % NG == 3 and s // NG + 1 < CT:
                 du_turn(s // NG + 1, nc.scalar.copy)
             if s == NSTEP - 1:
@@ -441,18 +467,26 @@ def tile_mambacell_pa_kernel(
             if s % NG == 2 and s // NG + 1 < CT:
                 sp_sum(s // NG + 1, nc.vector, cols(u_t, s // NG + 1))
             if s < NSTEP:
-                for rt in range(RT):
-                    v_t2(s, rt)
-                    v_t3(s, rt)
-                    add_hn(s, rt, add_eng)
+                if s >= GT2_FROM:
+                    g_t2(s, 1)
+                    v_t2(s, 0)
+                    v_t3(s, 0)
+                    add_hn(s, 0, add_eng)
+                    v_t3(s, 1)
+                    add_hn(s, 1, add_eng)
+                else:
+                    for rt in range(RT):
+                        v_t2(s, rt)
+                        v_t3(s, rt)
+                        add_hn(s, rt, add_eng)
             if 1 <= s <= NSTEP:
                 v_t4(s - 1, 0)
                 v_t4(s - 1, 1)
             if s == 0:
                 for half in range(2):
-                    nc.vector.tensor_copy(out=u_t[:, half * 512 : (half + 1) * 512], in_=u_banks[half][:])
-                w_ev(nxt, 2, nc.vector.tensor_copy)
-                w_ev(nxt, 3, nc.vector.tensor_copy)
+                    (nc.vector.tensor_copy if U_ON_V else nc.scalar.copy)(
+                        out=u_t[:, half * 512 : (half + 1) * 512], in_=u_banks[half][:]
+                    )
                 quant(s, 1)
                 quant(nxt, 0)
                 y_ps = [psy.tile([P, 512], F32, name="y_ps%d" % rt, tag="y%d" % rt) for rt in range(RT)]

@@ -26,7 +26,7 @@ FLOPS = 2 * B * D * (3 * D + 2 * D * S)
 
 PIN = True
 ADD_ON_GPSIMD = True
-GT2_FROM = 3
+GT2_FROM = 99
 V_EVAC = ((2, 0), (2, 1))
 U_ON_V = True
 SP_ALL = False

@@ -30,6 +30,9 @@ GT2_FROM = 99
 V_EVAC = ((2, 0), (2, 1))
 U_ON_V = True
 SP_ALL = False
+YLAG = 2
+GT2_EVERY = 1
+V_SUMS = (1,)
 
 
 def tile_mambacell_pa_kernel(
@@ -98,6 +101,7 @@ def tile_mambacell_pa_kernel(
         t2 = {}
         t3 = {}
         t4 = {}
+        t4r = {}
         hn = {}
 
         def load_w(s):
@@ -322,14 +326,30 @@ def tile_mambacell_pa_kernel(
                 nc.sync.dma_start(out=hnview[rt * P : (rt + 1) * P, ct * P * S : (ct + 1) * P * S], in_=hn[(ct, rt)][:])
 
         def v_t4(s, rt):
-            t4[(s, rt)] = tp.tile([P, 512], F32, name="t4_%d_%d" % (s, rt), tag="t4")
+            t4[(s, rt)] = tp.tile([P, 512], F32, name="t4_%d_%d" % (s, rt), tag="t4", bufs=8)
             nc.vector.tensor_tensor(
                 out=compact(t4[(s, rt)]), in0=by_channel(c_ps[(s, rt)]), in1=natural(hn[(s // NG, rt)], s % NG), op=ALU.mult
             )
+            if rt in V_SUMS:
+                v_sum(s, rt)
+
+        def v_sum(s, rt):
+            t4r[(s, rt)] = tp.tile([P, P], F32, name="t4r_%d_%d" % (s, rt), tag="t4r", bufs=4)
+            nc.vector.tensor_reduce(out=t4r[(s, rt)][:], in_=compact(t4[(s, rt)]), axis=mybir.AxisListType.X, op=ALU.add)
 
         def y_acc(s, rt):
             ct = s // NG
             g = s % NG
+            if rt in V_SUMS:
+                nc.tensor.matmul(
+                    out=y_ps[rt][:, ct * P : (ct + 1) * P],
+                    lhsT=t4r[(s, rt)][:],
+                    rhs=ident_f[:],
+                    is_transpose=True,
+                    start=(g == 0),
+                    stop=(g == NG - 1),
+                )
+                return
             for i in range(NN):
                 nc.tensor.matmul(
                     out=y_ps[rt][:, ct * P : (ct + 1) * P],
@@ -431,13 +451,13 @@ def tile_mambacell_pa_kernel(
             if 0 < s < NSTEP:
                 e_trans(s, 0)
                 e_trans(s, 1)
-                if s >= GT2_FROM:
+                if s >= GT2_FROM and s % GT2_EVERY == 0:
                     e_out(s, 1)
             if nxt < NSTEP:
                 exps(nxt)
-            if s >= 2:
-                y_acc(s - 2, 0)
-                y_acc(s - 2, 1)
+            if s >= YLAG:
+                y_acc(s - YLAG, 0)
+                y_acc(s - YLAG, 1)
             if nxt < NSTEP:
                 w_bank(nxt, 2, ev_eng(nxt, 2))
                 w_bank(nxt, 3, ev_eng(nxt, 3))
@@ -461,13 +481,13 @@ def tile_mambacell_pa_kernel(
             if s == NSTEP - 1:
                 mx_bc(s, 0, 1, c_ps, "cps")
                 mx_bc(s, 1, 1, c_ps, "cps")
-            if s >= 2 and (s - 2) % NG == NG - 1:
+            if s >= YLAG and (s - YLAG) % NG == NG - 1:
                 for rt in range(RT):
-                    fin_y((s - 2) // NG, rt)
+                    fin_y((s - YLAG) // NG, rt)
             if s % NG == 2 and s // NG + 1 < CT:
                 sp_sum(s // NG + 1, nc.vector, cols(u_t, s // NG + 1))
             if s < NSTEP:
-                if s >= GT2_FROM:
+                if s >= GT2_FROM and s % GT2_EVERY == 0:
                     g_t2(s, 1)
                     v_t2(s, 0)
                     v_t3(s, 0)
@@ -501,8 +521,9 @@ def tile_mambacell_pa_kernel(
         nc.vector.quantize_mx(out=woc[:].bitcast(FP8X4), scales=wos[:], in_=wog[:])
         sc = const.tile([P, B], U32, name="sc", align_bytes=64)
         ss = const.tile([P, B], U8, name="ss", align_bytes=64)
-        y_acc(last - 1, 0)
-        y_acc(last - 1, 1)
+        for s in range(NSTEP - YLAG, last):
+            y_acc(s, 0)
+            y_acc(s, 1)
         for rt in range(RT):
             y_acc(last, rt)
             fin_y(CT - 1, rt)

@@ -26,13 +26,14 @@ FLOPS = 2 * B * D * (3 * D + 2 * D * S)
 
 PIN = True
 ADD_ON_GPSIMD = True
-GT2_FROM = 99
+GT2_FROM = 3
 V_EVAC = ((2, 0), (2, 1))
 U_ON_V = True
 SP_ALL = False
-YLAG = 2
-GT2_EVERY = 1
-V_SUMS = (1,)
+YLAG = 3
+GT2_EVERY = 2
+SUM_ON_G = False
+V_SUMS = ()
 
 
 def tile_mambacell_pa_kernel(
@@ -484,7 +485,7 @@ def tile_mambacell_pa_kernel(
             if s >= YLAG and (s - YLAG) % NG == NG - 1:
                 for rt in range(RT):
                     fin_y((s - YLAG) // NG, rt)
-            if s % NG == 2 and s // NG + 1 < CT:
+            if s % NG == 2 and s // NG + 1 < CT and not SUM_ON_G:
                 sp_sum(s // NG + 1, nc.vector, cols(u_t, s // NG + 1))
             if s < NSTEP:
                 if s >= GT2_FROM and s % GT2_EVERY == 0:
@@ -499,6 +500,8 @@ def tile_mambacell_pa_kernel(
                         v_t2(s, rt)
                         v_t3(s, rt)
                         add_hn(s, rt, add_eng)
+            if s % NG == 2 and s // NG + 1 < CT and SUM_ON_G:
+                sp_sum(s // NG + 1, nc.gpsimd, cols(u_t, s // NG + 1))
             if 1 <= s <= NSTEP:
                 v_t4(s - 1, 0)
                 v_t4(s - 1, 1)

@@ -329,7 +329,7 @@ def tile_mambacell_pa_kernel(
         def v_t4(s, rt):
             t4[(s, rt)] = tp.tile([P, 512], F32, name="t4_%d_%d" % (s, rt), tag="t4", bufs=8)
             nc.vector.tensor_tensor(
-                out=compact(t4[(s, rt)]), in0=by_channel(c_ps[(s, rt)]), in1=natural(hn[(s // NG, rt)], s % NG), op=ALU.mult
+                out=by_channel(t4[(s, rt)]), in0=by_channel(c_ps[(s, rt)]), in1=natural(hn[(s // NG, rt)], s % NG), op=ALU.mult
             )
             if rt in V_SUMS:
                 v_sum(s, rt)
@@ -354,7 +354,7 @@ def tile_mambacell_pa_kernel(
             for i in range(NN):
                 nc.tensor.matmul(
                     out=y_ps[rt][:, ct * P : (ct + 1) * P],
-                    lhsT=compact(t4[(s, rt)])[:, :, i],
+                    lhsT=t4[(s, rt)][:, i * P : (i + 1) * P],
                     rhs=ident_f[:],
                     is_transpose=True,
                     start=(g == 0 and i == 0),

@@ -20,20 +20,31 @@ CT = D // P
 NG = 4
 NN = S // NG
 NSTEP = CT * NG
-PF = 3
 
 FLOPS = 2 * B * D * (3 * D + 2 * D * S)
 
-PIN = True
-ADD_ON_GPSIMD = True
-GT2_FROM = 3
-V_EVAC = ((2, 0), (2, 1))
-U_ON_V = True
-SP_ALL = False
-YLAG = 3
-GT2_EVERY = 2
-SUM_ON_G = False
-V_SUMS = ()
+W_BUFS = 2
+E_BUFS = 2
+BC_BUFS = 4
+WC_BUFS = 4
+WST_BUFS = 3
+Y_AT = (1, 3)
+DU_AT = 2
+W_RATE = 5
+W_AHEAD = 2
+Q_AHEAD = 1
+Y_TAG = "e"
+EXP_POS = 5
+ET_POS = 2
+V_ORDER = "ttqq"
+HI = 1
+QA = (4, 5, 2)
+SUM_AT = 1
+T4_BUFS = 13
+HN_BUFS = 4
+STORE_AT = (1, 2)
+V_EVAC = ()
+G_T2 = ()
 
 
 def tile_mambacell_pa_kernel(
@@ -41,49 +52,40 @@ def tile_mambacell_pa_kernel(
 ):
     nc = tc.nc
     with ExitStack() as ctx:
-        if PIN:
-            ctx.enter_context(tc.manual_schedule())
+        ctx.enter_context(tc.manual_schedule())
         const = ctx.enter_context(tc.tile_pool(name="const", bufs=1))
         stg = ctx.enter_context(tc.tile_pool(name="stg", bufs=1))
-        wstp = ctx.enter_context(tc.tile_pool(name="wstp", bufs=3))
+        wstp = ctx.enter_context(tc.tile_pool(name="wstp", bufs=WST_BUFS))
         wgp = ctx.enter_context(tc.tile_pool(name="wgp", bufs=2))
-        wcp = ctx.enter_context(tc.tile_pool(name="wcp", bufs=3))
+        wcp = ctx.enter_context(tc.tile_pool(name="wcp", bufs=WC_BUFS))
         hp = ctx.enter_context(tc.tile_pool(name="hp", bufs=4))
         ep = ctx.enter_context(tc.tile_pool(name="ep", bufs=3))
-        tp = ctx.enter_context(tc.tile_pool(name="tp", bufs=4))
-        hnp = ctx.enter_context(tc.tile_pool(name="hnp", bufs=4))
-        psw = ctx.enter_context(tc.psum_pool(name="psw", bufs=2))
-        pst = ctx.enter_context(tc.psum_pool(name="pst", bufs=4))
-        psy = ctx.enter_context(tc.psum_pool(name="psy", bufs=1))
+        tp = ctx.enter_context(tc.tile_pool(name="tp", bufs=3))
+        hnp = ctx.enter_context(tc.tile_pool(name="hnp", bufs=HN_BUFS))
+        psw = ctx.enter_context(tc.psum_pool(name="psw", bufs=W_BUFS))
+        pse = ctx.enter_context(tc.psum_pool(name="pse", bufs=E_BUFS))
+        psb = ctx.enter_context(tc.psum_pool(name="psb", bufs=BC_BUFS))
+        psy = ctx.enter_context(tc.psum_pool(name="psy", bufs=1)) if Y_TAG == "y" else pse
 
-        ident_f = const.tile([P, P], F32, name="ident_f")
-        make_identity(nc, ident_f[:])
-        ident_b = const.tile([P, P], BF16, name="ident_b")
-        make_identity(nc, ident_b[:])
-
-        vrows = stg.tile([P, P], BF16, name="vrows")
-        nc.vector.memset(vrows[:], 0.0)
         one = stg.tile([P, 1], F32, name="one")
         nc.vector.memset(one[:], 1.0)
+        vrows = stg.tile([P, P], BF16, name="vrows")
+        nc.vector.memset(vrows[:], 0.0)
         a_sb = stg.tile([P, CT * S], BF16, name="a_sb")
         ob = const.tile([P, D], BF16, name="ob")
         nc.scalar.dma_start(out=vrows[0:CT, :], in_=dt_proj_b.rearrange("(t c) -> t c", c=P))
         nc.scalar.dma_start(out=vrows[CT : 2 * CT, :], in_=d_param.rearrange("(t c) -> t c", c=P))
         nc.scalar.dma_start(out=a_sb[:].rearrange("p (t n) -> p t n", t=CT), in_=a_log.rearrange("(t p) n -> p t n", p=P))
+        nc.scalar.activation(out=one[:], in_=one[:], func=ACT.Ln)
+        ident_b = const.tile([P, P], BF16, name="ident_b")
+        make_identity(nc, ident_b[:])
+        ident_f = const.tile([P, P], F32, name="ident_f")
+        make_identity(nc, ident_f[:])
 
         x_sb = stg.tile([P, RT * D], BF16, name="x_sb")
         nc.sync.dma_start(
             out=x_sb[:].rearrange("p (t k) -> p t k", t=RT), in_=x.rearrange("(t p) k -> p t k", p=P)
         )
-        dtw_sb = stg.tile([P, CT * D], BF16, name="dtw_sb")
-        nc.sync.dma_start(
-            out=dtw_sb[:].rearrange("p (t k) -> p t k", t=CT), in_=dt_proj_w.rearrange("(t p) k -> p t k", p=P)
-        )
-        inw_sb = stg.tile([P, CT * D], BF16, name="inw_sb")
-        nc.sync.dma_start(
-            out=inw_sb[:].rearrange("p (t k) -> p t k", t=CT), in_=in_proj_w.rearrange("(t p) k -> p t k", p=P)
-        )
-        wo_sb = stg.tile([P, CT * D], BF16, name="wo_sb")
 
         wview = bc_proj_w.rearrange("(t p j g n) k -> t g p j n k", p=P, j=2, g=NG, n=NN)
         hview = h.rearrange("b c n -> b (c n)")
@@ -102,8 +104,8 @@ def tile_mambacell_pa_kernel(
         t2 = {}
         t3 = {}
         t4 = {}
-        t4r = {}
         hn = {}
+        y_ps = {}
 
         def load_w(s):
             wst[s] = wstp.tile([P, 2 * NN * D], BF16, name="wst%d" % s, tag="wst")
@@ -111,22 +113,45 @@ def tile_mambacell_pa_kernel(
                 out=wst[s][:].rearrange("p (j n k) -> p j n k", j=2, n=NN), in_=wview[s // NG, s % NG]
             )
 
-        def load_h(ct):
-            for rt in range(RT):
+        def load_w_half(s, j):
+            if j == 0:
+                wst[s] = wstp.tile([P, 2 * NN * D], BF16, name="wst%d" % s, tag="wst")
+            nc.sync.dma_start(
+                out=wst[s][:].rearrange("p (j n k) -> p j n k", j=2, n=NN)[:, j], in_=wview[s // NG, s % NG][:, j]
+            )
+
+        def load_rows(dst, w, half):
+            nc.sync.dma_start(
+                out=dst[:].rearrange("p (t k) -> p t k", t=CT)[:, 2 * half : 2 * half + 2],
+                in_=w.rearrange("(t p) k -> p t k", p=P)[:, 2 * half : 2 * half + 2],
+            )
+
+        def load_h(ct, rts=range(RT)):
+            for rt in rts:
                 h_sb[(ct, rt)] = hp.tile([P, P * S], BF16, name="h%d_%d" % (ct, rt), tag="h")
                 nc.sync.dma_start(
                     out=h_sb[(ct, rt)][:], in_=hview[rt * P : (rt + 1) * P, ct * P * S : (ct + 1) * P * S]
                 )
 
-        load_w(0)
-        load_h(0)
+        def store_h(ct, rt):
+            nc.sync.dma_start(out=hnview[rt * P : (rt + 1) * P, ct * P * S : (ct + 1) * P * S], in_=hn[(ct, rt)][:])
+
+        dtw_sb = stg.tile([P, CT * D], BF16, name="dtw_sb")
+        inw_sb = stg.tile([P, CT * D], BF16, name="inw_sb")
+        wo_sb = stg.tile([P, CT * D], BF16, name="wo_sb")
+        load_rows(dtw_sb, dt_proj_w, 0)
+        load_rows(inw_sb, in_proj_w, 0)
+        load_w_half(0, 0)
+        load_h(0, (0,))
+        load_h(0, (1,))
+        load_w_half(0, 1)
         load_w(1)
         load_w(2)
+        load_rows(dtw_sb, dt_proj_w, 1)
+        load_rows(inw_sb, in_proj_w, 1)
 
-        nc.scalar.activation(out=one[:], in_=one[:], func=ACT.Exp)
-
-        def words_to_bank(src_words, first_col, name):
-            ps = psw.tile([P, 512], F32, name=name, tag="wps")
+        def words_to_bank(src_words, first_col, name, pool=psw, tag="wps"):
+            ps = pool.tile([P, 512], F32, name=name, tag=tag)
             for j in range(2):
                 for u in range(2):
                     col = first_col + j * 256 + u * P
@@ -139,106 +164,23 @@ def tile_mambacell_pa_kernel(
                 in_=ps[:].rearrange("p (j u c) -> p j c u", j=2, u=2),
             )
 
-        xg = stg.tile([P, 4 * B], BF16, name="xg", align_bytes=64)
-        xc = const.tile([P, B], U32, name="xc", align_bytes=64)
-        xs = const.tile([P, B], U8, name="xs", align_bytes=64)
-        xp = words_to_bank(x_sb[:].bitcast(F32), 0, "xp")
-        bank_to_grouped(nc.vector.tensor_copy, xp, xg[:].bitcast(F32))
-
-        def prep_512(w_sb, nm, engs):
-            grouped = stg.tile([P, 4 * D], BF16, name="g_" + nm, align_bytes=64)
-            codes = const.tile([P, D], U32, name="c_" + nm, align_bytes=64)
-            scales = const.tile([P, D], U8, name="s_" + nm, align_bytes=64)
-            for half in range(2):
-                ps = words_to_bank(w_sb[:].bitcast(F32), half * 512, "ps_%s%d" % (nm, half))
-                bank_to_grouped(engs[half], ps, grouped[:].bitcast(F32)[:, half * 512 : (half + 1) * 512])
-            return grouped, codes, scales
-
-        dtg, dtc, dts = prep_512(dtw_sb, "dt", [nc.vector.tensor_copy, nc.scalar.copy])
-        nc.vector.quantize_mx(out=xc[:].bitcast(FP8X4), scales=xs[:], in_=xg[:])
-        nc.vector.quantize_mx(out=dtc[:].bitcast(FP8X4), scales=dts[:], in_=dtg[:])
-        ing, inc, ins = prep_512(inw_sb, "in", [nc.scalar.copy, nc.vector.tensor_copy])
-
-        vps = pst.tile([P, 1024], BF16, name="vps", tag="st")
-        nc.tensor.transpose(vps[:, 0:P], vrows[:], ident_b[:])
-        vec = const.tile([P, 2 * CT], F32, name="vec")
-        nc.vector.tensor_copy(out=vec[:], in_=vps[:, 0 : 2 * CT])
-
-        def proj_t(codes, scales, nm, pool, tags):
-            banks = []
-            for half in range(2):
-                ps = pool.tile([P, 512], F32, name="pj_%s%d" % (nm, half), tag=tags[half])
-                for j in range(2):
-                    ct = half * 2 + j
-                    nc.tensor.matmul_mx(
-                        out=ps[:, j * B : (j + 1) * B],
-                        lhsT=codes[:, ct * P : (ct + 1) * P].bitcast(FP8X4),
-                        lhsT_scale=scales[:, ct * P : (ct + 1) * P],
-                        rhs=xc[:].bitcast(FP8X4),
-                        rhs_scale=xs[:],
-                        start=True,
-                        stop=True,
-                    )
-                banks.append(ps)
-            return banks
-
-        d_banks = proj_t(dtc, dts, "dt", pst, ["st", "st"])
-        nc.vector.quantize_mx(out=inc[:].bitcast(FP8X4), scales=ins[:], in_=ing[:])
-        u_banks = proj_t(inc, ins, "in", psy, ["y0", "y1"])
-
-        sp = stg.tile([P, CT * B], F32, name="sp")
-        sp_max = stg.tile([P, CT * B], F32, name="sp_max")
-        delta_t = const.tile([P, CT * B], F32, name="delta_t")
-        u_t = const.tile([P, CT * B], F32, name="u_t")
-        du_t = stg.tile([P, CT * B], F32, name="du_t")
-        du = const.tile([P, CT * B], F32, name="du")
-        a_exp = stg.tile([P, CT * S], F32, name="a_exp")
-        neg_a = const.tile([P, CT * S], F32, name="neg_a")
-
-        def cols(t, ct):
-            return t[:, ct * B : (ct + 1) * B]
-
-        def sp_abs(ct):
-            nc.scalar.activation(
-                out=cols(sp, ct), in_=cols(d_banks[ct // 2], ct % 2), func=ACT.Abs, bias=vec[:, ct : ct + 1], scale=1.0
-            )
-
-        def sp_relu(ct):
-            nc.vector.tensor_scalar(
-                out=cols(sp_max, ct),
-                in0=cols(d_banks[ct // 2], ct % 2),
-                scalar1=vec[:, ct : ct + 1],
-                scalar2=0.0,
-                op0=ALU.add,
-                op1=ALU.max,
-            )
-
-        def sp_log(lo, hi):
-            part = sp[:, lo * B : hi * B]
-            nc.scalar.activation(out=part, in_=part, func=ACT.Exp, scale=-1.0)
-            nc.scalar.activation(out=part, in_=part, func=ACT.Ln, bias=1.0, scale=1.0)
-
-        def sp_sum(ct, eng, u_src):
-            eng.tensor_tensor(out=cols(delta_t, ct), in0=cols(sp_max, ct), in1=cols(sp, ct), op=ALU.add)
-            eng.tensor_tensor(out=cols(du_t, ct), in0=u_src, in1=cols(delta_t, ct), op=ALU.mult)
-
-        def du_turn(ct, eng_copy):
-            dps = pst.tile([P, 512], F32, name="dups%d" % ct, tag="st")
-            for rt in range(RT):
-                nc.tensor.transpose(dps[:, rt * P : (rt + 1) * P], du_t[:, ct * B + rt * P : ct * B + (rt + 1) * P], ident_f[:])
-            eng_copy(out=cols(du, ct), in_=dps[:, 0:B])
+        v_copy = nc.vector.tensor_copy
+        s_copy = nc.scalar.copy
 
         def w_tr(s, b):
             w_ps[(s, b)] = words_to_bank(wst[s][:].bitcast(F32), b * 512, "wps%d_%d" % (s, b))
 
-        def w_ev(s, b, eng_copy):
+        def w_ev(s, b):
+            bank_to_grouped_w(s, b, v_copy if (s, b) in V_EVAC else s_copy)
+
+        def bank_to_grouped_w(s, b, eng_copy):
             if b == 0:
                 wg[s] = wgp.tile([P, 4 * 2 * NN * P], BF16, name="wg%d" % s, tag="wg", align_bytes=64)
             bank_to_grouped(eng_copy, w_ps[(s, b)], wg[s][:].bitcast(F32)[:, b * 512 : (b + 1) * 512])
 
-        def w_bank(s, b, eng_copy):
+        def w_bank(s, b):
             w_tr(s, b)
-            w_ev(s, b, eng_copy)
+            w_ev(s, b)
 
         def quant(s, j):
             if j == 0:
@@ -249,6 +191,9 @@ def tile_mambacell_pa_kernel(
                 scales=ws[s][:, j * 512 : (j + 1) * 512],
                 in_=wg[s][:, j * 2048 : (j + 1) * 2048],
             )
+
+        def cols(t, ct):
+            return t[:, ct * B : (ct + 1) * B]
 
         def exps(s):
             ct = s // NG
@@ -264,14 +209,14 @@ def tile_mambacell_pa_kernel(
                 )
 
         def e_trans(s, rt):
-            e_ps[(s, rt)] = pst.tile([P, 512], F32, name="eps%d_%d" % (s, rt), tag="st")
+            e_ps[(s, rt)] = pse.tile([P, 512], F32, name="eps%d_%d" % (s, rt), tag="e")
             for i in range(NN):
                 nc.tensor.transpose(
                     e_ps[(s, rt)][:, i * P : (i + 1) * P], e_t[s][:, i * B + rt * P : i * B + (rt + 1) * P], ident_f[:]
                 )
 
         def mx_bc(s, rt, j, store, nm):
-            store[(s, rt)] = pst.tile([P, 512], F32, name="%s%d_%d" % (nm, s, rt), tag="st")
+            store[(s, rt)] = psb.tile([P, 512], F32, name="%s%d_%d" % (nm, s, rt), tag="bc")
             nc.tensor.matmul_mx(
                 out=store[(s, rt)][:],
                 lhsT=xc[:, rt * P : (rt + 1) * P].bitcast(FP8X4),
@@ -291,21 +236,17 @@ def tile_mambacell_pa_kernel(
         def natural(t, g):
             return t[:].rearrange("p (c n) -> p c n", n=S)[:, :, g * NN : (g + 1) * NN]
 
-        def v_t2(s, rt):
-            t2[(s, rt)] = tp.tile([P, 512], F32, name="t2_%d_%d" % (s, rt), tag="t2")
-            nc.vector.tensor_tensor(
-                out=compact(t2[(s, rt)]), in0=by_channel(e_ps[(s, rt)]), in1=natural(h_sb[(s // NG, rt)], s % NG), op=ALU.mult
-            )
-
         def e_out(s, rt):
-            e_sb[(s, rt)] = tp.tile([P, 512], F32, name="esb_%d_%d" % (s, rt), tag="esb")
+            e_sb[(s, rt)] = tp.tile([P, 512], F32, name="esb_%d_%d" % (s, rt), tag="esb", bufs=2)
             nc.scalar.copy(out=compact(e_sb[(s, rt)]), in_=by_channel(e_ps[(s, rt)]))
 
-        def g_t2(s, rt):
-            t2[(s, rt)] = tp.tile([P, 512], F32, name="t2_%d_%d" % (s, rt), tag="t2")
-            nc.gpsimd.tensor_tensor(
-                out=compact(t2[(s, rt)]), in0=compact(e_sb[(s, rt)]), in1=natural(h_sb[(s // NG, rt)], s % NG), op=ALU.mult
-            )
+        def mul_eh(s, rt):
+            t2[(s, rt)] = tp.tile([P, 512], F32, name="t2_%d_%d" % (s, rt), tag="t2", bufs=4)
+            hh = natural(h_sb[(s // NG, rt)], s % NG)
+            if rt == 1 and s in G_T2:
+                nc.gpsimd.tensor_tensor(out=compact(t2[(s, rt)]), in0=compact(e_sb[(s, rt)]), in1=hh, op=ALU.mult)
+            else:
+                nc.vector.tensor_tensor(out=compact(t2[(s, rt)]), in0=by_channel(e_ps[(s, rt)]), in1=hh, op=ALU.mult)
 
         def v_t3(s, rt):
             lo = (s // NG * RT + rt) * P
@@ -317,43 +258,26 @@ def tile_mambacell_pa_kernel(
                 op=ALU.mult,
             )
 
-        def add_hn(s, rt, eng):
+        def add_hn(s, rt):
             ct = s // NG
             g = s % NG
             if g == 0:
                 hn[(ct, rt)] = hnp.tile([P, P * S], F32, name="hn%d_%d" % (ct, rt), tag="hn")
-            eng.tensor_tensor(out=natural(hn[(ct, rt)], g), in0=compact(t2[(s, rt)]), in1=compact(t3[(s, rt)]), op=ALU.add)
-            if g == NG - 1:
-                nc.sync.dma_start(out=hnview[rt * P : (rt + 1) * P, ct * P * S : (ct + 1) * P * S], in_=hn[(ct, rt)][:])
+            nc.gpsimd.tensor_tensor(
+                out=natural(hn[(ct, rt)], g), in0=compact(t2[(s, rt)]), in1=compact(t3[(s, rt)]), op=ALU.add
+            )
 
         def v_t4(s, rt):
-            t4[(s, rt)] = tp.tile([P, 512], F32, name="t4_%d_%d" % (s, rt), tag="t4", bufs=8)
+            t4[(s, rt)] = tp.tile([P, 512], F32, name="t4_%d_%d" % (s, rt), tag="t4", bufs=T4_BUFS)
             nc.vector.tensor_tensor(
                 out=by_channel(t4[(s, rt)]), in0=by_channel(c_ps[(s, rt)]), in1=natural(hn[(s // NG, rt)], s % NG), op=ALU.mult
             )
-            if rt in V_SUMS:
-                v_sum(s, rt)
-
-        def v_sum(s, rt):
-            t4r[(s, rt)] = tp.tile([P, P], F32, name="t4r_%d_%d" % (s, rt), tag="t4r", bufs=4)
-            nc.vector.tensor_reduce(out=t4r[(s, rt)][:], in_=compact(t4[(s, rt)]), axis=mybir.AxisListType.X, op=ALU.add)
 
         def y_acc(s, rt):
-            ct = s // NG
             g = s % NG
-            if rt in V_SUMS:
-                nc.tensor.matmul(
-                    out=y_ps[rt][:, ct * P : (ct + 1) * P],
-                    lhsT=t4r[(s, rt)][:],
-                    rhs=ident_f[:],
-                    is_transpose=True,
-                    start=(g == 0),
-                    stop=(g == NG - 1),
-                )
-                return
             for i in range(NN):
                 nc.tensor.matmul(
-                    out=y_ps[rt][:, ct * P : (ct + 1) * P],
+                    out=y_ps[(s // NG, rt)][:, 0:P],
                     lhsT=t4[(s, rt)][:, i * P : (i + 1) * P],
                     rhs=ident_f[:],
                     is_transpose=True,
@@ -361,13 +285,16 @@ def tile_mambacell_pa_kernel(
                     stop=(g == NG - 1 and i == NN - 1),
                 )
 
+        def y_open(ct, rt, pool, tag):
+            y_ps[(ct, rt)] = pool.tile([P, 512], F32, name="y%d_%d" % (ct, rt), tag=tag)
+
         def fin_y(ct, rt):
             lo = ct * B + rt * P
             nc.vector.scalar_tensor_tensor(
                 out=y_f[:, lo : lo + P],
                 in0=u_t[:, lo : lo + P],
                 scalar=vec[:, CT + ct : CT + ct + 1],
-                in1=y_ps[rt][:, ct * P : (ct + 1) * P],
+                in1=y_ps[(ct, rt)][:, 0:P],
                 op0=ALU.mult,
                 op1=ALU.add,
             )
@@ -397,123 +324,245 @@ def tile_mambacell_pa_kernel(
                 in_=ps[:].rearrange("p (a t o) -> p a o t", a=2, t=CT),
             )
 
+        xg = stg.tile([P, 4 * B], BF16, name="xg", align_bytes=64)
+        xc = const.tile([P, B], U32, name="xc", align_bytes=64)
+        xs = const.tile([P, B], U8, name="xs", align_bytes=64)
+
+        def tiles_512(nm):
+            grouped = stg.tile([P, 4 * D], BF16, name="g_" + nm, align_bytes=64)
+            codes = const.tile([P, D], U32, name="c_" + nm, align_bytes=64)
+            scales = const.tile([P, D], U8, name="s_" + nm, align_bytes=64)
+            return grouped, codes, scales
+
+        def prep_half(w_sb, half, grouped, nm, eng, pool=psw, tag="wps"):
+            ps = words_to_bank(w_sb[:].bitcast(F32), half * 512, "ps_%s%d" % (nm, half), pool, tag)
+            bank_to_grouped(eng, ps, grouped[:].bitcast(F32)[:, half * 512 : (half + 1) * 512])
+
+        def quant_half(grouped, codes, scales, half):
+            nc.vector.quantize_mx(
+                out=codes[:, half * 256 : (half + 1) * 256].bitcast(FP8X4),
+                scales=scales[:, half * 256 : (half + 1) * 256],
+                in_=grouped[:, half * 1024 : (half + 1) * 1024],
+            )
+
+        dtg, dtc, dts = tiles_512("dt")
+        ing, inc, ins = tiles_512("in")
+
+        def proj_t(ct, codes, scales, ps):
+            j = ct % 2
+            nc.tensor.matmul_mx(
+                out=ps[:, j * B : (j + 1) * B],
+                lhsT=codes[:, ct * P : (ct + 1) * P].bitcast(FP8X4),
+                lhsT_scale=scales[:, ct * P : (ct + 1) * P],
+                rhs=xc[:].bitcast(FP8X4),
+                rhs_scale=xs[:],
+                start=True,
+                stop=True,
+            )
+
+        sp = stg.tile([P, CT * B], F32, name="sp")
+        sp_max = stg.tile([P, CT * B], F32, name="sp_max")
+        delta_t = const.tile([P, CT * B], F32, name="delta_t")
+        u_t = const.tile([P, CT * B], F32, name="u_t")
+        du_t = stg.tile([P, CT * B], F32, name="du_t")
+        du = const.tile([P, CT * B], F32, name="du")
+        a_exp = stg.tile([P, CT * S], F32, name="a_exp")
+        neg_a = const.tile([P, CT * S], F32, name="neg_a")
+        vec = const.tile([P, 2 * CT], F32, name="vec")
+
+        def sp_abs(ct):
+            nc.scalar.activation(
+                out=cols(sp, ct), in_=cols(d_banks[ct // 2], ct % 2), func=ACT.Abs, bias=vec[:, ct : ct + 1], scale=1.0
+            )
+
+        def sp_relu(ct):
+            nc.vector.tensor_scalar(
+                out=cols(sp_max, ct),
+                in0=cols(d_banks[ct // 2], ct % 2),
+                scalar1=vec[:, ct : ct + 1],
+                scalar2=0.0,
+                op0=ALU.add,
+                op1=ALU.max,
+            )
+
+        def sp_log(lo, hi):
+            part = sp[:, lo * B : hi * B]
+            nc.scalar.activation(out=part, in_=part, func=ACT.Exp, scale=-1.0)
+            nc.scalar.activation(out=part, in_=part, func=ACT.Ln, bias=1.0, scale=1.0)
+
+        def sp_sum(ct, eng):
+            eng.tensor_tensor(out=cols(delta_t, ct), in0=cols(sp_max, ct), in1=cols(sp, ct), op=ALU.add)
+
+        def du_mul(ct, eng, u_src):
+            eng.tensor_tensor(out=cols(du_t, ct), in0=u_src, in1=cols(delta_t, ct), op=ALU.mult)
+
+        def du_turn(ct, eng_copy):
+            dps = psy.tile([P, 512], F32, name="dups%d" % ct, tag=Y_TAG)
+            for rt in range(RT):
+                nc.tensor.transpose(dps[:, rt * P : (rt + 1) * P], du_t[:, ct * B + rt * P : ct * B + (rt + 1) * P], ident_f[:])
+            eng_copy(out=cols(du, ct), in_=dps[:, 0:B])
+
+        d_banks = {}
+        u_banks = {}
+
+        d_banks[0] = psb.tile([P, 512], F32, name="pj_dt0", tag="bc")
+        u_banks[0] = psb.tile([P, 512], F32, name="pj_in0", tag="bc")
+
+        vps = psy.tile([P, 1024], BF16, name="vps", tag=Y_TAG)
+        nc.tensor.transpose(vps[:, 0:P], vrows[:], ident_b[:])
+        nc.scalar.copy(out=vec[:], in_=vps[:, 0 : 2 * CT])
         nc.scalar.activation(out=a_exp[:], in_=a_sb[:], func=ACT.Exp)
+        xp = words_to_bank(x_sb[:].bitcast(F32), 0, "xp")
+        bank_to_grouped(v_copy, xp, xg[:].bitcast(F32))
+        prep_half(dtw_sb, 0, dtg, "dt", s_copy)
         nc.vector.tensor_scalar(out=neg_a[:], in0=a_exp[:], scalar1=-1.0, scalar2=None, op0=ALU.mult)
+        nc.vector.quantize_mx(out=xc[:].bitcast(FP8X4), scales=xs[:], in_=xg[:])
+        quant_half(dtg, dtc, dts, 0)
+        prep_half(inw_sb, 0, ing, "in", v_copy)
+        proj_t(0, dtc, dts, d_banks[0])
+        proj_t(1, dtc, dts, d_banks[0])
         sp_abs(0)
+        sp_abs(1)
         sp_relu(0)
-        if SP_ALL:
-            for ct in range(1, CT):
-                sp_abs(ct)
-                sp_relu(ct)
-            sp_log(0, CT)
-        else:
-            sp_log(0, 1)
-            sp_abs(1)
-            sp_relu(1)
-            sp_relu(2)
+        quant_half(ing, inc, ins, 0)
+        sp_log(0, 1)
         w_tr(0, 0)
         w_tr(0, 1)
-        sp_sum(0, nc.vector, cols(u_banks[0], 0))
+        proj_t(0, inc, ins, u_banks[0])
+        proj_t(1, inc, ins, u_banks[0])
+        bank_to_grouped_w(0, 0, v_copy)
+        sp_sum(0, nc.vector)
         exps(0)
-        du_turn(0, nc.vector.tensor_copy)
-        if not SP_ALL:
-            sp_relu(3)
-        w_ev(0, 0, nc.vector.tensor_copy)
-        w_ev(0, 1, nc.vector.tensor_copy)
+        bank_to_grouped_w(0, 1, v_copy)
+        du_mul(0, nc.vector, cols(u_banks[0], 0))
+        s_copy(out=u_t[:, 0:512], in_=u_banks[0][:])
+        sp_relu(1)
         quant(0, 0)
-        if not SP_ALL:
-            sp_abs(2)
-            sp_abs(3)
+        du_turn(0, v_copy)
         e_trans(0, 0)
         e_trans(0, 1)
-        w_bank(0, 2, nc.scalar.copy)
-        w_bank(0, 3, nc.scalar.copy)
-        mx_bc(0, 0, 0, b_ps, "bps")
-        mx_bc(0, 1, 0, b_ps, "bps")
-        add_eng = nc.gpsimd if ADD_ON_GPSIMD else nc.vector
+        mul_eh(0, 0)
+        for rt in range(RT):
+            mx_bc(0, rt, 0, b_ps, "bps")
+        mul_eh(0, 1)
+        w_bank(0, 2)
+        w_bank(0, 3)
+        exps(1)
 
-        def ev_eng(s, b):
-            return nc.vector.tensor_copy if (s, b) in V_EVAC else nc.scalar.copy
+        def w_upto(t):
+            return min(4 * NSTEP, 4 + W_RATE * (t + 1), 4 * (t + 2 + W_AHEAD))
 
-        for s in range(NSTEP):
-            nxt = s + 1
-            if s + PF < NSTEP:
-                load_w(s + PF)
-            if s % NG == 1 and s // NG + 1 < CT:
-                load_h(s // NG + 1)
-            if s == 8:
+        def q_upto(t):
+            return 1 if t < 0 else min(2 * NSTEP, QA[0] + QA[1] * t // QA[2], 2 * (t + 2 + Q_AHEAD))
+
+        for t in range(NSTEP):
+            last = t == NSTEP - 1
+            for s in range(3, min(NSTEP, w_upto(t - 1) // 4 + WST_BUFS)):
+                if s not in wst:
+                    load_w(s)
+            if t % NG == 1 and t // NG + 1 < CT:
+                load_h(t // NG + 1)
+            for rt in range(RT):
+                if t % NG == STORE_AT[rt] and t > NG - 1:
+                    store_h(t // NG - 1, rt)
+            if t == 8:
                 nc.sync.dma_start(
                     out=wo_sb[:].rearrange("p (t k) -> p t k", t=CT), in_=out_proj_w.rearrange("(t p) k -> p t k", p=P)
                 )
                 nc.sync.dma_start(out=ob[:], in_=out_proj_b.partition_broadcast(P))
-            if nxt < NSTEP:
-                w_bank(nxt, 0, ev_eng(nxt, 0))
-                w_bank(nxt, 1, ev_eng(nxt, 1))
-            if 0 < s < NSTEP:
-                e_trans(s, 0)
-                e_trans(s, 1)
-                if s >= GT2_FROM and s % GT2_EVERY == 0:
-                    e_out(s, 1)
-            if nxt < NSTEP:
-                exps(nxt)
-            if s >= YLAG:
-                y_acc(s - YLAG, 0)
-                y_acc(s - YLAG, 1)
-            if nxt < NSTEP:
-                w_bank(nxt, 2, ev_eng(nxt, 2))
-                w_bank(nxt, 3, ev_eng(nxt, 3))
-            if s == 1 and not SP_ALL:
-                sp_log(1, CT)
-            if s % NG == 3 and s // NG + 1 < CT:
-                du_turn(s // NG + 1, nc.scalar.copy)
-            if s == NSTEP - 1:
+            banks = [divmod(i, 4) for i in range(w_upto(t - 1), w_upto(t))]
+            if t == HI + 2:
+                for ct in (2, 3):
+                    sp_abs(ct)
+                    sp_relu(ct)
+            if t == HI + 3:
+                s_copy(out=u_t[:, 512:1024], in_=u_banks[1][:])
+            for rt in range(RT):
+                if t % NG == Y_AT[rt] and t // NG - 1 >= 0:
+                    ct = t // NG - 1
+                    y_open(ct, rt, psy, Y_TAG)
+                    for s in range(ct * NG, ct * NG + NG):
+                        y_acc(s, rt)
+            if t % NG == DU_AT and t // NG + 1 < CT:
+                du_turn(t // NG + 1, s_copy)
+            def e_part():
+                if not last:
+                    e_trans(t + 1, 0)
+                    e_trans(t + 1, 1)
+                    if t + 1 in G_T2:
+                        e_out(t + 1, 1)
+
+            for i in range(9):
+                if i == ET_POS:
+                    e_part()
+                if i == EXP_POS and t + 2 < NSTEP:
+                    exps(t + 2)
+                if i < len(banks):
+                    w_bank(*banks[i])
+            if t == NSTEP - 2:
+                for rt in range(RT):
+                    y_open(CT - 1, rt, psw, "wps")
+            if t >= NSTEP - 2:
+                for rt in range(RT):
+                    y_acc(t - 2, rt)
+            if t == HI:
+                prep_half(dtw_sb, 1, dtg, "dt", s_copy)
+                prep_half(inw_sb, 1, ing, "in", s_copy)
+            if t == 0:
+                sp_log(1, 2)
+            if t == HI + 3:
+                sp_log(2, CT)
+            if t == NSTEP - 3:
                 prep_wo(0)
                 prep_wo(1)
-            if 0 < s < NSTEP:
-                quant(s, 1)
-            if 0 < s and nxt < NSTEP:
-                quant(nxt, 0)
-            if 0 < s < NSTEP:
-                mx_bc(s, 0, 0, b_ps, "bps")
-                mx_bc(s, 1, 0, b_ps, "bps")
-            if 1 <= s <= NSTEP:
-                mx_bc(s - 1, 0, 1, c_ps, "cps")
-                mx_bc(s - 1, 1, 1, c_ps, "cps")
-            if s == NSTEP - 1:
-                mx_bc(s, 0, 1, c_ps, "cps")
-                mx_bc(s, 1, 1, c_ps, "cps")
-            if s >= YLAG and (s - YLAG) % NG == NG - 1:
+            v_t3(t, 0)
+            add_hn(t, 0)
+            v_t3(t, 1)
+            add_hn(t, 1)
+            if last:
                 for rt in range(RT):
-                    fin_y((s - YLAG) // NG, rt)
-            if s % NG == 2 and s // NG + 1 < CT and not SUM_ON_G:
-                sp_sum(s // NG + 1, nc.vector, cols(u_t, s // NG + 1))
-            if s < NSTEP:
-                if s >= GT2_FROM and s % GT2_EVERY == 0:
-                    g_t2(s, 1)
-                    v_t2(s, 0)
-                    v_t3(s, 0)
-                    add_hn(s, 0, add_eng)
-                    v_t3(s, 1)
-                    add_hn(s, 1, add_eng)
-                else:
-                    for rt in range(RT):
-                        v_t2(s, rt)
-                        v_t3(s, rt)
-                        add_hn(s, rt, add_eng)
-            if s % NG == 2 and s // NG + 1 < CT and SUM_ON_G:
-                sp_sum(s // NG + 1, nc.gpsimd, cols(u_t, s // NG + 1))
-            if 1 <= s <= NSTEP:
-                v_t4(s - 1, 0)
-                v_t4(s - 1, 1)
-            if s == 0:
-                for half in range(2):
-                    (nc.vector.tensor_copy if U_ON_V else nc.scalar.copy)(
-                        out=u_t[:, half * 512 : (half + 1) * 512], in_=u_banks[half][:]
-                    )
-                quant(s, 1)
-                quant(nxt, 0)
-                y_ps = [psy.tile([P, 512], F32, name="y_ps%d" % rt, tag="y%d" % rt) for rt in range(RT)]
-            if s == NSTEP - 1:
+                    store_h(CT - 1, rt)
+            if t > 0:
+                v_t4(t - 1, 0)
+                v_t4(t - 1, 1)
+            for rt in range(RT):
+                if t % NG == Y_AT[rt] and t // NG - 1 >= 0:
+                    fin_y(t // NG - 1, rt)
+            if t % NG == SUM_AT and t // NG + 1 < CT:
+                sp_sum(t // NG + 1, nc.gpsimd)
+                du_mul(t // NG + 1, nc.gpsimd, cols(u_t, t // NG + 1))
+            if t == HI + 1:
+                quant_half(dtg, dtc, dts, 1)
+                quant_half(ing, inc, ins, 1)
+            if not last:
+                qs = [divmod(i, 2) for i in range(q_upto(t - 1), q_upto(t))]
+                if V_ORDER == "tqqt":
+                    mul_eh(t + 1, 0)
+                for s, j in qs[:-2]:
+                    quant(s, j)
+                if V_ORDER == "ttqq":
+                    mul_eh(t + 1, 0)
+                    mul_eh(t + 1, 1)
+                for s, j in qs[-2:]:
+                    quant(s, j)
+                if V_ORDER == "tqqt":
+                    mul_eh(t + 1, 1)
+            if last:
+                nc.vector.quantize_mx(out=woc[:].bitcast(FP8X4), scales=wos[:], in_=wog[:])
+            if t == HI + 1:
+                d_banks[1] = psb.tile([P, 512], F32, name="pj_dt1", tag="bc")
+                for ct in (2, 3):
+                    proj_t(ct, dtc, dts, d_banks[1])
+            if t == HI + 2:
+                u_banks[1] = psb.tile([P, 512], F32, name="pj_in1", tag="bc")
+                for ct in (2, 3):
+                    proj_t(ct, inc, ins, u_banks[1])
+            if not last:
+                for rt in range(RT):
+                    mx_bc(t + 1, rt, 0, b_ps, "bps")
+            for rt in range(RT):
+                mx_bc(t, rt, 1, c_ps, "cps")
+            if t == NSTEP - 1:
                 for ct in range(CT - 1):
                     for rt in range(RT):
                         silu(ct, rt)
@@ -521,12 +570,11 @@ def tile_mambacell_pa_kernel(
         last = NSTEP - 1
         v_t4(last, 0)
         v_t4(last, 1)
-        nc.vector.quantize_mx(out=woc[:].bitcast(FP8X4), scales=wos[:], in_=wog[:])
         sc = const.tile([P, B], U32, name="sc", align_bytes=64)
         ss = const.tile([P, B], U8, name="ss", align_bytes=64)
-        for s in range(NSTEP - YLAG, last):
-            y_acc(s, 0)
-            y_acc(s, 1)
+        for s in range(last - 1, last):
+            for rt in range(RT):
+                y_acc(s, rt)
         for rt in range(RT):
             y_acc(last, rt)
             fin_y(CT - 1, rt)
@@ -539,7 +587,7 @@ def tile_mambacell_pa_kernel(
             )
         o_ps = []
         for rt in range(RT):
-            o_ps.append(pst.tile([P, 512], F32, name="ops%d" % rt, tag="st"))
+            o_ps.append(pse.tile([P, 512], F32, name="ops%d" % rt, tag="e"))
             nc.tensor.matmul_mx(
                 out=o_ps[rt][:],
                 lhsT=sc[:, rt * P : (rt + 1) * P].bitcast(FP8X4),

@@ -37,7 +37,6 @@ Y_TAG = "e"
 EXP_POS = 5
 ET_POS = 2
 V_ORDER = "ttqq"
-HI = 1
 QA = (4, 5, 2)
 SUM_AT = 1
 T4_BUFS = 13
@@ -73,10 +72,7 @@ def tile_mambacell_pa_kernel(
         nc.vector.memset(vrows[:], 0.0)
         a_sb = stg.tile([P, CT * S], BF16, name="a_sb")
         ob = const.tile([P, D], BF16, name="ob")
-        nc.scalar.dma_start(out=vrows[0:CT, :], in_=dt_proj_b.rearrange("(t c) -> t c", c=P))
-        nc.scalar.dma_start(out=vrows[CT : 2 * CT, :], in_=d_param.rearrange("(t c) -> t c", c=P))
-        nc.scalar.dma_start(out=a_sb[:].rearrange("p (t n) -> p t n", t=CT), in_=a_log.rearrange("(t p) n -> p t n", p=P))
-        nc.scalar.activation(out=one[:], in_=one[:], func=ACT.Ln)
+        nc.scalar.activation(out=one[:], in_=one[:], func=ACT.Exp)
         ident_b = const.tile([P, P], BF16, name="ident_b")
         make_identity(nc, ident_b[:])
         ident_f = const.tile([P, P], F32, name="ident_f")
@@ -139,16 +135,17 @@ def tile_mambacell_pa_kernel(
         dtw_sb = stg.tile([P, CT * D], BF16, name="dtw_sb")
         inw_sb = stg.tile([P, CT * D], BF16, name="inw_sb")
         wo_sb = stg.tile([P, CT * D], BF16, name="wo_sb")
+        nc.sync.dma_start(out=vrows[0:CT, :], in_=dt_proj_b.rearrange("(t c) -> t c", c=P))
+        nc.sync.dma_start(out=vrows[CT : 2 * CT, :], in_=d_param.rearrange("(t c) -> t c", c=P))
+        nc.sync.dma_start(out=a_sb[:].rearrange("p (t n) -> p t n", t=CT), in_=a_log.rearrange("(t p) n -> p t n", p=P))
         load_rows(dtw_sb, dt_proj_w, 0)
-        load_rows(inw_sb, in_proj_w, 0)
-        load_w_half(0, 0)
-        load_h(0, (0,))
-        load_h(0, (1,))
-        load_w_half(0, 1)
-        load_w(1)
-        load_w(2)
         load_rows(dtw_sb, dt_proj_w, 1)
+        load_w(0)
+        load_rows(inw_sb, in_proj_w, 0)
         load_rows(inw_sb, in_proj_w, 1)
+        load_w(1)
+        load_h(0)
+        load_w(2)
 
         def words_to_bank(src_words, first_col, name, pool=psw, tag="wps"):
             ps = pool.tile([P, 512], F32, name=name, tag=tag)
@@ -405,55 +402,72 @@ def tile_mambacell_pa_kernel(
         d_banks = {}
         u_banks = {}
 
-        d_banks[0] = psb.tile([P, 512], F32, name="pj_dt0", tag="bc")
-        u_banks[0] = psb.tile([P, 512], F32, name="pj_in0", tag="bc")
+        for half in range(2):
+            d_banks[half] = psb.tile([P, 512], F32, name="pj_dt%d" % half, tag="bc")
+        for half in range(2):
+            u_banks[half] = psb.tile([P, 512], F32, name="pj_in%d" % half, tag="bc")
 
-        vps = psy.tile([P, 1024], BF16, name="vps", tag=Y_TAG)
-        nc.tensor.transpose(vps[:, 0:P], vrows[:], ident_b[:])
-        nc.scalar.copy(out=vec[:], in_=vps[:, 0 : 2 * CT])
-        nc.scalar.activation(out=a_exp[:], in_=a_sb[:], func=ACT.Exp)
+        def v_bank(s, b):
+            w_tr(s, b)
+            bank_to_grouped_w(s, b, v_copy)
+
         xp = words_to_bank(x_sb[:].bitcast(F32), 0, "xp")
         bank_to_grouped(v_copy, xp, xg[:].bitcast(F32))
         prep_half(dtw_sb, 0, dtg, "dt", s_copy)
-        nc.vector.tensor_scalar(out=neg_a[:], in0=a_exp[:], scalar1=-1.0, scalar2=None, op0=ALU.mult)
         nc.vector.quantize_mx(out=xc[:].bitcast(FP8X4), scales=xs[:], in_=xg[:])
+        prep_half(dtw_sb, 1, dtg, "dt", v_copy, pse, "e")
         quant_half(dtg, dtc, dts, 0)
-        prep_half(inw_sb, 0, ing, "in", v_copy)
-        proj_t(0, dtc, dts, d_banks[0])
-        proj_t(1, dtc, dts, d_banks[0])
-        sp_abs(0)
-        sp_abs(1)
-        sp_relu(0)
-        quant_half(ing, inc, ins, 0)
-        sp_log(0, 1)
-        w_tr(0, 0)
-        w_tr(0, 1)
-        proj_t(0, inc, ins, u_banks[0])
-        proj_t(1, inc, ins, u_banks[0])
-        bank_to_grouped_w(0, 0, v_copy)
-        sp_sum(0, nc.vector)
-        exps(0)
-        bank_to_grouped_w(0, 1, v_copy)
-        du_mul(0, nc.vector, cols(u_banks[0], 0))
-        s_copy(out=u_t[:, 0:512], in_=u_banks[0][:])
-        sp_relu(1)
+        vps = pse.tile([P, 1024], BF16, name="vps", tag="e")
+        nc.tensor.transpose(vps[:, 0:P], vrows[:], ident_b[:])
+        nc.scalar.copy(out=vec[:], in_=vps[:, 0 : 2 * CT])
+        nc.scalar.activation(out=a_exp[:], in_=a_sb[:], func=ACT.Exp)
+        quant_half(dtg, dtc, dts, 1)
+        for ct in range(CT):
+            proj_t(ct, dtc, dts, d_banks[ct // 2])
+        for ct in range(CT):
+            sp_abs(ct)
+        for ct in range(CT):
+            sp_relu(ct)
+        sp_log(0, CT)
+        nc.scalar.activation(out=one[:], in_=sp[:, 0:1], func=ACT.Exp)
+        v_bank(0, 0)
+        v_bank(0, 1)
+        nc.vector.tensor_scalar(out=neg_a[:], in0=a_exp[:], scalar1=-1.0, scalar2=None, op0=ALU.mult)
+        v_bank(0, 2)
+        v_bank(0, 3)
         quant(0, 0)
-        du_turn(0, v_copy)
+        prep_half(inw_sb, 0, ing, "in", v_copy, pse, "e")
+        prep_half(inw_sb, 1, ing, "in", v_copy, pse, "e")
+        quant(0, 1)
+        sp_sum(0, nc.vector)
+        nc.vector.quantize_mx(out=inc[:].bitcast(FP8X4), scales=ins[:], in_=ing[:])
+        exps(0)
+        v_bank(1, 0)
+        v_bank(1, 1)
+        for ct in range(CT):
+            proj_t(ct, inc, ins, u_banks[ct // 2])
+        w_tr(1, 2)
+        w_tr(1, 3)
+        du_mul(0, nc.vector, cols(u_banks[0], 0))
+        bank_to_grouped_w(1, 2, v_copy)
         e_trans(0, 0)
-        e_trans(0, 1)
-        mul_eh(0, 0)
+        du_turn(0, v_copy)
         for rt in range(RT):
             mx_bc(0, rt, 0, b_ps, "bps")
-        mul_eh(0, 1)
-        w_bank(0, 2)
-        w_bank(0, 3)
+        mul_eh(0, 0)
+        bank_to_grouped_w(1, 3, s_copy)
+        for half in range(2):
+            s_copy(out=u_t[:, half * 512 : (half + 1) * 512], in_=u_banks[half][:])
         exps(1)
+        e_trans(0, 1)
+        mul_eh(0, 1)
+        quant(1, 0)
 
         def w_upto(t):
-            return min(4 * NSTEP, 4 + W_RATE * (t + 1), 4 * (t + 2 + W_AHEAD))
+            return min(4 * NSTEP, 8 + W_RATE * (t + 1), 4 * (t + 2 + W_AHEAD))
 
         def q_upto(t):
-            return 1 if t < 0 else min(2 * NSTEP, QA[0] + QA[1] * t // QA[2], 2 * (t + 2 + Q_AHEAD))
+            return 3 if t < 0 else min(2 * NSTEP, 2 * (t + 3))
 
         for t in range(NSTEP):
             last = t == NSTEP - 1
@@ -471,12 +485,6 @@ def tile_mambacell_pa_kernel(
                 )
                 nc.sync.dma_start(out=ob[:], in_=out_proj_b.partition_broadcast(P))
             banks = [divmod(i, 4) for i in range(w_upto(t - 1), w_upto(t))]
-            if t == HI + 2:
-                for ct in (2, 3):
-                    sp_abs(ct)
-                    sp_relu(ct)
-            if t == HI + 3:
-                s_copy(out=u_t[:, 512:1024], in_=u_banks[1][:])
             for rt in range(RT):
                 if t % NG == Y_AT[rt] and t // NG - 1 >= 0:
                     ct = t // NG - 1
@@ -505,13 +513,6 @@ def tile_mambacell_pa_kernel(
             if t >= NSTEP - 2:
                 for rt in range(RT):
                     y_acc(t - 2, rt)
-            if t == HI:
-                prep_half(dtw_sb, 1, dtg, "dt", s_copy)
-                prep_half(inw_sb, 1, ing, "in", s_copy)
-            if t == 0:
-                sp_log(1, 2)
-            if t == HI + 3:
-                sp_log(2, CT)
             if t == NSTEP - 3:
                 prep_wo(0)
                 prep_wo(1)
@@ -531,9 +532,6 @@ def tile_mambacell_pa_kernel(
             if t % NG == SUM_AT and t // NG + 1 < CT:
                 sp_sum(t // NG + 1, nc.gpsimd)
                 du_mul(t // NG + 1, nc.gpsimd, cols(u_t, t // NG + 1))
-            if t == HI + 1:
-                quant_half(dtg, dtc, dts, 1)
-                quant_half(ing, inc, ins, 1)
             if not last:
                 qs = [divmod(i, 2) for i in range(q_upto(t - 1), q_upto(t))]
                 if V_ORDER == "tqqt":
@@ -549,14 +547,6 @@ def tile_mambacell_pa_kernel(
                     mul_eh(t + 1, 1)
             if last:
                 nc.vector.quantize_mx(out=woc[:].bitcast(FP8X4), scales=wos[:], in_=wog[:])
-            if t == HI + 1:
-                d_banks[1] = psb.tile([P, 512], F32, name="pj_dt1", tag="bc")
-                for ct in (2, 3):
-                    proj_t(ct, dtc, dts, d_banks[1])
-            if t == HI + 2:
-                u_banks[1] = psb.tile([P, 512], F32, name="pj_in1", tag="bc")
-                for ct in (2, 3):
-                    proj_t(ct, inc, ins, u_banks[1])
             if not last:
                 for rt in range(RT):
                     mx_bc(t + 1, rt, 0, b_ps, "bps")

@@ -37,6 +37,7 @@ Y_TAG = "e"
 EXP_POS = 5
 ET_POS = 2
 V_ORDER = "ttqq"
+MB_POS = 3
 QA = (4, 5, 2)
 SUM_AT = 1
 T4_BUFS = 13
@@ -501,6 +502,9 @@ def tile_mambacell_pa_kernel(
                         e_out(t + 1, 1)
 
             for i in range(9):
+                if i == MB_POS and t > 2 and not last:
+                    for rt in range(RT):
+                        mx_bc(t + 1, rt, 0, b_ps, "bps")
                 if i == ET_POS:
                     e_part()
                 if i == EXP_POS and t + 2 < NSTEP:
@@ -547,7 +551,7 @@ def tile_mambacell_pa_kernel(
                     mul_eh(t + 1, 1)
             if last:
                 nc.vector.quantize_mx(out=woc[:].bitcast(FP8X4), scales=wos[:], in_=wog[:])
-            if not last:
+            if not last and t <= 2:
                 for rt in range(RT):
                     mx_bc(t + 1, rt, 0, b_ps, "bps")
             for rt in range(RT):

@@ -37,6 +37,7 @@ Y_TAG = "e"
 EXP_POS = 5
 ET_POS = 2
 V_ORDER = "ttqq"
+Q_WIDE = 1
 MB_POS = 3
 QA = (4, 5, 2)
 SUM_AT = 1
@@ -44,7 +45,7 @@ T4_BUFS = 13
 HN_BUFS = 4
 STORE_AT = (1, 2)
 V_EVAC = ()
-G_T2 = ()
+G_T2 = (5, 7, 9, 11, 13, 15)
 
 
 def tile_mambacell_pa_kernel(
@@ -141,9 +142,9 @@ def tile_mambacell_pa_kernel(
         nc.sync.dma_start(out=a_sb[:].rearrange("p (t n) -> p t n", t=CT), in_=a_log.rearrange("(t p) n -> p t n", p=P))
         load_rows(dtw_sb, dt_proj_w, 0)
         load_rows(dtw_sb, dt_proj_w, 1)
-        load_w(0)
         load_rows(inw_sb, in_proj_w, 0)
         load_rows(inw_sb, in_proj_w, 1)
+        load_w(0)
         load_w(1)
         load_h(0)
         load_w(2)
@@ -180,14 +181,14 @@ def tile_mambacell_pa_kernel(
             w_tr(s, b)
             w_ev(s, b)
 
-        def quant(s, j):
+        def quant(s, j, n=1):
             if j == 0:
                 wc[s] = wcp.tile([P, 2 * NN * P], U32, name="wc%d" % s, tag="wc", align_bytes=64)
                 ws[s] = wcp.tile([P, 2 * NN * P], U8, name="ws%d" % s, tag="ws", align_bytes=64)
             nc.vector.quantize_mx(
-                out=wc[s][:, j * 512 : (j + 1) * 512].bitcast(FP8X4),
-                scales=ws[s][:, j * 512 : (j + 1) * 512],
-                in_=wg[s][:, j * 2048 : (j + 1) * 2048],
+                out=wc[s][:, j * 512 : (j + n) * 512].bitcast(FP8X4),
+                scales=ws[s][:, j * 512 : (j + n) * 512],
+                in_=wg[s][:, j * 2048 : (j + n) * 2048],
             )
 
         def cols(t, ct):
@@ -394,8 +395,8 @@ def tile_mambacell_pa_kernel(
         def du_mul(ct, eng, u_src):
             eng.tensor_tensor(out=cols(du_t, ct), in0=u_src, in1=cols(delta_t, ct), op=ALU.mult)
 
-        def du_turn(ct, eng_copy):
-            dps = psy.tile([P, 512], F32, name="dups%d" % ct, tag=Y_TAG)
+        def du_turn(ct, eng_copy, pool=psy, tag=Y_TAG):
+            dps = pool.tile([P, 512], F32, name="dups%d" % ct, tag=tag)
             for rt in range(RT):
                 nc.tensor.transpose(dps[:, rt * P : (rt + 1) * P], du_t[:, ct * B + rt * P : ct * B + (rt + 1) * P], ident_f[:])
             eng_copy(out=cols(du, ct), in_=dps[:, 0:B])
@@ -413,16 +414,17 @@ def tile_mambacell_pa_kernel(
             bank_to_grouped_w(s, b, v_copy)
 
         xp = words_to_bank(x_sb[:].bitcast(F32), 0, "xp")
-        bank_to_grouped(v_copy, xp, xg[:].bitcast(F32))
+        bank_to_grouped(s_copy, xp, xg[:].bitcast(F32))
         prep_half(dtw_sb, 0, dtg, "dt", s_copy)
         nc.vector.quantize_mx(out=xc[:].bitcast(FP8X4), scales=xs[:], in_=xg[:])
-        prep_half(dtw_sb, 1, dtg, "dt", v_copy, pse, "e")
-        quant_half(dtg, dtc, dts, 0)
+        prep_half(dtw_sb, 1, dtg, "dt", s_copy, pse, "e")
         vps = pse.tile([P, 1024], BF16, name="vps", tag="e")
         nc.tensor.transpose(vps[:, 0:P], vrows[:], ident_b[:])
         nc.scalar.copy(out=vec[:], in_=vps[:, 0 : 2 * CT])
         nc.scalar.activation(out=a_exp[:], in_=a_sb[:], func=ACT.Exp)
-        quant_half(dtg, dtc, dts, 1)
+        nc.vector.quantize_mx(out=dtc[:].bitcast(FP8X4), scales=dts[:], in_=dtg[:])
+        prep_half(inw_sb, 0, ing, "in", v_copy)
+        prep_half(inw_sb, 1, ing, "in", v_copy)
         for ct in range(CT):
             proj_t(ct, dtc, dts, d_banks[ct // 2])
         for ct in range(CT):
@@ -431,37 +433,45 @@ def tile_mambacell_pa_kernel(
             sp_relu(ct)
         sp_log(0, CT)
         nc.scalar.activation(out=one[:], in_=sp[:, 0:1], func=ACT.Exp)
-        v_bank(0, 0)
-        v_bank(0, 1)
-        nc.vector.tensor_scalar(out=neg_a[:], in0=a_exp[:], scalar1=-1.0, scalar2=None, op0=ALU.mult)
-        v_bank(0, 2)
-        v_bank(0, 3)
-        quant(0, 0)
-        prep_half(inw_sb, 0, ing, "in", v_copy, pse, "e")
-        prep_half(inw_sb, 1, ing, "in", v_copy, pse, "e")
-        quant(0, 1)
-        sp_sum(0, nc.vector)
         nc.vector.quantize_mx(out=inc[:].bitcast(FP8X4), scales=ins[:], in_=ing[:])
-        exps(0)
-        v_bank(1, 0)
-        v_bank(1, 1)
+        w_tr(0, 0)
+        w_tr(0, 1)
         for ct in range(CT):
             proj_t(ct, inc, ins, u_banks[ct // 2])
-        w_tr(1, 2)
-        w_tr(1, 3)
-        du_mul(0, nc.vector, cols(u_banks[0], 0))
-        bank_to_grouped_w(1, 2, v_copy)
-        e_trans(0, 0)
-        du_turn(0, v_copy)
+        nc.gpsimd.tensor_scalar(out=neg_a[:], in0=a_exp[:], scalar1=-1.0, scalar2=0.0, op0=ALU.mult, op1=ALU.add)
+        sp_sum(0, nc.gpsimd)
+        bank_to_grouped_w(0, 0, v_copy)
+        bank_to_grouped_w(0, 1, v_copy)
+        w_tr(0, 2)
+        w_tr(0, 3)
+        quant(0, 0)
+        bank_to_grouped_w(0, 2, v_copy)
+        bank_to_grouped_w(0, 3, v_copy)
         for rt in range(RT):
             mx_bc(0, rt, 0, b_ps, "bps")
+        quant(0, 1)
+        w_tr(1, 0)
+        w_tr(1, 1)
+        bank_to_grouped_w(1, 0, v_copy)
+        du_mul(0, nc.vector, cols(u_banks[0], 0))
+        exps(0)
+        bank_to_grouped_w(1, 1, v_copy)
+        du_turn(0, v_copy, psw, "wps")
+        e_trans(0, 0)
+        e_trans(0, 1)
+        w_tr(1, 2)
+        w_tr(1, 3)
+        v_t3(0, 0)
+        v_t3(0, 1)
         mul_eh(0, 0)
+        add_hn(0, 0)
+        mul_eh(0, 1)
+        add_hn(0, 1)
+        exps(1)
+        bank_to_grouped_w(1, 2, s_copy)
         bank_to_grouped_w(1, 3, s_copy)
         for half in range(2):
             s_copy(out=u_t[:, half * 512 : (half + 1) * 512], in_=u_banks[half][:])
-        exps(1)
-        e_trans(0, 1)
-        mul_eh(0, 1)
         quant(1, 0)
 
         def w_upto(t):
@@ -520,10 +530,10 @@ def tile_mambacell_pa_kernel(
             if t == NSTEP - 3:
                 prep_wo(0)
                 prep_wo(1)
-            v_t3(t, 0)
-            add_hn(t, 0)
-            v_t3(t, 1)
-            add_hn(t, 1)
+            if t > 0:
+                for rt in range(RT):
+                    v_t3(t, rt)
+                    add_hn(t, rt)
             if last:
                 for rt in range(RT):
                     store_h(CT - 1, rt)
@@ -545,11 +555,14 @@ def tile_mambacell_pa_kernel(
                 if V_ORDER == "ttqq":
                     mul_eh(t + 1, 0)
                     mul_eh(t + 1, 1)
-                for s, j in qs[-2:]:
-                    quant(s, j)
+                if t >= Q_WIDE and len(qs) == 2:
+                    quant(qs[0][0], 0, 2)
+                else:
+                    for s, j in qs[-2:]:
+                        quant(s, j)
                 if V_ORDER == "tqqt":
                     mul_eh(t + 1, 1)
-            if last:
+            if t == NSTEP - 2:
                 nc.vector.quantize_mx(out=woc[:].bitcast(FP8X4), scales=wos[:], in_=wog[:])
             if not last and t <= 2:
                 for rt in range(RT):

@@ -27,7 +27,8 @@ W_BUFS = 2
 E_BUFS = 2
 BC_BUFS = 4
 WC_BUFS = 4
-WST_BUFS = 3
+WST_BUFS = 4
+H_EARLY = 5
 Y_AT = (1, 3)
 DU_AT = 2
 W_RATE = 5
@@ -38,9 +39,8 @@ EXP_POS = 5
 ET_POS = 2
 V_ORDER = "ttqq"
 Q_WIDE = 1
-MB_POS = 3
+MB_POS = 4
 QA = (4, 5, 2)
-SUM_AT = 1
 T4_BUFS = 13
 HN_BUFS = 4
 STORE_AT = (1, 2)
@@ -134,20 +134,21 @@ def tile_mambacell_pa_kernel(
         def store_h(ct, rt):
             nc.sync.dma_start(out=hnview[rt * P : (rt + 1) * P, ct * P * S : (ct + 1) * P * S], in_=hn[(ct, rt)][:])
 
-        dtw_sb = stg.tile([P, CT * D], BF16, name="dtw_sb")
+        dtw_sb = stg.tile([P, CT * D], BF16, name="dtw_sb", tag="w512")
         inw_sb = stg.tile([P, CT * D], BF16, name="inw_sb")
-        wo_sb = stg.tile([P, CT * D], BF16, name="wo_sb")
-        nc.sync.dma_start(out=vrows[0:CT, :], in_=dt_proj_b.rearrange("(t c) -> t c", c=P))
-        nc.sync.dma_start(out=vrows[CT : 2 * CT, :], in_=d_param.rearrange("(t c) -> t c", c=P))
-        nc.sync.dma_start(out=a_sb[:].rearrange("p (t n) -> p t n", t=CT), in_=a_log.rearrange("(t p) n -> p t n", p=P))
         load_rows(dtw_sb, dt_proj_w, 0)
         load_rows(dtw_sb, dt_proj_w, 1)
+        nc.sync.dma_start(out=vrows[0:CT, :], in_=dt_proj_b.rearrange("(t c) -> t c", c=P))
+        nc.sync.dma_start(out=vrows[CT : 2 * CT, :], in_=d_param.rearrange("(t c) -> t c", c=P))
         load_rows(inw_sb, in_proj_w, 0)
         load_rows(inw_sb, in_proj_w, 1)
         load_w(0)
+        nc.sync.dma_start(out=a_sb[:].rearrange("p (t n) -> p t n", t=CT), in_=a_log.rearrange("(t p) n -> p t n", p=P))
         load_w(1)
         load_h(0)
         load_w(2)
+        load_w(3)
+        load_h(1)
 
         def words_to_bank(src_words, first_col, name, pool=psw, tag="wps"):
             ps = pool.tile([P, 512], F32, name=name, tag=tag)
@@ -287,7 +288,7 @@ def tile_mambacell_pa_kernel(
         def y_open(ct, rt, pool, tag):
             y_ps[(ct, rt)] = pool.tile([P, 512], F32, name="y%d_%d" % (ct, rt), tag=tag)
 
-        def fin_y(ct, rt):
+        def fin_y(ct, rt, y_f):
             lo = ct * B + rt * P
             nc.vector.scalar_tensor_tensor(
                 out=y_f[:, lo : lo + P],
@@ -298,19 +299,17 @@ def tile_mambacell_pa_kernel(
                 op1=ALU.add,
             )
 
-        def silu(ct, rt):
+        def silu(ct, rt, y_f):
             lo = ct * B + rt * P
             nc.scalar.activation(
                 out=sg[:].rearrange("p (r t) -> p r t", t=CT)[:, rt * P : (rt + 1) * P, ct], in_=y_f[:, lo : lo + P], func=ACT.Silu
             )
 
-        y_f = const.tile([P, CT * B], F32, name="y_f")
         sg = const.tile([P, CT * B], BF16, name="sg", align_bytes=64)
-        wog = stg.tile([P, 4 * D], BF16, name="wog", align_bytes=64)
         woc = const.tile([P, D], U32, name="woc", align_bytes=64)
         wos = const.tile([P, D], U8, name="wos", align_bytes=64)
 
-        def prep_wo(half):
+        def prep_wo(half, wo_sb, wog):
             ps = psw.tile([P, 1024], BF16, name="wops%d" % half, tag="wps")
             for a in range(2):
                 ot = half * 2 + a
@@ -327,8 +326,8 @@ def tile_mambacell_pa_kernel(
         xc = const.tile([P, B], U32, name="xc", align_bytes=64)
         xs = const.tile([P, B], U8, name="xs", align_bytes=64)
 
-        def tiles_512(nm):
-            grouped = stg.tile([P, 4 * D], BF16, name="g_" + nm, align_bytes=64)
+        def tiles_512(nm, tag):
+            grouped = stg.tile([P, 4 * D], BF16, name="g_" + nm, tag=tag, align_bytes=64)
             codes = const.tile([P, D], U32, name="c_" + nm, align_bytes=64)
             scales = const.tile([P, D], U8, name="s_" + nm, align_bytes=64)
             return grouped, codes, scales
@@ -344,8 +343,8 @@ def tile_mambacell_pa_kernel(
                 in_=grouped[:, half * 1024 : (half + 1) * 1024],
             )
 
-        dtg, dtc, dts = tiles_512("dt")
-        ing, inc, ins = tiles_512("in")
+        dtg, dtc, dts = tiles_512("dt", "g512")
+        ing, inc, ins = tiles_512("in", "g_in")
 
         def proj_t(ct, codes, scales, ps):
             j = ct % 2
@@ -359,7 +358,7 @@ def tile_mambacell_pa_kernel(
                 stop=True,
             )
 
-        sp = stg.tile([P, CT * B], F32, name="sp")
+        sp = stg.tile([P, CT * B], F32, name="sp", tag="sp")
         sp_max = stg.tile([P, CT * B], F32, name="sp_max")
         delta_t = const.tile([P, CT * B], F32, name="delta_t")
         u_t = const.tile([P, CT * B], F32, name="u_t")
@@ -389,11 +388,9 @@ def tile_mambacell_pa_kernel(
             nc.scalar.activation(out=part, in_=part, func=ACT.Exp, scale=-1.0)
             nc.scalar.activation(out=part, in_=part, func=ACT.Ln, bias=1.0, scale=1.0)
 
-        def sp_sum(ct, eng):
-            eng.tensor_tensor(out=cols(delta_t, ct), in0=cols(sp_max, ct), in1=cols(sp, ct), op=ALU.add)
-
-        def du_mul(ct, eng, u_src):
-            eng.tensor_tensor(out=cols(du_t, ct), in0=u_src, in1=cols(delta_t, ct), op=ALU.mult)
+        def sp_sum(lo, hi):
+            part = slice(lo * B, hi * B)
+            nc.gpsimd.tensor_tensor(out=delta_t[:, part], in0=sp_max[:, part], in1=sp[:, part], op=ALU.add)
 
         def du_turn(ct, eng_copy, pool=psy, tag=Y_TAG):
             dps = pool.tile([P, 512], F32, name="dups%d" % ct, tag=tag)
@@ -421,7 +418,6 @@ def tile_mambacell_pa_kernel(
         vps = pse.tile([P, 1024], BF16, name="vps", tag="e")
         nc.tensor.transpose(vps[:, 0:P], vrows[:], ident_b[:])
         nc.scalar.copy(out=vec[:], in_=vps[:, 0 : 2 * CT])
-        nc.scalar.activation(out=a_exp[:], in_=a_sb[:], func=ACT.Exp)
         nc.vector.quantize_mx(out=dtc[:].bitcast(FP8X4), scales=dts[:], in_=dtg[:])
         prep_half(inw_sb, 0, ing, "in", v_copy)
         prep_half(inw_sb, 1, ing, "in", v_copy)
@@ -432,14 +428,15 @@ def tile_mambacell_pa_kernel(
         for ct in range(CT):
             sp_relu(ct)
         sp_log(0, CT)
-        nc.scalar.activation(out=one[:], in_=sp[:, 0:1], func=ACT.Exp)
+        nc.scalar.activation(out=a_exp[:], in_=a_sb[:], func=ACT.Exp)
+        nc.scalar.activation(out=neg_a[:], in_=a_exp[:], func=ACT.Copy, scale=-1.0)
         nc.vector.quantize_mx(out=inc[:].bitcast(FP8X4), scales=ins[:], in_=ing[:])
         w_tr(0, 0)
         w_tr(0, 1)
         for ct in range(CT):
             proj_t(ct, inc, ins, u_banks[ct // 2])
-        nc.gpsimd.tensor_scalar(out=neg_a[:], in0=a_exp[:], scalar1=-1.0, scalar2=0.0, op0=ALU.mult, op1=ALU.add)
-        sp_sum(0, nc.gpsimd)
+        sp_sum(0, 1)
+        sp_sum(1, CT)
         bank_to_grouped_w(0, 0, v_copy)
         bank_to_grouped_w(0, 1, v_copy)
         w_tr(0, 2)
@@ -452,15 +449,14 @@ def tile_mambacell_pa_kernel(
         quant(0, 1)
         w_tr(1, 0)
         w_tr(1, 1)
-        bank_to_grouped_w(1, 0, v_copy)
-        du_mul(0, nc.vector, cols(u_banks[0], 0))
+        for half in range(2):
+            v_copy(out=u_t[:, half * 512 : (half + 1) * 512], in_=u_banks[half][:])
+        nc.vector.tensor_tensor(out=cols(du_t, 0), in0=cols(u_banks[0], 0), in1=cols(delta_t, 0), op=ALU.mult)
         exps(0)
-        bank_to_grouped_w(1, 1, v_copy)
-        du_turn(0, v_copy, psw, "wps")
+        du_turn(0, v_copy)
         e_trans(0, 0)
         e_trans(0, 1)
-        w_tr(1, 2)
-        w_tr(1, 3)
+        nc.gpsimd.tensor_tensor(out=du_t[:, B:], in0=u_t[:, B:], in1=delta_t[:, B:], op=ALU.mult)
         v_t3(0, 0)
         v_t3(0, 1)
         mul_eh(0, 0)
@@ -468,29 +464,39 @@ def tile_mambacell_pa_kernel(
         mul_eh(0, 1)
         add_hn(0, 1)
         exps(1)
-        bank_to_grouped_w(1, 2, s_copy)
-        bank_to_grouped_w(1, 3, s_copy)
-        for half in range(2):
-            s_copy(out=u_t[:, half * 512 : (half + 1) * 512], in_=u_banks[half][:])
+        bank_to_grouped_w(1, 0, s_copy)
+        bank_to_grouped_w(1, 1, s_copy)
+        e_trans(1, 0)
+        e_trans(1, 1)
+        w_tr(1, 2)
+        w_tr(1, 3)
+        mul_eh(1, 0)
+        mul_eh(1, 1)
+        bank_to_grouped_w(1, 2, v_copy)
+        bank_to_grouped_w(1, 3, v_copy)
         quant(1, 0)
+        quant(1, 1)
 
         def w_upto(t):
             return min(4 * NSTEP, 8 + W_RATE * (t + 1), 4 * (t + 2 + W_AHEAD))
 
         def q_upto(t):
-            return 3 if t < 0 else min(2 * NSTEP, 2 * (t + 3))
+            return 4 if t < 0 else min(2 * NSTEP, 2 * (t + 3))
 
         for t in range(NSTEP):
             last = t == NSTEP - 1
-            for s in range(3, min(NSTEP, w_upto(t - 1) // 4 + WST_BUFS)):
+            for s in range(4, min(NSTEP, w_upto(t - 1) // 4 + WST_BUFS)):
                 if s not in wst:
                     load_w(s)
-            if t % NG == 1 and t // NG + 1 < CT:
-                load_h(t // NG + 1)
+            for rt in range(RT):
+                s = t + H_EARLY - rt
+                if s % NG == 0 and s // NG in range(2, CT):
+                    load_h(s // NG, (rt,))
             for rt in range(RT):
                 if t % NG == STORE_AT[rt] and t > NG - 1:
                     store_h(t // NG - 1, rt)
             if t == 8:
+                wo_sb = stg.tile([P, CT * D], BF16, name="wo_sb", tag="w512")
                 nc.sync.dma_start(
                     out=wo_sb[:].rearrange("p (t k) -> p t k", t=CT), in_=out_proj_w.rearrange("(t p) k -> p t k", p=P)
                 )
@@ -505,14 +511,14 @@ def tile_mambacell_pa_kernel(
             if t % NG == DU_AT and t // NG + 1 < CT:
                 du_turn(t // NG + 1, s_copy)
             def e_part():
-                if not last:
+                if 0 < t < NSTEP - 1:
                     e_trans(t + 1, 0)
                     e_trans(t + 1, 1)
                     if t + 1 in G_T2:
                         e_out(t + 1, 1)
 
             for i in range(9):
-                if i == MB_POS and t > 2 and not last:
+                if i == MB_POS and not last:
                     for rt in range(RT):
                         mx_bc(t + 1, rt, 0, b_ps, "bps")
                 if i == ET_POS:
@@ -528,8 +534,9 @@ def tile_mambacell_pa_kernel(
                 for rt in range(RT):
                     y_acc(t - 2, rt)
             if t == NSTEP - 3:
-                prep_wo(0)
-                prep_wo(1)
+                wog = stg.tile([P, 4 * D], BF16, name="wog", tag="g512", align_bytes=64)
+                prep_wo(0, wo_sb, wog)
+                prep_wo(1, wo_sb, wog)
             if t > 0:
                 for rt in range(RT):
                     v_t3(t, rt)
@@ -542,17 +549,16 @@ def tile_mambacell_pa_kernel(
                 v_t4(t - 1, 1)
             for rt in range(RT):
                 if t % NG == Y_AT[rt] and t // NG - 1 >= 0:
-                    fin_y(t // NG - 1, rt)
-            if t % NG == SUM_AT and t // NG + 1 < CT:
-                sp_sum(t // NG + 1, nc.gpsimd)
-                du_mul(t // NG + 1, nc.gpsimd, cols(u_t, t // NG + 1))
+                    fin_y(t // NG - 1, rt, y_f)
+            if t == 1:
+                y_f = stg.tile([P, CT * B], F32, name="y_f", tag="sp")
             if not last:
                 qs = [divmod(i, 2) for i in range(q_upto(t - 1), q_upto(t))]
                 if V_ORDER == "tqqt":
                     mul_eh(t + 1, 0)
                 for s, j in qs[:-2]:
                     quant(s, j)
-                if V_ORDER == "ttqq":
+                if V_ORDER == "ttqq" and t > 0:
                     mul_eh(t + 1, 0)
                     mul_eh(t + 1, 1)
                 if t >= Q_WIDE and len(qs) == 2:
@@ -564,15 +570,12 @@ def tile_mambacell_pa_kernel(
                     mul_eh(t + 1, 1)
             if t == NSTEP - 2:
                 nc.vector.quantize_mx(out=woc[:].bitcast(FP8X4), scales=wos[:], in_=wog[:])
-            if not last and t <= 2:
-                for rt in range(RT):
-                    mx_bc(t + 1, rt, 0, b_ps, "bps")
             for rt in range(RT):
                 mx_bc(t, rt, 1, c_ps, "cps")
             if t == NSTEP - 1:
                 for ct in range(CT - 1):
                     for rt in range(RT):
-                        silu(ct, rt)
+                        silu(ct, rt, y_f)
 
         last = NSTEP - 1
         v_t4(last, 0)
@@ -584,8 +587,8 @@ def tile_mambacell_pa_kernel(
                 y_acc(s, rt)
         for rt in range(RT):
             y_acc(last, rt)
-            fin_y(CT - 1, rt)
-            silu(CT - 1, rt)
+            fin_y(CT - 1, rt, y_f)
+            silu(CT - 1, rt, y_f)
         for rt in range(RT):
             nc.vector.quantize_mx(
                 out=sc[:, rt * P : (rt + 1) * P].bitcast(FP8X4),

@@ -45,7 +45,7 @@ T4_BUFS = 13
 HN_BUFS = 4
 STORE_AT = (1, 2)
 V_EVAC = ()
-G_T2 = (5, 7, 9, 11, 13, 15)
+G_T2 = (5, 7, 9, 11, 13)
 
 
 def tile_mambacell_pa_kernel(
@@ -449,39 +449,40 @@ def tile_mambacell_pa_kernel(
         quant(0, 1)
         w_tr(1, 0)
         w_tr(1, 1)
-        for half in range(2):
-            v_copy(out=u_t[:, half * 512 : (half + 1) * 512], in_=u_banks[half][:])
+        bank_to_grouped_w(1, 0, v_copy)
         nc.vector.tensor_tensor(out=cols(du_t, 0), in0=cols(u_banks[0], 0), in1=cols(delta_t, 0), op=ALU.mult)
         exps(0)
-        du_turn(0, v_copy)
+        bank_to_grouped_w(1, 1, v_copy)
+        du_turn(0, v_copy, psw, "wps")
         e_trans(0, 0)
         e_trans(0, 1)
-        nc.gpsimd.tensor_tensor(out=du_t[:, B:], in0=u_t[:, B:], in1=delta_t[:, B:], op=ALU.mult)
+        w_tr(1, 2)
+        w_tr(1, 3)
         v_t3(0, 0)
         v_t3(0, 1)
         mul_eh(0, 0)
         add_hn(0, 0)
         mul_eh(0, 1)
         add_hn(0, 1)
+        for lo, hi in ((1, 2), (2, CT)):
+            nc.vector.tensor_tensor(
+                out=du_t[:, lo * B : hi * B],
+                in0=u_banks[lo // 2][:, lo % 2 * B : lo % 2 * B + (hi - lo) * B],
+                in1=delta_t[:, lo * B : hi * B],
+                op=ALU.mult,
+            )
         exps(1)
-        bank_to_grouped_w(1, 0, s_copy)
-        bank_to_grouped_w(1, 1, s_copy)
-        e_trans(1, 0)
-        e_trans(1, 1)
-        w_tr(1, 2)
-        w_tr(1, 3)
-        mul_eh(1, 0)
-        mul_eh(1, 1)
-        bank_to_grouped_w(1, 2, v_copy)
-        bank_to_grouped_w(1, 3, v_copy)
+        bank_to_grouped_w(1, 2, s_copy)
+        bank_to_grouped_w(1, 3, s_copy)
+        for half in range(2):
+            s_copy(out=u_t[:, half * 512 : (half + 1) * 512], in_=u_banks[half][:])
         quant(1, 0)
-        quant(1, 1)
 
         def w_upto(t):
             return min(4 * NSTEP, 8 + W_RATE * (t + 1), 4 * (t + 2 + W_AHEAD))
 
         def q_upto(t):
-            return 4 if t < 0 else min(2 * NSTEP, 2 * (t + 3))
+            return 3 if t < 0 else min(2 * NSTEP, 2 * (t + 3))
 
         for t in range(NSTEP):
             last = t == NSTEP - 1
@@ -501,9 +502,12 @@ def tile_mambacell_pa_kernel(
                     out=wo_sb[:].rearrange("p (t k) -> p t k", t=CT), in_=out_proj_w.rearrange("(t p) k -> p t k", p=P)
                 )
                 nc.sync.dma_start(out=ob[:], in_=out_proj_b.partition_broadcast(P))
+            if last:
+                for rt in range(RT):
+                    mx_bc(t, rt, 1, c_ps, "cps")
             banks = [divmod(i, 4) for i in range(w_upto(t - 1), w_upto(t))]
             for rt in range(RT):
-                if t % NG == Y_AT[rt] and t // NG - 1 >= 0:
+                if t % NG == Y_AT[rt] and NG <= t < NSTEP - 1:
                     ct = t // NG - 1
                     y_open(ct, rt, psy, Y_TAG)
                     for s in range(ct * NG, ct * NG + NG):
@@ -511,7 +515,7 @@ def tile_mambacell_pa_kernel(
             if t % NG == DU_AT and t // NG + 1 < CT:
                 du_turn(t // NG + 1, s_copy)
             def e_part():
-                if 0 < t < NSTEP - 1:
+                if not last:
                     e_trans(t + 1, 0)
                     e_trans(t + 1, 1)
                     if t + 1 in G_T2:
@@ -533,14 +537,24 @@ def tile_mambacell_pa_kernel(
             if t >= NSTEP - 2:
                 for rt in range(RT):
                     y_acc(t - 2, rt)
+            if t == NSTEP - 2:
+                y_open(CT - 2, 1, psy, Y_TAG)
+                for s in range((CT - 2) * NG, (CT - 1) * NG):
+                    y_acc(s, 1)
             if t == NSTEP - 3:
                 wog = stg.tile([P, 4 * D], BF16, name="wog", tag="g512", align_bytes=64)
                 prep_wo(0, wo_sb, wog)
                 prep_wo(1, wo_sb, wog)
-            if t > 0:
+            if 0 < t < NSTEP - 1:
                 for rt in range(RT):
                     v_t3(t, rt)
                     add_hn(t, rt)
+            if t == NSTEP - 2:
+                for rt in range(RT):
+                    mul_eh(t + 1, rt)
+                for rt in range(RT):
+                    v_t3(t + 1, rt)
+                    add_hn(t + 1, rt)
             if last:
                 for rt in range(RT):
                     store_h(CT - 1, rt)
@@ -558,7 +572,7 @@ def tile_mambacell_pa_kernel(
                     mul_eh(t + 1, 0)
                 for s, j in qs[:-2]:
                     quant(s, j)
-                if V_ORDER == "ttqq" and t > 0:
+                if V_ORDER == "ttqq" and t < NSTEP - 2:
                     mul_eh(t + 1, 0)
                     mul_eh(t + 1, 1)
                 if t >= Q_WIDE and len(qs) == 2:
@@ -568,16 +582,16 @@ def tile_mambacell_pa_kernel(
                         quant(s, j)
                 if V_ORDER == "tqqt":
                     mul_eh(t + 1, 1)
-            if t == NSTEP - 2:
-                nc.vector.quantize_mx(out=woc[:].bitcast(FP8X4), scales=wos[:], in_=wog[:])
-            for rt in range(RT):
-                mx_bc(t, rt, 1, c_ps, "cps")
+            if not last:
+                for rt in range(RT):
+                    mx_bc(t, rt, 1, c_ps, "cps")
             if t == NSTEP - 1:
                 for ct in range(CT - 1):
                     for rt in range(RT):
                         silu(ct, rt, y_f)
 
         last = NSTEP - 1
+        nc.vector.quantize_mx(out=woc[:].bitcast(FP8X4), scales=wos[:], in_=wog[:])
         v_t4(last, 0)
         v_t4(last, 1)
         sc = const.tile([P, B], U32, name="sc", align_bytes=64)

@@ -35,7 +35,7 @@ W_RATE = 5
 W_AHEAD = 2
 Q_AHEAD = 1
 Y_TAG = "e"
-EXP_POS = 5
+EXP_POS = 2
 ET_POS = 2
 V_ORDER = "ttqq"
 Q_WIDE = 1

@@ -20,32 +20,16 @@ CT = D // P
 NG = 4
 NN = S // NG
 NSTEP = CT * NG
+BANK = 512
 
 FLOPS = 2 * B * D * (3 * D + 2 * D * S)
 
-W_BUFS = 2
-E_BUFS = 2
-BC_BUFS = 4
-WC_BUFS = 4
-WST_BUFS = 4
+WEIGHT_BUFS = 4
+Y_STEP = (1, 3)
+STORE_STEP = (1, 2)
+TURN_DU_STEP = 2
 H_EARLY = 5
-Y_AT = (1, 3)
-DU_AT = 2
-W_RATE = 5
-W_AHEAD = 2
-Q_AHEAD = 1
-Y_TAG = "e"
-EXP_POS = 2
-ET_POS = 2
-V_ORDER = "ttqq"
-Q_WIDE = 1
-MB_POS = 4
-QA = (4, 5, 2)
-T4_BUFS = 13
-HN_BUFS = 4
-STORE_AT = (1, 2)
-V_EVAC = ()
-G_T2 = (5, 7, 9, 11, 13)
+GPSIMD_STEPS = range(5, NSTEP - 2, 2)
 
 
 def tile_mambacell_pa_kernel(
@@ -55,67 +39,70 @@ def tile_mambacell_pa_kernel(
     with ExitStack() as ctx:
         ctx.enter_context(tc.manual_schedule())
         const = ctx.enter_context(tc.tile_pool(name="const", bufs=1))
-        stg = ctx.enter_context(tc.tile_pool(name="stg", bufs=1))
-        wstp = ctx.enter_context(tc.tile_pool(name="wstp", bufs=WST_BUFS))
-        wgp = ctx.enter_context(tc.tile_pool(name="wgp", bufs=2))
-        wcp = ctx.enter_context(tc.tile_pool(name="wcp", bufs=WC_BUFS))
-        hp = ctx.enter_context(tc.tile_pool(name="hp", bufs=4))
-        ep = ctx.enter_context(tc.tile_pool(name="ep", bufs=3))
-        tp = ctx.enter_context(tc.tile_pool(name="tp", bufs=3))
-        hnp = ctx.enter_context(tc.tile_pool(name="hnp", bufs=HN_BUFS))
-        psw = ctx.enter_context(tc.psum_pool(name="psw", bufs=W_BUFS))
-        pse = ctx.enter_context(tc.psum_pool(name="pse", bufs=E_BUFS))
-        psb = ctx.enter_context(tc.psum_pool(name="psb", bufs=BC_BUFS))
-        psy = ctx.enter_context(tc.psum_pool(name="psy", bufs=1)) if Y_TAG == "y" else pse
+        stage = ctx.enter_context(tc.tile_pool(name="stage", bufs=1))
+        raw_pool = ctx.enter_context(tc.tile_pool(name="raw_pool", bufs=WEIGHT_BUFS))
+        group_pool = ctx.enter_context(tc.tile_pool(name="group_pool", bufs=2))
+        code_pool = ctx.enter_context(tc.tile_pool(name="code_pool", bufs=4))
+        h_pool = ctx.enter_context(tc.tile_pool(name="h_pool", bufs=4))
+        exp_pool = ctx.enter_context(tc.tile_pool(name="exp_pool", bufs=3))
+        prod_pool = ctx.enter_context(tc.tile_pool(name="prod_pool", bufs=3))
+        hn_pool = ctx.enter_context(tc.tile_pool(name="hn_pool", bufs=4))
+        ps_weights = ctx.enter_context(tc.psum_pool(name="ps_weights", bufs=2))
+        ps_turned = ctx.enter_context(tc.psum_pool(name="ps_turned", bufs=2))
+        ps_mx = ctx.enter_context(tc.psum_pool(name="ps_mx", bufs=4))
+        WEIGHTS = (ps_weights, "weights")
+        TURNED = (ps_turned, "turned")
 
-        one = stg.tile([P, 1], F32, name="one")
+        v_copy = nc.vector.tensor_copy
+        s_copy = nc.scalar.copy
+
+        def mx_tiles(nm, groups):
+            codes = const.tile([P, groups], U32, name="codes_" + nm, align_bytes=64)
+            scales = const.tile([P, groups], U8, name="scales_" + nm, align_bytes=64)
+            return codes, scales
+
+        one = stage.tile([P, 1], F32, name="one")
         nc.vector.memset(one[:], 1.0)
-        vrows = stg.tile([P, P], BF16, name="vrows")
-        nc.vector.memset(vrows[:], 0.0)
-        a_sb = stg.tile([P, CT * S], BF16, name="a_sb")
-        ob = const.tile([P, D], BF16, name="ob")
+        vec_rows = stage.tile([P, P], BF16, name="vec_rows")
+        nc.vector.memset(vec_rows[:], 0.0)
+        a_sb = stage.tile([P, CT * S], BF16, name="a_sb")
+        out_bias = const.tile([P, D], BF16, name="out_bias")
         nc.scalar.activation(out=one[:], in_=one[:], func=ACT.Exp)
         ident_b = const.tile([P, P], BF16, name="ident_b")
         make_identity(nc, ident_b[:])
         ident_f = const.tile([P, P], F32, name="ident_f")
         make_identity(nc, ident_f[:])
 
-        x_sb = stg.tile([P, RT * D], BF16, name="x_sb")
+        x_sb = stage.tile([P, RT * D], BF16, name="x_sb")
         nc.sync.dma_start(
             out=x_sb[:].rearrange("p (t k) -> p t k", t=RT), in_=x.rearrange("(t p) k -> p t k", p=P)
         )
 
-        wview = bc_proj_w.rearrange("(t p j g n) k -> t g p j n k", p=P, j=2, g=NG, n=NN)
-        hview = h.rearrange("b c n -> b (c n)")
-        hnview = h_new.rearrange("b c n -> b (c n)")
-        wst = {}
-        w_ps = {}
-        wg = {}
-        wc = {}
-        ws = {}
+        weight_view = bc_proj_w.rearrange("(t p j g n) k -> t g p j n k", p=P, j=2, g=NG, n=NN)
+        h_view = h.rearrange("b c n -> b (c n)")
+        h_new_view = h_new.rearrange("b c n -> b (c n)")
+
+        raw = {}
+        w_bank = {}
+        grouped_w = {}
+        w_codes = {}
+        w_scales = {}
         h_sb = {}
-        e_t = {}
-        e_ps = {}
-        e_sb = {}
+        exp_t = {}
+        exp_ps = {}
+        exp_sb = {}
         b_ps = {}
         c_ps = {}
-        t2 = {}
-        t3 = {}
-        t4 = {}
+        eh = {}
+        bu = {}
+        ch = {}
         hn = {}
         y_ps = {}
 
         def load_w(s):
-            wst[s] = wstp.tile([P, 2 * NN * D], BF16, name="wst%d" % s, tag="wst")
+            raw[s] = raw_pool.tile([P, 2 * NN * D], BF16, name="raw%d" % s, tag="raw")
             nc.sync.dma_start(
-                out=wst[s][:].rearrange("p (j n k) -> p j n k", j=2, n=NN), in_=wview[s // NG, s % NG]
-            )
-
-        def load_w_half(s, j):
-            if j == 0:
-                wst[s] = wstp.tile([P, 2 * NN * D], BF16, name="wst%d" % s, tag="wst")
-            nc.sync.dma_start(
-                out=wst[s][:].rearrange("p (j n k) -> p j n k", j=2, n=NN)[:, j], in_=wview[s // NG, s % NG][:, j]
+                out=raw[s][:].rearrange("p (j n k) -> p j n k", j=2, n=NN), in_=weight_view[s // NG, s % NG]
             )
 
         def load_rows(dst, w, half):
@@ -124,174 +111,188 @@ def tile_mambacell_pa_kernel(
                 in_=w.rearrange("(t p) k -> p t k", p=P)[:, 2 * half : 2 * half + 2],
             )
 
-        def load_h(ct, rts=range(RT)):
-            for rt in rts:
-                h_sb[(ct, rt)] = hp.tile([P, P * S], BF16, name="h%d_%d" % (ct, rt), tag="h")
-                nc.sync.dma_start(
-                    out=h_sb[(ct, rt)][:], in_=hview[rt * P : (rt + 1) * P, ct * P * S : (ct + 1) * P * S]
-                )
+        def load_h(ct, rt):
+            h_sb[(ct, rt)] = h_pool.tile([P, P * S], BF16, name="h%d_%d" % (ct, rt), tag="h")
+            nc.sync.dma_start(
+                out=h_sb[(ct, rt)][:], in_=h_view[rt * P : (rt + 1) * P, ct * P * S : (ct + 1) * P * S]
+            )
 
         def store_h(ct, rt):
-            nc.sync.dma_start(out=hnview[rt * P : (rt + 1) * P, ct * P * S : (ct + 1) * P * S], in_=hn[(ct, rt)][:])
+            nc.sync.dma_start(
+                out=h_new_view[rt * P : (rt + 1) * P, ct * P * S : (ct + 1) * P * S], in_=hn[(ct, rt)][:]
+            )
 
-        dtw_sb = stg.tile([P, CT * D], BF16, name="dtw_sb", tag="w512")
-        inw_sb = stg.tile([P, CT * D], BF16, name="inw_sb")
-        load_rows(dtw_sb, dt_proj_w, 0)
-        load_rows(dtw_sb, dt_proj_w, 1)
-        nc.sync.dma_start(out=vrows[0:CT, :], in_=dt_proj_b.rearrange("(t c) -> t c", c=P))
-        nc.sync.dma_start(out=vrows[CT : 2 * CT, :], in_=d_param.rearrange("(t c) -> t c", c=P))
-        load_rows(inw_sb, in_proj_w, 0)
-        load_rows(inw_sb, in_proj_w, 1)
+        dt_sb = stage.tile([P, CT * D], BF16, name="dt_sb", tag="rows512")
+        in_sb = stage.tile([P, CT * D], BF16, name="in_sb")
+        for half in range(2):
+            load_rows(dt_sb, dt_proj_w, half)
+        nc.sync.dma_start(out=vec_rows[0:CT, :], in_=dt_proj_b.rearrange("(t c) -> t c", c=P))
+        nc.sync.dma_start(out=vec_rows[CT : 2 * CT, :], in_=d_param.rearrange("(t c) -> t c", c=P))
+        for half in range(2):
+            load_rows(in_sb, in_proj_w, half)
         load_w(0)
         nc.sync.dma_start(out=a_sb[:].rearrange("p (t n) -> p t n", t=CT), in_=a_log.rearrange("(t p) n -> p t n", p=P))
         load_w(1)
-        load_h(0)
+        for rt in range(RT):
+            load_h(0, rt)
         load_w(2)
         load_w(3)
-        load_h(1)
+        for rt in range(RT):
+            load_h(1, rt)
 
-        def words_to_bank(src_words, first_col, name, pool=psw, tag="wps"):
-            ps = pool.tile([P, 512], F32, name=name, tag=tag)
+        def turn_words(words, first, name, pool, tag):
+            ps = pool.tile([P, BANK], F32, name=name, tag=tag)
             for j in range(2):
                 for u in range(2):
-                    col = first_col + j * 256 + u * P
-                    nc.tensor.transpose(ps[:, (j * 2 + u) * P : (j * 2 + u + 1) * P], src_words[:, col : col + P], ident_f[:])
+                    col = first + j * 256 + u * P
+                    nc.tensor.transpose(ps[:, (j * 2 + u) * P : (j * 2 + u + 1) * P], words[:, col : col + P], ident_f[:])
             return ps
 
-        def bank_to_grouped(eng_copy, ps, dst_words):
-            eng_copy(
-                out=dst_words.rearrange("p (j c u) -> p j c u", j=2, u=2),
+        def group_words(copy, ps, dst):
+            copy(
+                out=dst.rearrange("p (j c u) -> p j c u", j=2, u=2),
                 in_=ps[:].rearrange("p (j u c) -> p j c u", j=2, u=2),
             )
 
-        v_copy = nc.vector.tensor_copy
-        s_copy = nc.scalar.copy
+        def turn_w(s, b):
+            w_bank[(s, b)] = turn_words(raw[s][:].bitcast(F32), b * BANK, "w%d_%d" % (s, b), *WEIGHTS)
 
-        def w_tr(s, b):
-            w_ps[(s, b)] = words_to_bank(wst[s][:].bitcast(F32), b * 512, "wps%d_%d" % (s, b))
-
-        def w_ev(s, b):
-            bank_to_grouped_w(s, b, v_copy if (s, b) in V_EVAC else s_copy)
-
-        def bank_to_grouped_w(s, b, eng_copy):
+        def group_w(s, b, copy):
             if b == 0:
-                wg[s] = wgp.tile([P, 4 * 2 * NN * P], BF16, name="wg%d" % s, tag="wg", align_bytes=64)
-            bank_to_grouped(eng_copy, w_ps[(s, b)], wg[s][:].bitcast(F32)[:, b * 512 : (b + 1) * 512])
+                grouped_w[s] = group_pool.tile([P, 4 * 2 * NN * P], BF16, name="group%d" % s, tag="group", align_bytes=64)
+            group_words(copy, w_bank[(s, b)], grouped_w[s][:].bitcast(F32)[:, b * BANK : (b + 1) * BANK])
 
-        def w_bank(s, b):
-            w_tr(s, b)
-            w_ev(s, b)
-
-        def quant(s, j, n=1):
-            if j == 0:
-                wc[s] = wcp.tile([P, 2 * NN * P], U32, name="wc%d" % s, tag="wc", align_bytes=64)
-                ws[s] = wcp.tile([P, 2 * NN * P], U8, name="ws%d" % s, tag="ws", align_bytes=64)
+        def quantise_w(s, first, count):
+            if first == 0:
+                w_codes[s] = code_pool.tile([P, 2 * NN * P], U32, name="w_codes%d" % s, tag="w_codes", align_bytes=64)
+                w_scales[s] = code_pool.tile([P, 2 * NN * P], U8, name="w_scales%d" % s, tag="w_scales", align_bytes=64)
+            lo = first * NN * P
+            hi = (first + count) * NN * P
             nc.vector.quantize_mx(
-                out=wc[s][:, j * 512 : (j + n) * 512].bitcast(FP8X4),
-                scales=ws[s][:, j * 512 : (j + n) * 512],
-                in_=wg[s][:, j * 2048 : (j + n) * 2048],
+                out=w_codes[s][:, lo:hi].bitcast(FP8X4), scales=w_scales[s][:, lo:hi], in_=grouped_w[s][:, 4 * lo : 4 * hi]
             )
 
         def cols(t, ct):
             return t[:, ct * B : (ct + 1) * B]
 
-        def exps(s):
+        def exponential(s, i):
             ct = s // NG
-            g = s % NG
-            e_t[s] = ep.tile([P, NN * B], F32, name="et%d" % s, tag="et")
-            for i in range(NN):
-                n = g * NN + i
-                nc.scalar.activation(
-                    out=e_t[s][:, i * B : (i + 1) * B],
-                    in_=cols(delta_t, ct),
-                    func=ACT.Exp,
-                    scale=neg_a[:, ct * S + n : ct * S + n + 1],
-                )
-
-        def e_trans(s, rt):
-            e_ps[(s, rt)] = pse.tile([P, 512], F32, name="eps%d_%d" % (s, rt), tag="e")
-            for i in range(NN):
-                nc.tensor.transpose(
-                    e_ps[(s, rt)][:, i * P : (i + 1) * P], e_t[s][:, i * B + rt * P : i * B + (rt + 1) * P], ident_f[:]
-                )
-
-        def mx_bc(s, rt, j, store, nm):
-            store[(s, rt)] = psb.tile([P, 512], F32, name="%s%d_%d" % (nm, s, rt), tag="bc")
-            nc.tensor.matmul_mx(
-                out=store[(s, rt)][:],
-                lhsT=xc[:, rt * P : (rt + 1) * P].bitcast(FP8X4),
-                lhsT_scale=xs[:, rt * P : (rt + 1) * P],
-                rhs=wc[s][:, j * 512 : (j + 1) * 512].bitcast(FP8X4),
-                rhs_scale=ws[s][:, j * 512 : (j + 1) * 512],
-                start=True,
-                stop=True,
+            n = s % NG * NN + i
+            if i == 0:
+                exp_t[s] = exp_pool.tile([P, NN * B], F32, name="exp%d" % s, tag="exp")
+            nc.scalar.activation(
+                out=exp_t[s][:, i * B : (i + 1) * B],
+                in_=cols(delta_t, ct),
+                func=ACT.Exp,
+                scale=neg_a[:, ct * S + n : ct * S + n + 1],
             )
 
-        def by_channel(ps):
-            return ps[:].rearrange("p (n c) -> p c n", n=NN)
+        def turn_exp(s, rt):
+            exp_ps[(s, rt)] = ps_turned.tile([P, BANK], F32, name="exp_ps%d_%d" % (s, rt), tag="turned")
+            for i in range(NN):
+                nc.tensor.transpose(
+                    exp_ps[(s, rt)][:, i * P : (i + 1) * P], exp_t[s][:, i * B + rt * P : i * B + (rt + 1) * P], ident_f[:]
+                )
+
+        def multiply_w(s, j, store, nm):
+            for rt in range(RT):
+                store[(s, rt)] = ps_mx.tile([P, BANK], F32, name="%s%d_%d" % (nm, s, rt), tag="mx")
+                nc.tensor.matmul_mx(
+                    out=store[(s, rt)][:],
+                    lhsT=x_codes[:, rt * P : (rt + 1) * P].bitcast(FP8X4),
+                    lhsT_scale=x_scales[:, rt * P : (rt + 1) * P],
+                    rhs=w_codes[s][:, j * NN * P : (j + 1) * NN * P].bitcast(FP8X4),
+                    rhs_scale=w_scales[s][:, j * NN * P : (j + 1) * NN * P],
+                    start=True,
+                    stop=True,
+                )
+
+        def multiply_b(s):
+            multiply_w(s, 0, b_ps, "b")
+
+        def multiply_c(s):
+            multiply_w(s, 1, c_ps, "c")
+
+        def by_channel(t):
+            return t[:].rearrange("p (n c) -> p c n", n=NN)
 
         def compact(t):
             return t[:].rearrange("p (c n) -> p c n", n=NN)
 
-        def natural(t, g):
+        def group_of(t, s):
+            g = s % NG
             return t[:].rearrange("p (c n) -> p c n", n=S)[:, :, g * NN : (g + 1) * NN]
 
-        def e_out(s, rt):
-            e_sb[(s, rt)] = tp.tile([P, 512], F32, name="esb_%d_%d" % (s, rt), tag="esb", bufs=2)
-            nc.scalar.copy(out=compact(e_sb[(s, rt)]), in_=by_channel(e_ps[(s, rt)]))
+        def copy_exp(s):
+            exp_sb[s] = prod_pool.tile([P, BANK], F32, name="exp_sb%d" % s, tag="exp_sb", bufs=2)
+            nc.scalar.copy(out=compact(exp_sb[s]), in_=by_channel(exp_ps[(s, 1)]))
 
-        def mul_eh(s, rt):
-            t2[(s, rt)] = tp.tile([P, 512], F32, name="t2_%d_%d" % (s, rt), tag="t2", bufs=4)
-            hh = natural(h_sb[(s // NG, rt)], s % NG)
-            if rt == 1 and s in G_T2:
-                nc.gpsimd.tensor_tensor(out=compact(t2[(s, rt)]), in0=compact(e_sb[(s, rt)]), in1=hh, op=ALU.mult)
+        def product_eh(s, rt):
+            eh[(s, rt)] = prod_pool.tile([P, BANK], F32, name="eh%d_%d" % (s, rt), tag="eh", bufs=4)
+            here = group_of(h_sb[(s // NG, rt)], s)
+            if rt == 1 and s in GPSIMD_STEPS:
+                nc.gpsimd.tensor_tensor(out=compact(eh[(s, rt)]), in0=compact(exp_sb[s]), in1=here, op=ALU.mult)
             else:
-                nc.vector.tensor_tensor(out=compact(t2[(s, rt)]), in0=by_channel(e_ps[(s, rt)]), in1=hh, op=ALU.mult)
+                nc.vector.tensor_tensor(out=compact(eh[(s, rt)]), in0=by_channel(exp_ps[(s, rt)]), in1=here, op=ALU.mult)
 
-        def v_t3(s, rt):
+        def product_bu(s, rt):
             lo = (s // NG * RT + rt) * P
-            t3[(s, rt)] = tp.tile([P, 512], F32, name="t3_%d_%d" % (s, rt), tag="t3")
+            bu[(s, rt)] = prod_pool.tile([P, BANK], F32, name="bu%d_%d" % (s, rt), tag="bu")
             nc.vector.tensor_tensor(
-                out=compact(t3[(s, rt)]),
+                out=compact(bu[(s, rt)]),
                 in0=by_channel(b_ps[(s, rt)]),
                 in1=du[:, lo : lo + P].unsqueeze(2).to_broadcast([P, P, NN]),
                 op=ALU.mult,
             )
 
-        def add_hn(s, rt):
+        def add_h_new(s, rt):
+            ct = s // NG
+            if s % NG == 0:
+                hn[(ct, rt)] = hn_pool.tile([P, P * S], F32, name="hn%d_%d" % (ct, rt), tag="hn")
+            nc.gpsimd.tensor_tensor(
+                out=group_of(hn[(ct, rt)], s), in0=compact(eh[(s, rt)]), in1=compact(bu[(s, rt)]), op=ALU.add
+            )
+
+        def product_ch(s, rt):
+            ch[(s, rt)] = prod_pool.tile([P, BANK], F32, name="ch%d_%d" % (s, rt), tag="ch", bufs=13)
+            nc.vector.tensor_tensor(
+                out=by_channel(ch[(s, rt)]), in0=by_channel(c_ps[(s, rt)]), in1=group_of(hn[(s // NG, rt)], s), op=ALU.mult
+            )
+
+        def open_y(ct, rt, pool, tag):
+            y_ps[(ct, rt)] = pool.tile([P, BANK], F32, name="y%d_%d" % (ct, rt), tag=tag)
+
+        def sum_y(s, rt):
             ct = s // NG
             g = s % NG
-            if g == 0:
-                hn[(ct, rt)] = hnp.tile([P, P * S], F32, name="hn%d_%d" % (ct, rt), tag="hn")
-            nc.gpsimd.tensor_tensor(
-                out=natural(hn[(ct, rt)], g), in0=compact(t2[(s, rt)]), in1=compact(t3[(s, rt)]), op=ALU.add
-            )
-
-        def v_t4(s, rt):
-            t4[(s, rt)] = tp.tile([P, 512], F32, name="t4_%d_%d" % (s, rt), tag="t4", bufs=T4_BUFS)
-            nc.vector.tensor_tensor(
-                out=by_channel(t4[(s, rt)]), in0=by_channel(c_ps[(s, rt)]), in1=natural(hn[(s // NG, rt)], s % NG), op=ALU.mult
-            )
-
-        def y_acc(s, rt):
-            g = s % NG
+            tail = ct == CT - 1
+            if tail and g == 0:
+                nc.tensor.matmul(
+                    out=y_ps[(ct, rt)][:, 0:P],
+                    lhsT=d_diag[:],
+                    rhs=u_t[:, ct * B + rt * P : ct * B + (rt + 1) * P],
+                    start=True,
+                    stop=False,
+                )
             for i in range(NN):
                 nc.tensor.matmul(
-                    out=y_ps[(s // NG, rt)][:, 0:P],
-                    lhsT=t4[(s, rt)][:, i * P : (i + 1) * P],
+                    out=y_ps[(ct, rt)][:, 0:P],
+                    lhsT=ch[(s, rt)][:, i * P : (i + 1) * P],
                     rhs=ident_f[:],
                     is_transpose=True,
-                    start=(g == 0 and i == 0),
+                    start=(g == 0 and i == 0 and not tail),
                     stop=(g == NG - 1 and i == NN - 1),
                 )
 
-        def y_open(ct, rt, pool, tag):
-            y_ps[(ct, rt)] = pool.tile([P, 512], F32, name="y%d_%d" % (ct, rt), tag=tag)
+        def sum_tile(ct, rt):
+            open_y(ct, rt, *TURNED)
+            for s in range(ct * NG, (ct + 1) * NG):
+                sum_y(s, rt)
 
-        def fin_y(ct, rt, y_f):
+        def finish_y(ct, rt):
             lo = ct * B + rt * P
             nc.vector.scalar_tensor_tensor(
-                out=y_f[:, lo : lo + P],
+                out=y_sb[:, lo : lo + P],
                 in0=u_t[:, lo : lo + P],
                 scalar=vec[:, CT + ct : CT + ct + 1],
                 in1=y_ps[(ct, rt)][:, 0:P],
@@ -299,329 +300,280 @@ def tile_mambacell_pa_kernel(
                 op1=ALU.add,
             )
 
-        def silu(ct, rt, y_f):
+        def silu(ct, rt):
             lo = ct * B + rt * P
             nc.scalar.activation(
-                out=sg[:].rearrange("p (r t) -> p r t", t=CT)[:, rt * P : (rt + 1) * P, ct], in_=y_f[:, lo : lo + P], func=ACT.Silu
+                out=silu_y[:].rearrange("p (r t) -> p r t", t=CT)[:, rt * P : (rt + 1) * P, ct],
+                in_=y_sb[:, lo : lo + P] if ct < CT - 1 else y_ps[(ct, rt)][:, 0:P],
+                func=ACT.Silu,
             )
 
-        sg = const.tile([P, CT * B], BF16, name="sg", align_bytes=64)
-        woc = const.tile([P, D], U32, name="woc", align_bytes=64)
-        wos = const.tile([P, D], U8, name="wos", align_bytes=64)
+        silu_y = const.tile([P, CT * B], BF16, name="silu_y", align_bytes=64)
+        out_codes, out_scales = mx_tiles("out", D)
 
-        def prep_wo(half, wo_sb, wog):
-            ps = psw.tile([P, 1024], BF16, name="wops%d" % half, tag="wps")
+        def turn_out_w(half):
+            ps = ps_weights.tile([P, 2 * BANK], BF16, name="out_ps%d" % half, tag="weights")
             for a in range(2):
-                ot = half * 2 + a
+                row = (half * 2 + a) * D
                 for t in range(CT):
                     nc.tensor.transpose(
-                        ps[:, (a * CT + t) * P : (a * CT + t + 1) * P], wo_sb[:, ot * D + t * P : ot * D + (t + 1) * P], ident_b[:]
+                        ps[:, (a * CT + t) * P : (a * CT + t + 1) * P], out_sb[:, row + t * P : row + (t + 1) * P], ident_b[:]
                     )
             nc.scalar.copy(
-                out=wog[:, half * 1024 : (half + 1) * 1024].rearrange("p (a o t) -> p a o t", a=2, t=CT),
+                out=grouped_out[:, half * 1024 : (half + 1) * 1024].rearrange("p (a o t) -> p a o t", a=2, t=CT),
                 in_=ps[:].rearrange("p (a t o) -> p a o t", a=2, t=CT),
             )
 
-        xg = stg.tile([P, 4 * B], BF16, name="xg", align_bytes=64)
-        xc = const.tile([P, B], U32, name="xc", align_bytes=64)
-        xs = const.tile([P, B], U8, name="xs", align_bytes=64)
+        grouped_x = stage.tile([P, 4 * B], BF16, name="grouped_x", align_bytes=64)
+        x_codes, x_scales = mx_tiles("x", B)
+        grouped_dt = stage.tile([P, 4 * D], BF16, name="grouped_dt", tag="grouped512", align_bytes=64)
+        dt_codes, dt_scales = mx_tiles("dt", D)
+        grouped_in = stage.tile([P, 4 * D], BF16, name="grouped_in", align_bytes=64)
+        in_codes, in_scales = mx_tiles("in", D)
 
-        def tiles_512(nm, tag):
-            grouped = stg.tile([P, 4 * D], BF16, name="g_" + nm, tag=tag, align_bytes=64)
-            codes = const.tile([P, D], U32, name="c_" + nm, align_bytes=64)
-            scales = const.tile([P, D], U8, name="s_" + nm, align_bytes=64)
-            return grouped, codes, scales
+        def prepare(w_sb, half, grouped, nm, copy, pool, tag):
+            ps = turn_words(w_sb[:].bitcast(F32), half * BANK, "%s_ps%d" % (nm, half), pool, tag)
+            group_words(copy, ps, grouped[:].bitcast(F32)[:, half * BANK : (half + 1) * BANK])
 
-        def prep_half(w_sb, half, grouped, nm, eng, pool=psw, tag="wps"):
-            ps = words_to_bank(w_sb[:].bitcast(F32), half * 512, "ps_%s%d" % (nm, half), pool, tag)
-            bank_to_grouped(eng, ps, grouped[:].bitcast(F32)[:, half * 512 : (half + 1) * 512])
+        def quantise(codes, scales, grouped):
+            nc.vector.quantize_mx(out=codes[:].bitcast(FP8X4), scales=scales[:], in_=grouped[:])
 
-        def quant_half(grouped, codes, scales, half):
-            nc.vector.quantize_mx(
-                out=codes[:, half * 256 : (half + 1) * 256].bitcast(FP8X4),
-                scales=scales[:, half * 256 : (half + 1) * 256],
-                in_=grouped[:, half * 1024 : (half + 1) * 1024],
-            )
+        def project(codes, scales, banks):
+            for ct in range(CT):
+                nc.tensor.matmul_mx(
+                    out=cols(banks[ct // 2], ct % 2),
+                    lhsT=codes[:, ct * P : (ct + 1) * P].bitcast(FP8X4),
+                    lhsT_scale=scales[:, ct * P : (ct + 1) * P],
+                    rhs=x_codes[:].bitcast(FP8X4),
+                    rhs_scale=x_scales[:],
+                    start=True,
+                    stop=True,
+                )
 
-        dtg, dtc, dts = tiles_512("dt", "g512")
-        ing, inc, ins = tiles_512("in", "g_in")
-
-        def proj_t(ct, codes, scales, ps):
-            j = ct % 2
-            nc.tensor.matmul_mx(
-                out=ps[:, j * B : (j + 1) * B],
-                lhsT=codes[:, ct * P : (ct + 1) * P].bitcast(FP8X4),
-                lhsT_scale=scales[:, ct * P : (ct + 1) * P],
-                rhs=xc[:].bitcast(FP8X4),
-                rhs_scale=xs[:],
-                start=True,
-                stop=True,
-            )
-
-        sp = stg.tile([P, CT * B], F32, name="sp", tag="sp")
-        sp_max = stg.tile([P, CT * B], F32, name="sp_max")
+        soft = stage.tile([P, CT * B], F32, name="soft", tag="soft")
+        soft_max = stage.tile([P, CT * B], F32, name="soft_max")
         delta_t = const.tile([P, CT * B], F32, name="delta_t")
         u_t = const.tile([P, CT * B], F32, name="u_t")
-        du_t = stg.tile([P, CT * B], F32, name="du_t")
+        du_t = stage.tile([P, CT * B], F32, name="du_t")
         du = const.tile([P, CT * B], F32, name="du")
-        a_exp = stg.tile([P, CT * S], F32, name="a_exp")
+        a_exp = stage.tile([P, CT * S], F32, name="a_exp")
         neg_a = const.tile([P, CT * S], F32, name="neg_a")
         vec = const.tile([P, 2 * CT], F32, name="vec")
+        d_diag = const.tile([P, P], F32, name="d_diag")
 
-        def sp_abs(ct):
-            nc.scalar.activation(
-                out=cols(sp, ct), in_=cols(d_banks[ct // 2], ct % 2), func=ACT.Abs, bias=vec[:, ct : ct + 1], scale=1.0
+        def multiply_du(lo, hi):
+            first = lo % 2 * B
+            nc.vector.tensor_tensor(
+                out=du_t[:, lo * B : hi * B],
+                in0=u_banks[lo // 2][:, first : first + (hi - lo) * B],
+                in1=delta_t[:, lo * B : hi * B],
+                op=ALU.mult,
             )
 
-        def sp_relu(ct):
+        def turn_du(ct, copy, pool, tag):
+            ps = pool.tile([P, BANK], F32, name="du_ps%d" % ct, tag=tag)
+            for rt in range(RT):
+                nc.tensor.transpose(ps[:, rt * P : (rt + 1) * P], du_t[:, ct * B + rt * P : ct * B + (rt + 1) * P], ident_f[:])
+            copy(out=cols(du, ct), in_=ps[:, 0:B])
+
+        d_banks = [ps_mx.tile([P, BANK], F32, name="dt_out%d" % half, tag="mx") for half in range(2)]
+        u_banks = [ps_mx.tile([P, BANK], F32, name="in_out%d" % half, tag="mx") for half in range(2)]
+
+        group_words(s_copy, turn_words(x_sb[:].bitcast(F32), 0, "x_ps", *WEIGHTS), grouped_x[:].bitcast(F32))
+        prepare(dt_sb, 0, grouped_dt, "dt", s_copy, *WEIGHTS)
+        quantise(x_codes, x_scales, grouped_x)
+        prepare(dt_sb, 1, grouped_dt, "dt", s_copy, *TURNED)
+        vec_ps = ps_turned.tile([P, 2 * BANK], BF16, name="vec_ps", tag="turned")
+        nc.tensor.transpose(vec_ps[:, 0:P], vec_rows[:], ident_b[:])
+        nc.scalar.copy(out=vec[:], in_=vec_ps[:, 0 : 2 * CT])
+        quantise(dt_codes, dt_scales, grouped_dt)
+        for half in range(2):
+            prepare(in_sb, half, grouped_in, "in", v_copy, *WEIGHTS)
+        project(dt_codes, dt_scales, d_banks)
+        for ct in range(CT):
+            nc.scalar.activation(
+                out=cols(soft, ct), in_=cols(d_banks[ct // 2], ct % 2), func=ACT.Abs, bias=vec[:, ct : ct + 1], scale=1.0
+            )
+        for ct in range(CT):
             nc.vector.tensor_scalar(
-                out=cols(sp_max, ct),
+                out=cols(soft_max, ct),
                 in0=cols(d_banks[ct // 2], ct % 2),
                 scalar1=vec[:, ct : ct + 1],
                 scalar2=0.0,
                 op0=ALU.add,
                 op1=ALU.max,
             )
-
-        def sp_log(lo, hi):
-            part = sp[:, lo * B : hi * B]
-            nc.scalar.activation(out=part, in_=part, func=ACT.Exp, scale=-1.0)
-            nc.scalar.activation(out=part, in_=part, func=ACT.Ln, bias=1.0, scale=1.0)
-
-        def sp_sum(lo, hi):
-            part = slice(lo * B, hi * B)
-            nc.gpsimd.tensor_tensor(out=delta_t[:, part], in0=sp_max[:, part], in1=sp[:, part], op=ALU.add)
-
-        def du_turn(ct, eng_copy, pool=psy, tag=Y_TAG):
-            dps = pool.tile([P, 512], F32, name="dups%d" % ct, tag=tag)
-            for rt in range(RT):
-                nc.tensor.transpose(dps[:, rt * P : (rt + 1) * P], du_t[:, ct * B + rt * P : ct * B + (rt + 1) * P], ident_f[:])
-            eng_copy(out=cols(du, ct), in_=dps[:, 0:B])
-
-        d_banks = {}
-        u_banks = {}
-
-        for half in range(2):
-            d_banks[half] = psb.tile([P, 512], F32, name="pj_dt%d" % half, tag="bc")
-        for half in range(2):
-            u_banks[half] = psb.tile([P, 512], F32, name="pj_in%d" % half, tag="bc")
-
-        def v_bank(s, b):
-            w_tr(s, b)
-            bank_to_grouped_w(s, b, v_copy)
-
-        xp = words_to_bank(x_sb[:].bitcast(F32), 0, "xp")
-        bank_to_grouped(s_copy, xp, xg[:].bitcast(F32))
-        prep_half(dtw_sb, 0, dtg, "dt", s_copy)
-        nc.vector.quantize_mx(out=xc[:].bitcast(FP8X4), scales=xs[:], in_=xg[:])
-        prep_half(dtw_sb, 1, dtg, "dt", s_copy, pse, "e")
-        vps = pse.tile([P, 1024], BF16, name="vps", tag="e")
-        nc.tensor.transpose(vps[:, 0:P], vrows[:], ident_b[:])
-        nc.scalar.copy(out=vec[:], in_=vps[:, 0 : 2 * CT])
-        nc.vector.quantize_mx(out=dtc[:].bitcast(FP8X4), scales=dts[:], in_=dtg[:])
-        prep_half(inw_sb, 0, ing, "in", v_copy)
-        prep_half(inw_sb, 1, ing, "in", v_copy)
-        for ct in range(CT):
-            proj_t(ct, dtc, dts, d_banks[ct // 2])
-        for ct in range(CT):
-            sp_abs(ct)
-        for ct in range(CT):
-            sp_relu(ct)
-        sp_log(0, CT)
+        nc.scalar.activation(out=soft[:], in_=soft[:], func=ACT.Exp, scale=-1.0)
+        nc.scalar.activation(out=soft[:], in_=soft[:], func=ACT.Ln, bias=1.0, scale=1.0)
         nc.scalar.activation(out=a_exp[:], in_=a_sb[:], func=ACT.Exp)
         nc.scalar.activation(out=neg_a[:], in_=a_exp[:], func=ACT.Copy, scale=-1.0)
-        nc.vector.quantize_mx(out=inc[:].bitcast(FP8X4), scales=ins[:], in_=ing[:])
-        w_tr(0, 0)
-        w_tr(0, 1)
-        for ct in range(CT):
-            proj_t(ct, inc, ins, u_banks[ct // 2])
-        sp_sum(0, 1)
-        sp_sum(1, CT)
-        bank_to_grouped_w(0, 0, v_copy)
-        bank_to_grouped_w(0, 1, v_copy)
-        w_tr(0, 2)
-        w_tr(0, 3)
-        quant(0, 0)
-        bank_to_grouped_w(0, 2, v_copy)
-        bank_to_grouped_w(0, 3, v_copy)
+        quantise(in_codes, in_scales, grouped_in)
+        turn_w(0, 0)
+        turn_w(0, 1)
+        project(in_codes, in_scales, u_banks)
+        nc.gpsimd.tensor_scalar(
+            out=d_diag[:], in0=ident_f[:], scalar1=vec[:, 2 * CT - 1 : 2 * CT], scalar2=None, op0=ALU.mult
+        )
+        for part in (slice(0, B), slice(B, CT * B)):
+            nc.gpsimd.tensor_tensor(out=delta_t[:, part], in0=soft_max[:, part], in1=soft[:, part], op=ALU.add)
+        group_w(0, 0, v_copy)
+        group_w(0, 1, v_copy)
+        turn_w(0, 2)
+        turn_w(0, 3)
+        quantise_w(0, 0, 1)
+        group_w(0, 2, v_copy)
+        group_w(0, 3, v_copy)
+        multiply_b(0)
+        quantise_w(0, 1, 1)
+        turn_w(1, 0)
+        turn_w(1, 1)
+        group_w(1, 0, v_copy)
+        multiply_du(0, 1)
+        for i in range(NN):
+            exponential(0, i)
+        group_w(1, 1, v_copy)
+        turn_du(0, v_copy, *WEIGHTS)
         for rt in range(RT):
-            mx_bc(0, rt, 0, b_ps, "bps")
-        quant(0, 1)
-        w_tr(1, 0)
-        w_tr(1, 1)
-        bank_to_grouped_w(1, 0, v_copy)
-        nc.vector.tensor_tensor(out=cols(du_t, 0), in0=cols(u_banks[0], 0), in1=cols(delta_t, 0), op=ALU.mult)
-        exps(0)
-        bank_to_grouped_w(1, 1, v_copy)
-        du_turn(0, v_copy, psw, "wps")
-        e_trans(0, 0)
-        e_trans(0, 1)
-        w_tr(1, 2)
-        w_tr(1, 3)
-        v_t3(0, 0)
-        v_t3(0, 1)
-        mul_eh(0, 0)
-        add_hn(0, 0)
-        mul_eh(0, 1)
-        add_hn(0, 1)
-        for lo, hi in ((1, 2), (2, CT)):
-            nc.vector.tensor_tensor(
-                out=du_t[:, lo * B : hi * B],
-                in0=u_banks[lo // 2][:, lo % 2 * B : lo % 2 * B + (hi - lo) * B],
-                in1=delta_t[:, lo * B : hi * B],
-                op=ALU.mult,
-            )
-        exps(1)
-        bank_to_grouped_w(1, 2, s_copy)
-        bank_to_grouped_w(1, 3, s_copy)
+            turn_exp(0, rt)
+        turn_w(1, 2)
+        turn_w(1, 3)
+        for rt in range(RT):
+            product_bu(0, rt)
+        for rt in range(RT):
+            product_eh(0, rt)
+            add_h_new(0, rt)
+        multiply_du(1, 2)
+        multiply_du(2, CT)
+        for i in range(NN):
+            exponential(1, i)
+        group_w(1, 2, s_copy)
+        group_w(1, 3, s_copy)
         for half in range(2):
-            s_copy(out=u_t[:, half * 512 : (half + 1) * 512], in_=u_banks[half][:])
-        quant(1, 0)
+            s_copy(out=u_t[:, half * BANK : (half + 1) * BANK], in_=u_banks[half][:])
+        quantise_w(1, 0, 1)
 
-        def w_upto(t):
-            return min(4 * NSTEP, 8 + W_RATE * (t + 1), 4 * (t + 2 + W_AHEAD))
-
-        def q_upto(t):
-            return 3 if t < 0 else min(2 * NSTEP, 2 * (t + 3))
+        def turned_by(t):
+            return min(4 * NSTEP, 8 + 5 * (t + 1), 4 * (t + 4))
 
         for t in range(NSTEP):
             last = t == NSTEP - 1
-            for s in range(4, min(NSTEP, w_upto(t - 1) // 4 + WST_BUFS)):
-                if s not in wst:
+            ct = t // NG
+            for s in range(4, min(NSTEP, turned_by(t - 1) // 4 + WEIGHT_BUFS)):
+                if s not in raw:
                     load_w(s)
             for rt in range(RT):
                 s = t + H_EARLY - rt
                 if s % NG == 0 and s // NG in range(2, CT):
-                    load_h(s // NG, (rt,))
+                    load_h(s // NG, rt)
             for rt in range(RT):
-                if t % NG == STORE_AT[rt] and t > NG - 1:
-                    store_h(t // NG - 1, rt)
-            if t == 8:
-                wo_sb = stg.tile([P, CT * D], BF16, name="wo_sb", tag="w512")
+                if t % NG == STORE_STEP[rt] and ct > 0:
+                    store_h(ct - 1, rt)
+            if t == NSTEP // 2:
+                out_sb = stage.tile([P, CT * D], BF16, name="out_sb", tag="rows512")
                 nc.sync.dma_start(
-                    out=wo_sb[:].rearrange("p (t k) -> p t k", t=CT), in_=out_proj_w.rearrange("(t p) k -> p t k", p=P)
+                    out=out_sb[:].rearrange("p (t k) -> p t k", t=CT), in_=out_proj_w.rearrange("(t p) k -> p t k", p=P)
                 )
-                nc.sync.dma_start(out=ob[:], in_=out_proj_b.partition_broadcast(P))
+                nc.sync.dma_start(out=out_bias[:], in_=out_proj_b.partition_broadcast(P))
             if last:
-                for rt in range(RT):
-                    mx_bc(t, rt, 1, c_ps, "cps")
-            banks = [divmod(i, 4) for i in range(w_upto(t - 1), w_upto(t))]
+                multiply_c(t)
             for rt in range(RT):
-                if t % NG == Y_AT[rt] and NG <= t < NSTEP - 1:
-                    ct = t // NG - 1
-                    y_open(ct, rt, psy, Y_TAG)
-                    for s in range(ct * NG, ct * NG + NG):
-                        y_acc(s, rt)
-            if t % NG == DU_AT and t // NG + 1 < CT:
-                du_turn(t // NG + 1, s_copy)
-            def e_part():
-                if not last:
-                    e_trans(t + 1, 0)
-                    e_trans(t + 1, 1)
-                    if t + 1 in G_T2:
-                        e_out(t + 1, 1)
-
-            for i in range(9):
-                if i == MB_POS and not last:
+                if t % NG == Y_STEP[rt] and ct > 0 and not last:
+                    sum_tile(ct - 1, rt)
+            if t % NG == TURN_DU_STEP and ct + 1 < CT:
+                turn_du(ct + 1, s_copy, *TURNED)
+            banks = [divmod(i, 4) for i in range(turned_by(t - 1), turned_by(t))]
+            for i in range(max(NN, len(banks))):
+                if i == NN // 2 and not last:
                     for rt in range(RT):
-                        mx_bc(t + 1, rt, 0, b_ps, "bps")
-                if i == ET_POS:
-                    e_part()
-                if i == EXP_POS and t + 2 < NSTEP:
-                    exps(t + 2)
-                if i < len(banks):
-                    w_bank(*banks[i])
+                        turn_exp(t + 1, rt)
+                    if t + 1 in GPSIMD_STEPS:
+                        copy_exp(t + 1)
+                if i == NN - 1 and not last:
+                    multiply_b(t + 1)
+                for s, b in banks[i : i + 1]:
+                    turn_w(s, b)
+                    group_w(s, b, s_copy)
+                if i < NN and t + 2 < NSTEP:
+                    exponential(t + 2, i)
             if t == NSTEP - 2:
                 for rt in range(RT):
-                    y_open(CT - 1, rt, psw, "wps")
+                    open_y(CT - 1, rt, *WEIGHTS)
             if t >= NSTEP - 2:
                 for rt in range(RT):
-                    y_acc(t - 2, rt)
+                    sum_y(t - 2, rt)
             if t == NSTEP - 2:
-                y_open(CT - 2, 1, psy, Y_TAG)
-                for s in range((CT - 2) * NG, (CT - 1) * NG):
-                    y_acc(s, 1)
+                sum_tile(CT - 2, 1)
             if t == NSTEP - 3:
-                wog = stg.tile([P, 4 * D], BF16, name="wog", tag="g512", align_bytes=64)
-                prep_wo(0, wo_sb, wog)
-                prep_wo(1, wo_sb, wog)
+                grouped_out = stage.tile([P, 4 * D], BF16, name="grouped_out", tag="grouped512", align_bytes=64)
+                for half in range(2):
+                    turn_out_w(half)
             if 0 < t < NSTEP - 1:
                 for rt in range(RT):
-                    v_t3(t, rt)
-                    add_hn(t, rt)
+                    product_bu(t, rt)
+                    add_h_new(t, rt)
             if t == NSTEP - 2:
                 for rt in range(RT):
-                    mul_eh(t + 1, rt)
+                    product_eh(t + 1, rt)
                 for rt in range(RT):
-                    v_t3(t + 1, rt)
-                    add_hn(t + 1, rt)
+                    product_bu(t + 1, rt)
+                    add_h_new(t + 1, rt)
             if last:
                 for rt in range(RT):
                     store_h(CT - 1, rt)
             if t > 0:
-                v_t4(t - 1, 0)
-                v_t4(t - 1, 1)
-            for rt in range(RT):
-                if t % NG == Y_AT[rt] and t // NG - 1 >= 0:
-                    fin_y(t // NG - 1, rt, y_f)
-            if t == 1:
-                y_f = stg.tile([P, CT * B], F32, name="y_f", tag="sp")
-            if not last:
-                qs = [divmod(i, 2) for i in range(q_upto(t - 1), q_upto(t))]
-                if V_ORDER == "tqqt":
-                    mul_eh(t + 1, 0)
-                for s, j in qs[:-2]:
-                    quant(s, j)
-                if V_ORDER == "ttqq" and t < NSTEP - 2:
-                    mul_eh(t + 1, 0)
-                    mul_eh(t + 1, 1)
-                if t >= Q_WIDE and len(qs) == 2:
-                    quant(qs[0][0], 0, 2)
-                else:
-                    for s, j in qs[-2:]:
-                        quant(s, j)
-                if V_ORDER == "tqqt":
-                    mul_eh(t + 1, 1)
-            if not last:
+                product_ch(t - 1, 0)
                 for rt in range(RT):
-                    mx_bc(t, rt, 1, c_ps, "cps")
-            if t == NSTEP - 1:
+                    if t % NG == Y_STEP[rt] and ct > 0:
+                        finish_y(ct - 1, rt)
+                product_ch(t - 1, 1)
+            if t == 1:
+                y_sb = stage.tile([P, CT * B], F32, name="y_sb", tag="soft")
+            if t == 0:
+                quantise_w(1, 1, 1)
+            if t < NSTEP - 2:
+                for rt in range(RT):
+                    product_eh(t + 1, rt)
+                if t + 2 < NSTEP:
+                    if t == 0:
+                        quantise_w(2, 0, 1)
+                        quantise_w(2, 1, 1)
+                    else:
+                        quantise_w(t + 2, 0, 2)
+            if not last:
+                multiply_c(t)
+            if last:
                 for ct in range(CT - 1):
                     for rt in range(RT):
-                        silu(ct, rt, y_f)
+                        silu(ct, rt)
 
-        last = NSTEP - 1
-        nc.vector.quantize_mx(out=woc[:].bitcast(FP8X4), scales=wos[:], in_=wog[:])
-        v_t4(last, 0)
-        v_t4(last, 1)
-        sc = const.tile([P, B], U32, name="sc", align_bytes=64)
-        ss = const.tile([P, B], U8, name="ss", align_bytes=64)
-        for s in range(last - 1, last):
-            for rt in range(RT):
-                y_acc(s, rt)
         for rt in range(RT):
-            y_acc(last, rt)
-            fin_y(CT - 1, rt, y_f)
-            silu(CT - 1, rt, y_f)
+            product_ch(NSTEP - 1, rt)
+        quantise(out_codes, out_scales, grouped_out)
+        for rt in range(RT):
+            sum_y(NSTEP - 2, rt)
+        for rt in range(RT):
+            sum_y(NSTEP - 1, rt)
+            silu(CT - 1, rt)
+        y_codes, y_scales = mx_tiles("y", B)
         for rt in range(RT):
             nc.vector.quantize_mx(
-                out=sc[:, rt * P : (rt + 1) * P].bitcast(FP8X4),
-                scales=ss[:, rt * P : (rt + 1) * P],
-                in_=sg[:, rt * 4 * P : (rt + 1) * 4 * P],
+                out=y_codes[:, rt * P : (rt + 1) * P].bitcast(FP8X4),
+                scales=y_scales[:, rt * P : (rt + 1) * P],
+                in_=silu_y[:, rt * 4 * P : (rt + 1) * 4 * P],
             )
-        o_ps = []
+        out_ps = []
         for rt in range(RT):
-            o_ps.append(pse.tile([P, 512], F32, name="ops%d" % rt, tag="e"))
+            out_ps.append(ps_turned.tile([P, BANK], F32, name="out_mx%d" % rt, tag="turned"))
             nc.tensor.matmul_mx(
-                out=o_ps[rt][:],
-                lhsT=sc[:, rt * P : (rt + 1) * P].bitcast(FP8X4),
-                lhsT_scale=ss[:, rt * P : (rt + 1) * P],
-                rhs=woc[:].bitcast(FP8X4),
-                rhs_scale=wos[:],
+                out=out_ps[rt][:],
+                lhsT=y_codes[:, rt * P : (rt + 1) * P].bitcast(FP8X4),
+                lhsT_scale=y_scales[:, rt * P : (rt + 1) * P],
+                rhs=out_codes[:].bitcast(FP8X4),
+                rhs_scale=out_scales[:],
                 start=True,
                 stop=True,
             )
         for rt in range(RT):
-            o_sb = tp.tile([P, D], F32, name="o_sb%d" % rt, tag="o_sb", bufs=2)
-            nc.vector.tensor_tensor(out=o_sb[:], in0=o_ps[rt][:], in1=ob[:], op=ALU.add)
-            nc.sync.dma_start(out=out[rt * P : (rt + 1) * P, :], in_=o_sb[:])
+            result = prod_pool.tile([P, D], F32, name="result%d" % rt, tag="result", bufs=2)
+            nc.vector.tensor_tensor(out=result[:], in0=out_ps[rt][:], in1=out_bias[:], op=ALU.add)
+            nc.sync.dma_start(out=out[rt * P : (rt + 1) * P, :], in_=result[:])

from contextlib import ExitStack

import concourse.mybir as mybir
from concourse.masks import make_identity

F32 = mybir.dt.float32
BF16 = mybir.dt.bfloat16
U32 = mybir.dt.uint32
U8 = mybir.dt.uint8
FP8X4 = mybir.dt.float8_e4m3fn_x4
ACT = mybir.ActivationFunctionType
ALU = mybir.AluOpType

P = 128
B = 256
D = 512
S = 16
RT = B // P
CT = D // P
NG = 4
NN = S // NG
NSTEP = CT * NG
BANK = 512

FLOPS = 2 * B * D * (3 * D + 2 * D * S)

WEIGHT_BUFS = 4
Y_STEP = (1, 3)
STORE_STEP = (1, 2)
TURN_DU_STEP = 2
H_EARLY = 5
GPSIMD_STEPS = range(5, NSTEP - 2, 2)


def tile_mambacell_pa_kernel(
    tc, x, h, in_proj_w, dt_proj_w, dt_proj_b, bc_proj_w, a_log, d_param, out_proj_w, out_proj_b, out, h_new
):
    nc = tc.nc
    with ExitStack() as ctx:
        ctx.enter_context(tc.manual_schedule())
        const = ctx.enter_context(tc.tile_pool(name="const", bufs=1))
        stage = ctx.enter_context(tc.tile_pool(name="stage", bufs=1))
        raw_pool = ctx.enter_context(tc.tile_pool(name="raw_pool", bufs=WEIGHT_BUFS))
        group_pool = ctx.enter_context(tc.tile_pool(name="group_pool", bufs=2))
        code_pool = ctx.enter_context(tc.tile_pool(name="code_pool", bufs=4))
        h_pool = ctx.enter_context(tc.tile_pool(name="h_pool", bufs=4))
        exp_pool = ctx.enter_context(tc.tile_pool(name="exp_pool", bufs=3))
        prod_pool = ctx.enter_context(tc.tile_pool(name="prod_pool", bufs=3))
        hn_pool = ctx.enter_context(tc.tile_pool(name="hn_pool", bufs=4))
        ps_weights = ctx.enter_context(tc.psum_pool(name="ps_weights", bufs=2))
        ps_turned = ctx.enter_context(tc.psum_pool(name="ps_turned", bufs=2))
        ps_mx = ctx.enter_context(tc.psum_pool(name="ps_mx", bufs=4))
        WEIGHTS = (ps_weights, "weights")
        TURNED = (ps_turned, "turned")

        v_copy = nc.vector.tensor_copy
        s_copy = nc.scalar.copy

        def mx_tiles(nm, groups):
            codes = const.tile([P, groups], U32, name="codes_" + nm, align_bytes=64)
            scales = const.tile([P, groups], U8, name="scales_" + nm, align_bytes=64)
            return codes, scales

        one = stage.tile([P, 1], F32, name="one")
        nc.vector.memset(one[:], 1.0)
        vec_rows = stage.tile([P, P], BF16, name="vec_rows")
        nc.vector.memset(vec_rows[:], 0.0)
        a_sb = stage.tile([P, CT * S], BF16, name="a_sb")
        out_bias = const.tile([P, D], BF16, name="out_bias")
        nc.scalar.activation(out=one[:], in_=one[:], func=ACT.Exp)
        ident_b = const.tile([P, P], BF16, name="ident_b")
        make_identity(nc, ident_b[:])
        ident_f = const.tile([P, P], F32, name="ident_f")
        make_identity(nc, ident_f[:])

        x_sb = stage.tile([P, RT * D], BF16, name="x_sb")
        nc.sync.dma_start(
            out=x_sb[:].rearrange("p (t k) -> p t k", t=RT), in_=x.rearrange("(t p) k -> p t k", p=P)
        )

        weight_view = bc_proj_w.rearrange("(t p j g n) k -> t g p j n k", p=P, j=2, g=NG, n=NN)
        h_view = h.rearrange("b c n -> b (c n)")
        h_new_view = h_new.rearrange("b c n -> b (c n)")

        raw = {}
        w_bank = {}
        grouped_w = {}
        w_codes = {}
        w_scales = {}
        h_sb = {}
        exp_t = {}
        exp_ps = {}
        exp_sb = {}
        b_ps = {}
        c_ps = {}
        eh = {}
        bu = {}
        ch = {}
        hn = {}
        y_ps = {}

        def load_w(s):
            raw[s] = raw_pool.tile([P, 2 * NN * D], BF16, name="raw%d" % s, tag="raw")
            nc.sync.dma_start(
                out=raw[s][:].rearrange("p (j n k) -> p j n k", j=2, n=NN), in_=weight_view[s // NG, s % NG]
            )

        def load_rows(dst, w, half):
            nc.sync.dma_start(
                out=dst[:].rearrange("p (t k) -> p t k", t=CT)[:, 2 * half : 2 * half + 2],
                in_=w.rearrange("(t p) k -> p t k", p=P)[:, 2 * half : 2 * half + 2],
            )

        def load_h(ct, rt):
            h_sb[(ct, rt)] = h_pool.tile([P, P * S], BF16, name="h%d_%d" % (ct, rt), tag="h")
            nc.sync.dma_start(
                out=h_sb[(ct, rt)][:], in_=h_view[rt * P : (rt + 1) * P, ct * P * S : (ct + 1) * P * S]
            )

        def store_h(ct, rt):
            nc.sync.dma_start(
                out=h_new_view[rt * P : (rt + 1) * P, ct * P * S : (ct + 1) * P * S], in_=hn[(ct, rt)][:]
            )

        dt_sb = stage.tile([P, CT * D], BF16, name="dt_sb", tag="rows512")
        in_sb = stage.tile([P, CT * D], BF16, name="in_sb")
        for half in range(2):
            load_rows(dt_sb, dt_proj_w, half)
        nc.sync.dma_start(out=vec_rows[0:CT, :], in_=dt_proj_b.rearrange("(t c) -> t c", c=P))
        nc.sync.dma_start(out=vec_rows[CT : 2 * CT, :], in_=d_param.rearrange("(t c) -> t c", c=P))
        for half in range(2):
            load_rows(in_sb, in_proj_w, half)
        load_w(0)
        nc.sync.dma_start(out=a_sb[:].rearrange("p (t n) -> p t n", t=CT), in_=a_log.rearrange("(t p) n -> p t n", p=P))
        load_w(1)
        for rt in range(RT):
            load_h(0, rt)
        load_w(2)
        load_w(3)
        for rt in range(RT):
            load_h(1, rt)

        def turn_words(words, first, name, pool, tag):
            ps = pool.tile([P, BANK], F32, name=name, tag=tag)
            for j in range(2):
                for u in range(2):
                    col = first + j * 256 + u * P
                    nc.tensor.transpose(ps[:, (j * 2 + u) * P : (j * 2 + u + 1) * P], words[:, col : col + P], ident_f[:])
            return ps

        def group_words(copy, ps, dst):
            copy(
                out=dst.rearrange("p (j c u) -> p j c u", j=2, u=2),
                in_=ps[:].rearrange("p (j u c) -> p j c u", j=2, u=2),
            )

        def turn_w(s, b):
            w_bank[(s, b)] = turn_words(raw[s][:].bitcast(F32), b * BANK, "w%d_%d" % (s, b), *WEIGHTS)

        def group_w(s, b, copy):
            if b == 0:
                grouped_w[s] = group_pool.tile([P, 4 * 2 * NN * P], BF16, name="group%d" % s, tag="group", align_bytes=64)
            group_words(copy, w_bank[(s, b)], grouped_w[s][:].bitcast(F32)[:, b * BANK : (b + 1) * BANK])

        def quantise_w(s, first, count):
            if first == 0:
                w_codes[s] = code_pool.tile([P, 2 * NN * P], U32, name="w_codes%d" % s, tag="w_codes", align_bytes=64)
                w_scales[s] = code_pool.tile([P, 2 * NN * P], U8, name="w_scales%d" % s, tag="w_scales", align_bytes=64)
            lo = first * NN * P
            hi = (first + count) * NN * P
            nc.vector.quantize_mx(
                out=w_codes[s][:, lo:hi].bitcast(FP8X4), scales=w_scales[s][:, lo:hi], in_=grouped_w[s][:, 4 * lo : 4 * hi]
            )

        def cols(t, ct):
            return t[:, ct * B : (ct + 1) * B]

        def exponential(s, i):
            ct = s // NG
            n = s % NG * NN + i
            if i == 0:
                exp_t[s] = exp_pool.tile([P, NN * B], F32, name="exp%d" % s, tag="exp")
            nc.scalar.activation(
                out=exp_t[s][:, i * B : (i + 1) * B],
                in_=cols(delta_t, ct),
                func=ACT.Exp,
                scale=neg_a[:, ct * S + n : ct * S + n + 1],
            )

        def turn_exp(s, rt):
            exp_ps[(s, rt)] = ps_turned.tile([P, BANK], F32, name="exp_ps%d_%d" % (s, rt), tag="turned")
            for i in range(NN):
                nc.tensor.transpose(
                    exp_ps[(s, rt)][:, i * P : (i + 1) * P], exp_t[s][:, i * B + rt * P : i * B + (rt + 1) * P], ident_f[:]
                )

        def multiply_w(s, j, store, nm):
            for rt in range(RT):
                store[(s, rt)] = ps_mx.tile([P, BANK], F32, name="%s%d_%d" % (nm, s, rt), tag="mx")
                nc.tensor.matmul_mx(
                    out=store[(s, rt)][:],
                    lhsT=x_codes[:, rt * P : (rt + 1) * P].bitcast(FP8X4),
                    lhsT_scale=x_scales[:, rt * P : (rt + 1) * P],
                    rhs=w_codes[s][:, j * NN * P : (j + 1) * NN * P].bitcast(FP8X4),
                    rhs_scale=w_scales[s][:, j * NN * P : (j + 1) * NN * P],
                    start=True,
                    stop=True,
                )

        def multiply_b(s):
            multiply_w(s, 0, b_ps, "b")

        def multiply_c(s):
            multiply_w(s, 1, c_ps, "c")

        def by_channel(t):
            return t[:].rearrange("p (n c) -> p c n", n=NN)

        def compact(t):
            return t[:].rearrange("p (c n) -> p c n", n=NN)

        def group_of(t, s):
            g = s % NG
            return t[:].rearrange("p (c n) -> p c n", n=S)[:, :, g * NN : (g + 1) * NN]

        def copy_exp(s):
            exp_sb[s] = prod_pool.tile([P, BANK], F32, name="exp_sb%d" % s, tag="exp_sb", bufs=2)
            nc.scalar.copy(out=compact(exp_sb[s]), in_=by_channel(exp_ps[(s, 1)]))

        def product_eh(s, rt):
            eh[(s, rt)] = prod_pool.tile([P, BANK], F32, name="eh%d_%d" % (s, rt), tag="eh", bufs=4)
            here = group_of(h_sb[(s // NG, rt)], s)
            if rt == 1 and s in GPSIMD_STEPS:
                nc.gpsimd.tensor_tensor(out=compact(eh[(s, rt)]), in0=compact(exp_sb[s]), in1=here, op=ALU.mult)
            else:
                nc.vector.tensor_tensor(out=compact(eh[(s, rt)]), in0=by_channel(exp_ps[(s, rt)]), in1=here, op=ALU.mult)

        def product_bu(s, rt):
            lo = (s // NG * RT + rt) * P
            bu[(s, rt)] = prod_pool.tile([P, BANK], F32, name="bu%d_%d" % (s, rt), tag="bu")
            nc.vector.tensor_tensor(
                out=compact(bu[(s, rt)]),
                in0=by_channel(b_ps[(s, rt)]),
                in1=du[:, lo : lo + P].unsqueeze(2).to_broadcast([P, P, NN]),
                op=ALU.mult,
            )

        def add_h_new(s, rt):
            ct = s // NG
            if s % NG == 0:
                hn[(ct, rt)] = hn_pool.tile([P, P * S], F32, name="hn%d_%d" % (ct, rt), tag="hn")
            nc.gpsimd.tensor_tensor(
                out=group_of(hn[(ct, rt)], s), in0=compact(eh[(s, rt)]), in1=compact(bu[(s, rt)]), op=ALU.add
            )

        def product_ch(s, rt):
            ch[(s, rt)] = prod_pool.tile([P, BANK], F32, name="ch%d_%d" % (s, rt), tag="ch", bufs=13)
            nc.vector.tensor_tensor(
                out=by_channel(ch[(s, rt)]), in0=by_channel(c_ps[(s, rt)]), in1=group_of(hn[(s // NG, rt)], s), op=ALU.mult
            )

        def open_y(ct, rt, pool, tag):
            y_ps[(ct, rt)] = pool.tile([P, BANK], F32, name="y%d_%d" % (ct, rt), tag=tag)

        def sum_y(s, rt):
            ct = s // NG
            g = s % NG
            tail = ct == CT - 1
            if tail and g == 0:
                nc.tensor.matmul(
                    out=y_ps[(ct, rt)][:, 0:P],
                    lhsT=d_diag[:],
                    rhs=u_t[:, ct * B + rt * P : ct * B + (rt + 1) * P],
                    start=True,
                    stop=False,
                )
            for i in range(NN):
                nc.tensor.matmul(
                    out=y_ps[(ct, rt)][:, 0:P],
                    lhsT=ch[(s, rt)][:, i * P : (i + 1) * P],
                    rhs=ident_f[:],
                    is_transpose=True,
                    start=(g == 0 and i == 0 and not tail),
                    stop=(g == NG - 1 and i == NN - 1),
                )

        def sum_tile(ct, rt):
            open_y(ct, rt, *TURNED)
            for s in range(ct * NG, (ct + 1) * NG):
                sum_y(s, rt)

        def finish_y(ct, rt):
            lo = ct * B + rt * P
            nc.vector.scalar_tensor_tensor(
                out=y_sb[:, lo : lo + P],
                in0=u_t[:, lo : lo + P],
                scalar=vec[:, CT + ct : CT + ct + 1],
                in1=y_ps[(ct, rt)][:, 0:P],
                op0=ALU.mult,
                op1=ALU.add,
            )

        def silu(ct, rt):
            lo = ct * B + rt * P
            nc.scalar.activation(
                out=silu_y[:].rearrange("p (r t) -> p r t", t=CT)[:, rt * P : (rt + 1) * P, ct],
                in_=y_sb[:, lo : lo + P] if ct < CT - 1 else y_ps[(ct, rt)][:, 0:P],
                func=ACT.Silu,
            )

        silu_y = const.tile([P, CT * B], BF16, name="silu_y", align_bytes=64)
        out_codes, out_scales = mx_tiles("out", D)

        def turn_out_w(half):
            ps = ps_weights.tile([P, 2 * BANK], BF16, name="out_ps%d" % half, tag="weights")
            for a in range(2):
                row = (half * 2 + a) * D
                for t in range(CT):
                    nc.tensor.transpose(
                        ps[:, (a * CT + t) * P : (a * CT + t + 1) * P], out_sb[:, row + t * P : row + (t + 1) * P], ident_b[:]
                    )
            nc.scalar.copy(
                out=grouped_out[:, half * 1024 : (half + 1) * 1024].rearrange("p (a o t) -> p a o t", a=2, t=CT),
                in_=ps[:].rearrange("p (a t o) -> p a o t", a=2, t=CT),
            )

        grouped_x = stage.tile([P, 4 * B], BF16, name="grouped_x", align_bytes=64)
        x_codes, x_scales = mx_tiles("x", B)
        grouped_dt = stage.tile([P, 4 * D], BF16, name="grouped_dt", tag="grouped512", align_bytes=64)
        dt_codes, dt_scales = mx_tiles("dt", D)
        grouped_in = stage.tile([P, 4 * D], BF16, name="grouped_in", align_bytes=64)
        in_codes, in_scales = mx_tiles("in", D)

        def prepare(w_sb, half, grouped, nm, copy, pool, tag):
            ps = turn_words(w_sb[:].bitcast(F32), half * BANK, "%s_ps%d" % (nm, half), pool, tag)
            group_words(copy, ps, grouped[:].bitcast(F32)[:, half * BANK : (half + 1) * BANK])

        def quantise(codes, scales, grouped):
            nc.vector.quantize_mx(out=codes[:].bitcast(FP8X4), scales=scales[:], in_=grouped[:])

        def project(codes, scales, banks):
            for ct in range(CT):
                nc.tensor.matmul_mx(
                    out=cols(banks[ct // 2], ct % 2),
                    lhsT=codes[:, ct * P : (ct + 1) * P].bitcast(FP8X4),
                    lhsT_scale=scales[:, ct * P : (ct + 1) * P],
                    rhs=x_codes[:].bitcast(FP8X4),
                    rhs_scale=x_scales[:],
                    start=True,
                    stop=True,
                )

        soft = stage.tile([P, CT * B], F32, name="soft", tag="soft")
        soft_max = stage.tile([P, CT * B], F32, name="soft_max")
        delta_t = const.tile([P, CT * B], F32, name="delta_t")
        u_t = const.tile([P, CT * B], F32, name="u_t")
        du_t = stage.tile([P, CT * B], F32, name="du_t")
        du = const.tile([P, CT * B], F32, name="du")
        a_exp = stage.tile([P, CT * S], F32, name="a_exp")
        neg_a = const.tile([P, CT * S], F32, name="neg_a")
        vec = const.tile([P, 2 * CT], F32, name="vec")
        d_diag = const.tile([P, P], F32, name="d_diag")

        def multiply_du(lo, hi):
            first = lo % 2 * B
            nc.vector.tensor_tensor(
                out=du_t[:, lo * B : hi * B],
                in0=u_banks[lo // 2][:, first : first + (hi - lo) * B],
                in1=delta_t[:, lo * B : hi * B],
                op=ALU.mult,
            )

        def turn_du(ct, copy, pool, tag):
            ps = pool.tile([P, BANK], F32, name="du_ps%d" % ct, tag=tag)
            for rt in range(RT):
                nc.tensor.transpose(ps[:, rt * P : (rt + 1) * P], du_t[:, ct * B + rt * P : ct * B + (rt + 1) * P], ident_f[:])
            copy(out=cols(du, ct), in_=ps[:, 0:B])

        d_banks = [ps_mx.tile([P, BANK], F32, name="dt_out%d" % half, tag="mx") for half in range(2)]
        u_banks = [ps_mx.tile([P, BANK], F32, name="in_out%d" % half, tag="mx") for half in range(2)]

        group_words(s_copy, turn_words(x_sb[:].bitcast(F32), 0, "x_ps", *WEIGHTS), grouped_x[:].bitcast(F32))
        prepare(dt_sb, 0, grouped_dt, "dt", s_copy, *WEIGHTS)
        quantise(x_codes, x_scales, grouped_x)
        prepare(dt_sb, 1, grouped_dt, "dt", s_copy, *TURNED)
        vec_ps = ps_turned.tile([P, 2 * BANK], BF16, name="vec_ps", tag="turned")
        nc.tensor.transpose(vec_ps[:, 0:P], vec_rows[:], ident_b[:])
        nc.scalar.copy(out=vec[:], in_=vec_ps[:, 0 : 2 * CT])
        quantise(dt_codes, dt_scales, grouped_dt)
        for half in range(2):
            prepare(in_sb, half, grouped_in, "in", v_copy, *WEIGHTS)
        project(dt_codes, dt_scales, d_banks)
        for ct in range(CT):
            nc.scalar.activation(
                out=cols(soft, ct), in_=cols(d_banks[ct // 2], ct % 2), func=ACT.Abs, bias=vec[:, ct : ct + 1], scale=1.0
            )
        for ct in range(CT):
            nc.vector.tensor_scalar(
                out=cols(soft_max, ct),
                in0=cols(d_banks[ct // 2], ct % 2),
                scalar1=vec[:, ct : ct + 1],
                scalar2=0.0,
                op0=ALU.add,
                op1=ALU.max,
            )
        nc.scalar.activation(out=soft[:], in_=soft[:], func=ACT.Exp, scale=-1.0)
        nc.scalar.activation(out=soft[:], in_=soft[:], func=ACT.Ln, bias=1.0, scale=1.0)
        nc.scalar.activation(out=a_exp[:], in_=a_sb[:], func=ACT.Exp)
        nc.scalar.activation(out=neg_a[:], in_=a_exp[:], func=ACT.Copy, scale=-1.0)
        quantise(in_codes, in_scales, grouped_in)
        turn_w(0, 0)
        turn_w(0, 1)
        project(in_codes, in_scales, u_banks)
        nc.gpsimd.tensor_scalar(
            out=d_diag[:], in0=ident_f[:], scalar1=vec[:, 2 * CT - 1 : 2 * CT], scalar2=None, op0=ALU.mult
        )
        for part in (slice(0, B), slice(B, CT * B)):
            nc.gpsimd.tensor_tensor(out=delta_t[:, part], in0=soft_max[:, part], in1=soft[:, part], op=ALU.add)
        group_w(0, 0, v_copy)
        group_w(0, 1, v_copy)
        turn_w(0, 2)
        turn_w(0, 3)
        quantise_w(0, 0, 1)
        group_w(0, 2, v_copy)
        group_w(0, 3, v_copy)
        multiply_b(0)
        quantise_w(0, 1, 1)
        turn_w(1, 0)
        turn_w(1, 1)
        group_w(1, 0, v_copy)
        multiply_du(0, 1)
        for i in range(NN):
            exponential(0, i)
        group_w(1, 1, v_copy)
        turn_du(0, v_copy, *WEIGHTS)
        for rt in range(RT):
            turn_exp(0, rt)
        turn_w(1, 2)
        turn_w(1, 3)
        for rt in range(RT):
            product_bu(0, rt)
        for rt in range(RT):
            product_eh(0, rt)
            add_h_new(0, rt)
        multiply_du(1, 2)
        multiply_du(2, CT)
        for i in range(NN):
            exponential(1, i)
        group_w(1, 2, s_copy)
        group_w(1, 3, s_copy)
        for half in range(2):
            s_copy(out=u_t[:, half * BANK : (half + 1) * BANK], in_=u_banks[half][:])
        quantise_w(1, 0, 1)

        def turned_by(t):
            return min(4 * NSTEP, 8 + 5 * (t + 1), 4 * (t + 4))

        for t in range(NSTEP):
            last = t == NSTEP - 1
            ct = t // NG
            for s in range(4, min(NSTEP, turned_by(t - 1) // 4 + WEIGHT_BUFS)):
                if s not in raw:
                    load_w(s)
            for rt in range(RT):
                s = t + H_EARLY - rt
                if s % NG == 0 and s // NG in range(2, CT):
                    load_h(s // NG, rt)
            for rt in range(RT):
                if t % NG == STORE_STEP[rt] and ct > 0:
                    store_h(ct - 1, rt)
            if t == NSTEP // 2:
                out_sb = stage.tile([P, CT * D], BF16, name="out_sb", tag="rows512")
                nc.sync.dma_start(
                    out=out_sb[:].rearrange("p (t k) -> p t k", t=CT), in_=out_proj_w.rearrange("(t p) k -> p t k", p=P)
                )
                nc.sync.dma_start(out=out_bias[:], in_=out_proj_b.partition_broadcast(P))
            if last:
                multiply_c(t)
            for rt in range(RT):
                if t % NG == Y_STEP[rt] and ct > 0 and not last:
                    sum_tile(ct - 1, rt)
            if t % NG == TURN_DU_STEP and ct + 1 < CT:
                turn_du(ct + 1, s_copy, *TURNED)
            banks = [divmod(i, 4) for i in range(turned_by(t - 1), turned_by(t))]
            for i in range(max(NN, len(banks))):
                if i == NN // 2 and not last:
                    for rt in range(RT):
                        turn_exp(t + 1, rt)
                    if t + 1 in GPSIMD_STEPS:
                        copy_exp(t + 1)
                if i == NN - 1 and not last:
                    multiply_b(t + 1)
                for s, b in banks[i : i + 1]:
                    turn_w(s, b)
                    group_w(s, b, s_copy)
                if i < NN and t + 2 < NSTEP:
                    exponential(t + 2, i)
            if t == NSTEP - 2:
                for rt in range(RT):
                    open_y(CT - 1, rt, *WEIGHTS)
            if t >= NSTEP - 2:
                for rt in range(RT):
                    sum_y(t - 2, rt)
            if t == NSTEP - 2:
                sum_tile(CT - 2, 1)
            if t == NSTEP - 3:
                grouped_out = stage.tile([P, 4 * D], BF16, name="grouped_out", tag="grouped512", align_bytes=64)
                for half in range(2):
                    turn_out_w(half)
            if 0 < t < NSTEP - 1:
                for rt in range(RT):
                    product_bu(t, rt)
                    add_h_new(t, rt)
            if t == NSTEP - 2:
                for rt in range(RT):
                    product_eh(t + 1, rt)
                for rt in range(RT):
                    product_bu(t + 1, rt)
                    add_h_new(t + 1, rt)
            if last:
                for rt in range(RT):
                    store_h(CT - 1, rt)
            if t > 0:
                product_ch(t - 1, 0)
                for rt in range(RT):
                    if t % NG == Y_STEP[rt] and ct > 0:
                        finish_y(ct - 1, rt)
                product_ch(t - 1, 1)
            if t == 1:
                y_sb = stage.tile([P, CT * B], F32, name="y_sb", tag="soft")
            if t == 0:
                quantise_w(1, 1, 1)
            if t < NSTEP - 2:
                for rt in range(RT):
                    product_eh(t + 1, rt)
                if t + 2 < NSTEP:
                    if t == 0:
                        quantise_w(2, 0, 1)
                        quantise_w(2, 1, 1)
                    else:
                        quantise_w(t + 2, 0, 2)
            if not last:
                multiply_c(t)
            if last:
                for ct in range(CT - 1):
                    for rt in range(RT):
                        silu(ct, rt)

        for rt in range(RT):
            product_ch(NSTEP - 1, rt)
        quantise(out_codes, out_scales, grouped_out)
        for rt in range(RT):
            sum_y(NSTEP - 2, rt)
        for rt in range(RT):
            sum_y(NSTEP - 1, rt)
            silu(CT - 1, rt)
        y_codes, y_scales = mx_tiles("y", B)
        for rt in range(RT):
            nc.vector.quantize_mx(
                out=y_codes[:, rt * P : (rt + 1) * P].bitcast(FP8X4),
                scales=y_scales[:, rt * P : (rt + 1) * P],
                in_=silu_y[:, rt * 4 * P : (rt + 1) * 4 * P],
            )
        out_ps = []
        for rt in range(RT):
            out_ps.append(ps_turned.tile([P, BANK], F32, name="out_mx%d" % rt, tag="turned"))
            nc.tensor.matmul_mx(
                out=out_ps[rt][:],
                lhsT=y_codes[:, rt * P : (rt + 1) * P].bitcast(FP8X4),
                lhsT_scale=y_scales[:, rt * P : (rt + 1) * P],
                rhs=out_codes[:].bitcast(FP8X4),
                rhs_scale=out_scales[:],
                start=True,
                stop=True,
            )
        for rt in range(RT):
            result = prod_pool.tile([P, D], F32, name="result%d" % rt, tag="result", bufs=2)
            nc.vector.tensor_tensor(out=result[:], in0=out_ps[rt][:], in1=out_bias[:], op=ALU.add)
            nc.sync.dma_start(out=out[rt * P : (rt + 1) * P, :], in_=result[:])
